import numpy as np
import ml_dtypes


def mxq(x, axis, fmt="e4m3"):
    dtype, down = {"e4m3": (ml_dtypes.float8_e4m3fn, 7), "e5m2": (ml_dtypes.float8_e5m2, 14)}[fmt]
    v = np.moveaxis(np.asarray(x, np.float32).astype(ml_dtypes.bfloat16).astype(np.float64), axis, -1)
    blocks = v.reshape(v.shape[:-1] + (-1, 32))
    amax = np.abs(blocks).max(-1, keepdims=True)
    byte = np.maximum(np.where(amax > 0, np.frexp(amax)[1] - 1 + 127, 0) - down, 1)
    scale = np.exp2(byte - 127.0)
    codes = (blocks / scale).astype(np.float32).astype(dtype).astype(np.float64)
    return np.moveaxis((codes * scale).reshape(v.shape), -1, axis)


WIDE = False


def mx_kscale(k):
    if not WIDE:
        return np.ones(k)
    levels = np.array([10, -10, 5, -5, 0])
    if k % 512:
        return np.exp2(np.random.permutation(np.resize(levels, k // 32))).repeat(32)
    a = np.empty((k // 512, 16))
    for p in range(k // 512):
        a[p, :8] = np.random.permutation(np.resize(levels, 8))
        for g in range(8):
            far = levels[np.abs(levels - a[p, g]) >= 10]
            a[p, g + 8] = far[np.random.randint(len(far))]
    return np.exp2(a.ravel()).repeat(32)


BF16 = ml_dtypes.bfloat16


def bf(x):
    return np.asarray(x, np.float32).astype(BF16)


def f64(x):
    return np.asarray(x).astype(np.float64)


B, L, D, T = 1024, 16, 512, 8
F = 2 * D
LN_EPS = 1e-5


def erf(v):
    a = np.minimum(np.abs(v), 6.0)
    term = a.copy()
    total = a.copy()
    for n in range(1, 200):
        term = term * (2.0 * a * a / (2 * n + 1))
        total = total + term
    return np.sign(v) * (2.0 / np.sqrt(np.pi)) * np.exp(-a * a) * total


def gelu_erf(v):
    return 0.5 * v * (1.0 + erf(v / np.sqrt(2.0)))


def draw0():
    s, t = mx_kscale(D), mx_kscale(F)
    counts = np.random.randint(1, T + 1, B)
    counts[0] = T
    target_mask = (np.arange(L)[None, :] < counts[:, None]).astype(np.float64)
    context_mask = 1.0 - target_mask
    context_mask[np.random.random(B) < 0.125] = 0.0
    return {"context_repr": bf(np.random.standard_normal((B, L, D)) * (0.75 * np.sqrt(L)) * s),
            "target_mask": bf(target_mask),
            "context_mask": bf(context_mask),
            "W1": bf(np.random.standard_normal((D, F)) / np.sqrt(D) / s[:, None]),
            "b1": bf(np.random.standard_normal(F) * 0.5),
            "gamma": bf((1.0 + 0.1 * np.random.standard_normal(F)) * t),
            "beta": bf(0.2 * np.random.standard_normal(F) * t),
            "W2": bf(np.random.standard_normal((F, D)) / np.sqrt(F) / t[:, None]),
            "b2": bf(np.random.standard_normal(D) * 0.3),
            "num_targets": T}


def core(context_repr, target_mask, context_mask, W1, b1, gamma, beta, W2, b2, num_targets):
    ctx_count = f64(context_mask).sum(axis=-1)
    ctx_sum = f64(context_repr).sum(axis=1)
    mean = ctx_sum / np.maximum(ctx_count, 1.0)[:, None]
    mean = np.where((ctx_count > 0)[:, None], mean, 0.0)
    h = gelu_erf((mxq(mean, 1, "e4m3") @ mxq(f64(W1), 0, "e4m3")) + f64(b1))
    mu = h.mean(axis=-1, keepdims=True)
    var = ((h - mu) ** 2).mean(axis=-1, keepdims=True)
    hn = (h - mu) / np.sqrt(var + LN_EPS) * f64(gamma) + f64(beta)
    out = (mxq(hn, 1, "e4m3") @ mxq(f64(W2), 0, "e4m3")) + f64(b2)
    tgt_counts = f64(target_mask).sum(axis=-1)
    valid = np.arange(num_targets)[None, :] < tgt_counts[:, None]
    return np.where(valid[:, :, None], out[:, None, :], 0.0)


def e4m3fn_bytes(y):
    return np.clip(np.asarray(y, np.float64), -448.0, 448.0).astype(np.float32).astype(ml_dtypes.float8_e4m3fn).view(np.uint8)


def e4m3fn_values(b):
    return np.asarray(b, np.uint8).view(ml_dtypes.float8_e4m3fn).astype(np.float64)


def setup_inputs():
    d = draw0()
    x0 = np.asarray(d['W2']).astype(np.float64)
    s = (np.max(np.abs(x0), axis=(1,), keepdims=True) / 448.0).astype(np.float32)
    out = {}
    for k, v in d.items():
        if k == 'W2':
            out['W2_bytes'] = e4m3fn_bytes(x0 / s.astype(np.float64))
            out['W2_scale'] = s
        else:
            out[k] = v
    return out


def reference(context_repr, target_mask, context_mask, W1, b1, gamma, beta, W2_bytes, W2_scale, b2, num_targets):
    return core(context_repr, target_mask, context_mask, W1, b1, gamma, beta, e4m3fn_values(W2_bytes) * W2_scale.astype(np.float64), b2, num_targets)

@@ -1,0 +1,499 @@
+from contextlib import ExitStack
+
+import concourse.mybir as mybir
+from concourse.masks import make_identity
+
+B, L, D, T = 1024, 16, 512, 8
+F = 2 * D
+LN_EPS = 1e-5
+
+FLOPS = 2 * B * D * F + 2 * B * F * D
+
+P = 128
+NT = B // P
+LAST = NT - 1
+HALF = F // 2
+QUARTERS = 4
+BLOCKS = 4
+
+PAIRED_QUARTERS = 19
+
+QUARTERS_PER_LOAD = (1, 1, 1, 2, 4, 4, 4, 4)
+
+FIRST_HALF_STORED = 3
+
+LOW, HIGH = (0, 1, 2, 3), (4, 5, 6, 7)
+
+F32 = mybir.dt.float32
+BF16 = mybir.dt.bfloat16
+U32 = mybir.dt.uint32
+U8 = mybir.dt.uint8
+FP8 = mybir.dt.float8_e4m3fn
+FP8X4 = mybir.dt.float8_e4m3fn_x4
+ALU = mybir.AluOpType
+ACT = mybir.ActivationFunctionType
+X = mybir.AxisListType.X
+
+
+def rows_per_partition(i, quarter):
+    return 2 if QUARTERS * i + quarter < PAIRED_QUARTERS else 1
+
+
+def hidden_block(g, u):
+    c0 = HALF * g + 256 * u
+    return slice(c0, c0 + 256)
+
+
+def tile_simplepredictor_t_kernel(
+    tc, context_repr, target_mask, context_mask, W1, b1, gamma, beta, W2_bytes, W2_scale, b2, num_targets, out
+):
+    nc = tc.nc
+    assert num_targets == T
+    with ExitStack() as es:
+        keep = es.enter_context(tc.tile_pool(name="keep", bufs=1))
+        ctxp = es.enter_context(tc.tile_pool(name="ctxp", bufs=4))
+        work = es.enter_context(tc.tile_pool(name="work", bufs=2))
+        outp = es.enter_context(tc.tile_pool(name="outp", bufs=4))
+        psum = es.enter_context(tc.psum_pool(name="psum", bufs=2))
+
+        es.enter_context(tc.manual_schedule())
+
+        def load_vector(vec, per, name):
+            cols = keep.tile([P, per], BF16, name=name)
+            nc.scalar.dma_start(out=cols[:], in_=vec.rearrange("(p i) -> p i", i=per))
+            return cols
+
+        cmask = keep.tile([P, 8, L], BF16)
+        nc.scalar.dma_start(out=cmask[:], in_=context_mask.rearrange("(p i) l -> p i l", i=8))
+        b1_cols = load_vector(b1, 8, "b1_cols")
+        w2_scale = keep.tile([P, 2, 4], F32)
+        nc.scalar.dma_start(out=w2_scale[:], in_=W2_scale.rearrange("(g p t) o -> p g (t o)", g=2, t=4))
+        gamma_cols = load_vector(gamma, 8, "gamma_cols")
+        beta_cols = load_vector(beta, 8, "beta_cols")
+        b2_cols = load_vector(b2, 4, "b2_cols")
+        tmask = keep.tile([P, 8, L], BF16)
+        nc.scalar.dma_start(out=tmask[:], in_=target_mask.rearrange("(p i) l -> p i l", i=8))
+
+        w1_rows = keep.tile([P, 4, F], BF16)
+        nc.sync.dma_start(out=w1_rows[:], in_=W1.rearrange("(p t) c -> p t c", t=4))
+
+        rows = context_repr.rearrange("b l d -> (b l) d")
+        ctx = {}
+
+        def load_rows(i):
+            ctx[i] = ctxp.tile([P, QUARTERS, BLOCKS, D], BF16, tag="ctx", name="ctx")
+            q = 0
+            while q < QUARTERS:
+                r = rows_per_partition(i, q)
+                n = 1
+                while n < QUARTERS_PER_LOAD[i] and q + n < QUARTERS and rows_per_partition(i, q + n) == r:
+                    n += 1
+                row0 = 512 * (QUARTERS * i + q)
+                nc.sync.dma_start(
+                    out=ctx[i][:, q : q + n].rearrange("p q (c r) d -> p (q c) (r d)", r=r),
+                    in_=rows[row0 : row0 + 512 * n, :].rearrange("(c p r) d -> p c (r d)", p=P, r=r),
+                )
+                q += n
+
+        load_rows(0)
+        w2_bytes = keep.tile([P, 2, 4, D], U8)
+        nc.sync.dma_start(
+            out=w2_bytes[:].rearrange("p g t n -> p g (t n)"), in_=W2_bytes.rearrange("(g p t) n -> p g (t n)", g=2, t=4)
+        )
+        for i in range(1, 4):
+            load_rows(i)
+
+        ident_f32 = keep.tile([P, P], F32)
+        make_identity(nc, ident_f32[:])
+        minus_half = keep.tile([P, 1], F32)
+        nc.gpsimd.memset(minus_half[:], -0.5)
+        slot_index = keep.tile([P, T], F32)
+        nc.gpsimd.iota(
+            slot_index[:], pattern=[[1, T]], base=0, channel_multiplier=0, allow_small_or_imprecise_dtypes=True
+        )
+        table_in = keep.tile([P, 1], F32)
+        nc.gpsimd.memset(table_in[:], 0.0)
+        table_out = keep.tile([P, 1], F32)
+        nc.scalar.activation(out=table_out[:], in_=table_in[:], func=ACT.Gelu)
+
+        ident_bf16 = keep.tile([P, P], BF16)
+        nc.vector.tensor_copy(out=ident_bf16[:], in_=ident_f32[:])
+        sel2_f32 = keep.tile([P, 16], F32)
+        sel2 = keep.tile([P, 16], BF16)
+        nc.vector.tensor_reduce(out=sel2_f32[:], in_=ident_f32[:].rearrange("p (j q) -> p j q", q=8), axis=X, op=ALU.add)
+        nc.vector.tensor_copy(out=sel2[:], in_=sel2_f32[:])
+        sel1_f32 = keep.tile([P, 8], F32)
+        sel1 = keep.tile([P, 8], BF16)
+        nc.vector.tensor_reduce(out=sel1_f32[:], in_=ident_f32[:].rearrange("p (j q) -> p j q", q=16), axis=X, op=ALU.add)
+        pooling = {1: sel1, 2: sel2}
+        mod16 = keep.tile([P, 16], F32)
+        nc.vector.tensor_reduce(out=mod16[:], in_=ident_f32[:].rearrange("p (j q) -> p q j", q=16), axis=X, op=ALU.add)
+
+        count = keep.tile([P, 8], F32)
+        count_or_1 = keep.tile([P, 8], F32)
+        reciprocal = keep.tile([P, 8], F32)
+        factor = keep.tile([P, 8], F32)
+        factor_all = keep.tile([P, B], F32)
+
+        def spread_factor(k):
+            turned = psum.tile([P, 4, P], F32, tag="h", bufs=4, name="turned")
+            for i in range(4):
+                column = factor[:, 4 * k + i : 4 * k + i + 1]
+                nc.tensor.transpose(turned[:, i, :], column.to_broadcast([P, P]), ident_f32[:])
+            nc.vector.tensor_copy(
+                out=factor_all[:].rearrange("p (n i) -> p n i", i=8)[:, :, 4 * k : 4 * k + 4],
+                in_=turned[:].rearrange("p i n -> p n i"),
+            )
+
+        def turn_vector(cols, per):
+            turned = psum.tile([P, per, P], BF16, tag="h", bufs=4, name="turned")
+            for i in range(per):
+                nc.tensor.transpose(turned[:, i, :], cols[:, i : i + 1].to_broadcast([P, P]), ident_bf16[:])
+            return turned
+
+        def spread_hidden(cols, name):
+            dst = keep.tile([P, F], BF16, name=name)
+            src = turn_vector(cols, 8)[:].rearrange("p (v u e) n -> p u n v e", u=2, e=2)
+            for g in range(2):
+                for u in range(2):
+                    nc.scalar.copy(
+                        out=dst[:, hidden_block(g, u)].rearrange("p (n v e) -> p n v e", v=2, e=2),
+                        in_=src[:, u, 64 * g : 64 * g + 64],
+                    )
+            return dst
+
+        w1_codes = keep.tile([P, F], U32, align_bytes=64)
+        w1_planes = keep.tile([P, F], U8, align_bytes=64)
+        w1_words = [keep.tile([P, HALF, 4], BF16, align_bytes=64, name="w1_words%d" % g) for g in range(2)]
+
+        def interleave_w1(g):
+            copy = (nc.vector.tensor_copy, nc.scalar.copy)[g]
+            src = w1_rows[:, :, HALF * g : HALF * g + HALF].rearrange("p t (m u e) -> p u m e t", u=2, e=2)
+            for u in range(2):
+                copy(out=w1_words[g][:, hidden_block(0, u), :].rearrange("p (m e) t -> p m e t", e=2), in_=src[:, u])
+
+        def quantise_w1(g):
+            cols = slice(HALF * g, HALF * g + HALF)
+            nc.vector.quantize_mx(
+                out=w1_codes[:, cols].bitcast(FP8X4),
+                scales=w1_planes[:, cols],
+                in_=w1_words[g][:].rearrange("p c t -> p (c t)"),
+            )
+
+        w2_rows = keep.tile([P, 2, 4, D], BF16)
+        w2_words = [keep.tile([P, D, 4], BF16, align_bytes=64, name="w2_words%d" % g) for g in range(2)]
+        w2_codes = keep.tile([P, 2, D], U32, align_bytes=64)
+        w2_planes = keep.tile([P, 2, D], U8, align_bytes=64)
+
+        def widen_w2(g):
+            for t in range(4):
+                nc.scalar.activation(
+                    out=w2_rows[:, g, t, :],
+                    in_=w2_bytes[:, g, t, :].bitcast(FP8),
+                    func=ACT.Copy,
+                    scale=w2_scale[:, g, t : t + 1],
+                )
+
+        def interleave_w2(g):
+            nc.scalar.copy(out=w2_words[g][:], in_=w2_rows[:, g].rearrange("p t n -> p n t"))
+
+        def quantise_w2(g):
+            nc.vector.quantize_mx(
+                out=w2_codes[:, g, :].bitcast(FP8X4),
+                scales=w2_planes[:, g, :],
+                in_=w2_words[g][:].rearrange("p n t -> p (n t)"),
+            )
+
+        st = {}
+
+        def pool(i, q):
+            if q == 0:
+                st["sums", i] = psum.tile([P, 4, P], F32, tag="pool", name="sums")
+            r = rows_per_partition(i, q)
+            width = 8 * r
+            x = ctx[i][:, q].rearrange("p (c r) d -> p c (r d)", r=r)
+            for c in range(BLOCKS // r):
+                b0 = 32 * q + width * c
+                for t in range(4):
+                    for e in range(r):
+                        nc.tensor.matmul(
+                            out=st["sums", i][:, t, b0 : b0 + width],
+                            lhsT=x[:, c, D * e + t : D * e + D : 4],
+                            rhs=pooling[r][:],
+                            start=(e == 0),
+                            stop=(e == r - 1),
+                        )
+
+        def scale_mean(i):
+            mean = work.tile([P, P, 4], BF16, align_bytes=64, tag="mean", name="mean")
+            nc.vector.tensor_tensor(
+                out=mean[:],
+                in0=st["sums", i][:].rearrange("p t b -> p b t"),
+                in1=factor_all[:, P * i : P * i + P].unsqueeze(2).to_broadcast([P, P, 4]),
+                op=ALU.mult,
+            )
+            st["mean", i] = mean
+
+        def quantise_mean(i):
+            codes = work.tile([P, P], U32, align_bytes=64, tag="mean_codes", name="mean_codes")
+            plane = work.tile([P, P], U8, align_bytes=64, tag="mean_plane", name="mean_plane")
+            nc.vector.quantize_mx(
+                out=codes[:].bitcast(FP8X4), scales=plane[:], in_=st["mean", i][:].rearrange("p b t -> p (b t)")
+            )
+            st["mean_codes", i], st["mean_plane", i] = codes, plane
+
+        def multiply_w1(i):
+            for g in range(2):
+                cols = slice(HALF * g, HALF * g + HALF)
+                acc = psum.tile([P, HALF], F32, tag="h", bufs=4, name="acc")
+                nc.tensor.matmul_mx(
+                    out=acc[:],
+                    lhsT=st["mean_codes", i][:].bitcast(FP8X4),
+                    lhsT_scale=st["mean_plane", i][:],
+                    rhs=w1_codes[:, cols].bitcast(FP8X4),
+                    rhs_scale=w1_planes[:, cols],
+                    start=True,
+                    stop=True,
+                )
+                st["acc", i, g] = acc
+
+        def bias_and_gelu(i, g):
+            if g == 0:
+                st["v", i] = work.tile([P, F], F32, tag="v", name="v")
+                st["h", i] = work.tile([P, F], F32, tag="h", name="h")
+            cols = slice(HALF * g, HALF * g + HALF)
+            v = st["v", i][:, cols]
+            nc.vector.tensor_tensor(out=v, in0=st["acc", i, g][:], in1=b1_all[:, cols], op=ALU.add)
+            nc.scalar.activation(out=st["h", i][:, cols], in_=v, func=ACT.Gelu)
+
+        def half_statistics(i, g):
+            if g == 0:
+                st["half_stats", i] = work.tile([P, 2, 6], F32, tag="half_stats", name="half_stats")
+            nc.vector.bn_stats(out=st["half_stats", i][:, g, :], in_=st["h", i][:, HALF * g : HALF * g + HALF])
+
+        def statistics(i):
+            stats = work.tile([P, 2], F32, tag="stats", name="stats")
+            nc.vector.bn_aggr(out=stats[:], in_=st["half_stats", i][:].rearrange("p g s -> p (g s)"))
+            var_eps = work.tile([P, 1], F32, tag="var_eps", name="var_eps")
+            nc.gpsimd.tensor_scalar_add(var_eps[:], stats[:, 1:2], LN_EPS)
+            rstd = work.tile([P, 1], F32, tag="rstd", name="rstd")
+            nc.gpsimd.tensor_tensor(out=rstd[:], in0=var_eps[:], in1=minus_half[:], op=ALU.pow)
+            st["stats", i], st["rstd", i] = stats, rstd
+
+        def centre(i):
+            centred = work.tile([P, F], F32, tag="centred", name="centred")
+            nc.vector.scalar_tensor_tensor(
+                out=centred[:],
+                in0=st["h", i][:],
+                scalar=st["stats", i][:, 0:1],
+                in1=gamma_all[:],
+                op0=ALU.subtract,
+                op1=ALU.mult,
+            )
+            st["centred", i] = centred
+
+        def normalise(i):
+            hn = work.tile([P, F], BF16, tag="hn", name="hn")
+            nc.vector.scalar_tensor_tensor(
+                out=hn[:], in0=st["centred", i][:], scalar=st["rstd", i][:], in1=beta_all[:], op0=ALU.mult, op1=ALU.add
+            )
+            st["hn", i] = hn
+
+        def transpose_hn(i):
+            turned = psum.tile([P, 2, 2, P], F32, tag="turned_hn", bufs=1, name="turned_hn")
+            words = st["hn", i][:].bitcast(F32)
+            for g in range(2):
+                for u in range(2):
+                    w0 = 256 * g + 128 * u
+                    nc.tensor.transpose(turned[:, g, u, :], words[:, w0 : w0 + 128], ident_f32[:])
+            st["turned_hn", i] = turned
+
+        def interleave_hn(i):
+            hn_words = work.tile([P, 2 * P * 4], BF16, align_bytes=64, tag="hn_words", name="hn_words")
+            nc.scalar.copy(
+                out=hn_words[:].bitcast(F32).rearrange("p (g b u) -> p g b u", g=2, u=2),
+                in_=st["turned_hn", i][:].rearrange("p g u b -> p g b u"),
+            )
+            st["hn_words", i] = hn_words
+
+        def quantise_hn(i):
+            codes = work.tile([P, 2 * P], U32, align_bytes=64, tag="hn_codes", name="hn_codes")
+            plane = work.tile([P, 2 * P], U8, align_bytes=64, tag="hn_plane", name="hn_plane")
+            nc.vector.quantize_mx(out=codes[:].bitcast(FP8X4), scales=plane[:], in_=st["hn_words", i][:])
+            st["hn_codes", i], st["hn_plane", i] = codes, plane
+
+        def multiply_w2(i):
+            acc = psum.tile([P, D], F32, tag="out", bufs=1, name="acc2")
+            for g in range(2):
+                part = slice(P * g, P * g + P)
+                nc.tensor.matmul_mx(
+                    out=acc[:],
+                    lhsT=st["hn_codes", i][:, part].bitcast(FP8X4),
+                    lhsT_scale=st["hn_plane", i][:, part],
+                    rhs=w2_codes[:, g, :].bitcast(FP8X4),
+                    rhs_scale=w2_planes[:, g, :],
+                    start=(g == 0),
+                    stop=(g == 1),
+                )
+            st["acc2", i] = acc
+
+        def add_b2(i):
+            prediction = work.tile([P, D], F32, tag="prediction", name="prediction")
+            nc.vector.tensor_tensor(out=prediction[:], in0=st["acc2", i][:], in1=b2_all[:], op=ALU.add)
+            st["prediction", i] = prediction
+
+        def fill_slots(i, slots, on_vector=()):
+            if slots[0] == 0:
+                st["slots", i] = outp.tile([P, T, D], F32, tag="slots", name="slots")
+            for j in slots:
+                mask = valid[:, i, j : j + 1]
+                dst = st["slots", i][:, j, :]
+                if j in on_vector:
+                    nc.vector.tensor_scalar_mul(dst, st["prediction", i][:], mask)
+                else:
+                    nc.scalar.activation(out=dst, in_=st["prediction", i][:], func=ACT.Copy, scale=mask)
+
+        def store_slots(i, slots):
+            part = slice(slots[0], slots[0] + len(slots))
+            nc.sync.dma_start(out=out[P * i : P * i + P, part, :], in_=st["slots", i][:, part, :])
+
+        nc.vector.tensor_reduce(out=count[:], in_=cmask[:], axis=X, op=ALU.add)
+        nc.vector.tensor_scalar_max(count_or_1[:], count[:], 1.0)
+        nc.vector.reciprocal(reciprocal[:], count_or_1[:])
+        nc.vector.scalar_tensor_tensor(
+            out=factor[:], in0=count[:], scalar=0.0, in1=reciprocal[:], op0=ALU.is_gt, op1=ALU.mult
+        )
+        b1_all = spread_hidden(b1_cols, "b1_all")
+        interleave_w1(0)
+        interleave_w1(1)
+        spread_factor(0)
+        pool(0, 0)
+        spread_factor(1)
+        pool(0, 1)
+        pool(0, 2)
+        pool(0, 3)
+        quantise_w1(0)
+        quantise_w1(1)
+        load_rows(4)
+        scale_mean(0)
+
+        target_n = keep.tile([P, 8], F32)
+        nc.vector.tensor_reduce(out=target_n[:], in_=tmask[:], axis=X, op=ALU.add)
+        nc.vector.tensor_copy(out=sel1[:], in_=sel1_f32[:])
+        quantise_mean(0)
+        multiply_w1(0)
+        picked = keep.tile([P, 16, 8], BF16)
+        nc.vector.tensor_tensor(
+            out=picked[:],
+            in0=target_n[:].unsqueeze(1).to_broadcast([P, 16, 8]),
+            in1=mod16[:].unsqueeze(2).to_broadcast([P, 16, 8]),
+            op=ALU.mult,
+        )
+        widen_w2(0)
+        n_of_row = keep.tile([P, NT], F32)
+        valid = keep.tile([P, NT, T], F32)
+
+        for s in range(NT):
+            nxt = s + 1
+            if 0 < s < NT - 4:
+                load_rows(s + 4)
+            if s >= 2:
+                interleave_hn(s - 2)
+            if s >= 3:
+                fill_slots(s - 3, HIGH)
+                store_slots(s - 3, LOW + HIGH if s - 3 < FIRST_HALF_STORED else HIGH)
+            if nxt < NT:
+                if s == 0:
+                    pool(nxt, 0)
+                    pool(nxt, 1)
+                pool(nxt, 2)
+                if s != 2:
+                    pool(nxt, 3)
+            if s >= 1:
+                half_statistics(s - 1, 0)
+                half_statistics(s - 1, 1)
+            bias_and_gelu(s, 0)
+            if s >= 1:
+                statistics(s - 1)
+            if s == 2:
+                quantise_w2(1)
+            if s >= 2:
+                quantise_hn(s - 2)
+                multiply_w2(s - 2)
+            if s == 2:
+                pool(nxt, 3)
+            if 1 <= s < NT - 2:
+                pool(s + 2, 0)
+                pool(s + 2, 1)
+            bias_and_gelu(s, 1)
+
+            if s == 0:
+                interleave_w2(0)
+                gamma_all = spread_hidden(gamma_cols, "gamma_all")
+                beta_all = spread_hidden(beta_cols, "beta_all")
+                widen_w2(1)
+                n_psum = psum.tile([P, NT], F32, tag="out", bufs=1, name="n_psum")
+                nc.tensor.matmul(
+                    out=n_psum[:], lhsT=picked[:].rearrange("p q i -> p (q i)"), rhs=sel1[:], start=True, stop=True
+                )
+            if s == 1:
+                nc.vector.tensor_copy(out=n_of_row[:], in_=n_psum[:])
+                interleave_w2(1)
+                b2_all = keep.tile([P, D], BF16)
+                nc.scalar.copy(
+                    out=b2_all[:].rearrange("p (n i) -> p n i", i=4),
+                    in_=turn_vector(b2_cols, 4)[:].rearrange("p i n -> p n i"),
+                )
+                quantise_w2(0)
+
+            if s >= 1:
+                centre(s - 1)
+            if s >= 2:
+                add_b2(s - 2)
+                fill_slots(s - 2, LOW)
+                if s - 2 >= FIRST_HALF_STORED:
+                    store_slots(s - 2, LOW)
+            if nxt < NT:
+                scale_mean(nxt)
+            if s == 1:
+                nc.vector.tensor_tensor(
+                    out=valid[:],
+                    in0=slot_index[:].unsqueeze(1).to_broadcast([P, NT, T]),
+                    in1=n_of_row[:].unsqueeze(2).to_broadcast([P, NT, T]),
+                    op=ALU.is_lt,
+                )
+            if s == 0:
+                pool(s + 2, 0)
+            if s >= 1:
+                normalise(s - 1)
+                transpose_hn(s - 1)
+            if nxt < NT:
+                quantise_mean(nxt)
+                multiply_w1(nxt)
+            if s == 0:
+                pool(s + 2, 1)
+
+        interleave_hn(LAST - 1)
+        fill_slots(LAST - 2, HIGH)
+        store_slots(LAST - 2, HIGH)
+        half_statistics(LAST, 0)
+        half_statistics(LAST, 1)
+        statistics(LAST)
+        centre(LAST)
+        quantise_hn(LAST - 1)
+        multiply_w2(LAST - 1)
+        normalise(LAST)
+        transpose_hn(LAST)
+        add_b2(LAST - 1)
+        interleave_hn(LAST)
+        fill_slots(LAST - 1, LOW, on_vector=(1, 2, 3))
+        store_slots(LAST - 1, LOW)
+        quantise_hn(LAST)
+        multiply_w2(LAST)
+        fill_slots(LAST - 1, HIGH, on_vector=(6, 7))
+        store_slots(LAST - 1, HIGH)
+        add_b2(LAST)
+        for j in range(0, T, 2):
+            pair = (j, j + 1)
+            fill_slots(LAST, pair, on_vector=pair if j == T - 2 else (j + 1,))
+            store_slots(LAST, pair)

@@ -20,9 +20,11 @@ PAIRED_QUARTERS = 19
 
 QUARTERS_PER_LOAD = (1, 1, 1, 2, 4, 4, 4, 4)
 
-FIRST_HALF_STORED = 3
+BIG_BUFFERS = NT + 2
 
-LOW, HIGH = (0, 1, 2, 3), (4, 5, 6, 7)
+VECTOR_SLOTS = 3
+
+FIRST_SPLIT_STORE = NT - 3
 
 F32 = mybir.dt.float32
 BF16 = mybir.dt.bfloat16
@@ -51,37 +53,32 @@ def tile_simplepredictor_t_kernel(
     assert num_targets == T
     with ExitStack() as es:
         keep = es.enter_context(tc.tile_pool(name="keep", bufs=1))
-        ctxp = es.enter_context(tc.tile_pool(name="ctxp", bufs=4))
+        big = es.enter_context(tc.tile_pool(name="big", bufs=BIG_BUFFERS))
         work = es.enter_context(tc.tile_pool(name="work", bufs=2))
-        outp = es.enter_context(tc.tile_pool(name="outp", bufs=4))
         psum = es.enter_context(tc.psum_pool(name="psum", bufs=2))
 
         es.enter_context(tc.manual_schedule())
 
-        def load_vector(vec, per, name):
+        def load_vector(queue, vec, per, name):
             cols = keep.tile([P, per], BF16, name=name)
-            nc.scalar.dma_start(out=cols[:], in_=vec.rearrange("(p i) -> p i", i=per))
+            queue.dma_start(out=cols[:], in_=vec.rearrange("(p i) -> p i", i=per))
             return cols
+
+        def big_tile(shape, dtype, name):
+            return big.tile(shape, dtype, tag="big", align_bytes=64, name=name)
 
         cmask = keep.tile([P, 8, L], BF16)
         nc.scalar.dma_start(out=cmask[:], in_=context_mask.rearrange("(p i) l -> p i l", i=8))
-        b1_cols = load_vector(b1, 8, "b1_cols")
-        w2_scale = keep.tile([P, 2, 4], F32)
-        nc.scalar.dma_start(out=w2_scale[:], in_=W2_scale.rearrange("(g p t) o -> p g (t o)", g=2, t=4))
-        gamma_cols = load_vector(gamma, 8, "gamma_cols")
-        beta_cols = load_vector(beta, 8, "beta_cols")
-        b2_cols = load_vector(b2, 4, "b2_cols")
-        tmask = keep.tile([P, 8, L], BF16)
-        nc.scalar.dma_start(out=tmask[:], in_=target_mask.rearrange("(p i) l -> p i l", i=8))
-
-        w1_rows = keep.tile([P, 4, F], BF16)
-        nc.sync.dma_start(out=w1_rows[:], in_=W1.rearrange("(p t) c -> p t c", t=4))
+        w1_stage = big_tile([P, 2, 4 * F], BF16, "w1_stage")
+        w1_rows = w1_stage[:, 0].rearrange("p (t c) -> p t c", t=4)
+        nc.sync.dma_start(out=w1_rows, in_=W1.rearrange("(p t) c -> p t c", t=4))
+        b1_cols = load_vector(nc.scalar, b1, 8, "b1_cols")
 
         rows = context_repr.rearrange("b l d -> (b l) d")
         ctx = {}
 
         def load_rows(i):
-            ctx[i] = ctxp.tile([P, QUARTERS, BLOCKS, D], BF16, tag="ctx", name="ctx")
+            ctx[i] = big_tile([P, QUARTERS, BLOCKS, D], BF16, "ctx")
             q = 0
             while q < QUARTERS:
                 r = rows_per_partition(i, q)
@@ -100,7 +97,16 @@ def tile_simplepredictor_t_kernel(
         nc.sync.dma_start(
             out=w2_bytes[:].rearrange("p g t n -> p g (t n)"), in_=W2_bytes.rearrange("(g p t) n -> p g (t n)", g=2, t=4)
         )
-        for i in range(1, 4):
+        w2_scale = keep.tile([P, 2, 4], F32)
+        nc.sync.dma_start(out=w2_scale[:], in_=W2_scale.rearrange("(g p t) o -> p g (t o)", g=2, t=4))
+        gamma_cols = load_vector(nc.sync, gamma, 8, "gamma_cols")
+        beta_cols = load_vector(nc.sync, beta, 8, "beta_cols")
+        load_rows(1)
+        b2_cols = load_vector(nc.sync, b2, 4, "b2_cols")
+        tmask = keep.tile([P, 8, L], BF16)
+        nc.sync.dma_start(out=tmask[:], in_=target_mask.rearrange("(p i) l -> p i l", i=8))
+        w2_stage = big_tile([P, 2, 8 * D], BF16, "w2_stage")
+        for i in range(2, NT):
             load_rows(i)
 
         ident_f32 = keep.tile([P, P], F32)
@@ -116,8 +122,6 @@ def tile_simplepredictor_t_kernel(
         table_out = keep.tile([P, 1], F32)
         nc.scalar.activation(out=table_out[:], in_=table_in[:], func=ACT.Gelu)
 
-        ident_bf16 = keep.tile([P, P], BF16)
-        nc.vector.tensor_copy(out=ident_bf16[:], in_=ident_f32[:])
         sel2_f32 = keep.tile([P, 16], F32)
         sel2 = keep.tile([P, 16], BF16)
         nc.vector.tensor_reduce(out=sel2_f32[:], in_=ident_f32[:].rearrange("p (j q) -> p j q", q=8), axis=X, op=ALU.add)
@@ -146,25 +150,23 @@ def tile_simplepredictor_t_kernel(
             )
 
         def turn_vector(cols, per):
-            turned = psum.tile([P, per, P], BF16, tag="h", bufs=4, name="turned")
+            turned = psum.tile([P, per, P], F32, tag="h", bufs=4, name="turned")
+            words = cols[:].bitcast(F32)
             for i in range(per):
-                nc.tensor.transpose(turned[:, i, :], cols[:, i : i + 1].to_broadcast([P, P]), ident_bf16[:])
+                nc.tensor.transpose(turned[:, i, :], words[:, i : i + 1].to_broadcast([P, P]), ident_f32[:])
             return turned
 
         def spread_hidden(cols, name):
             dst = keep.tile([P, F], BF16, name=name)
-            src = turn_vector(cols, 8)[:].rearrange("p (v u e) n -> p u n v e", u=2, e=2)
-            for g in range(2):
-                for u in range(2):
-                    nc.scalar.copy(
-                        out=dst[:, hidden_block(g, u)].rearrange("p (n v e) -> p n v e", v=2, e=2),
-                        in_=src[:, u, 64 * g : 64 * g + 64],
-                    )
+            nc.scalar.copy(
+                out=dst[:].bitcast(F32).rearrange("p (g u n v) -> p g u n v", g=2, u=2, v=2),
+                in_=turn_vector(cols, 4)[:].rearrange("p (v u) (g n) -> p g u n v", u=2, g=2),
+            )
             return dst
 
         w1_codes = keep.tile([P, F], U32, align_bytes=64)
         w1_planes = keep.tile([P, F], U8, align_bytes=64)
-        w1_words = [keep.tile([P, HALF, 4], BF16, align_bytes=64, name="w1_words%d" % g) for g in range(2)]
+        w1_words = [w1_stage[:, 1, 4 * HALF * g : 4 * HALF * (g + 1)].rearrange("p (c t) -> p c t", t=4) for g in range(2)]
 
         def interleave_w1(g):
             copy = (nc.vector.tensor_copy, nc.scalar.copy)[g]
@@ -177,31 +179,31 @@ def tile_simplepredictor_t_kernel(
             nc.vector.quantize_mx(
                 out=w1_codes[:, cols].bitcast(FP8X4),
                 scales=w1_planes[:, cols],
-                in_=w1_words[g][:].rearrange("p c t -> p (c t)"),
+                in_=w1_words[g].rearrange("p c t -> p (c t)"),
             )
 
-        w2_rows = keep.tile([P, 2, 4, D], BF16)
-        w2_words = [keep.tile([P, D, 4], BF16, align_bytes=64, name="w2_words%d" % g) for g in range(2)]
+        w2_rows = w2_stage[:, 0].rearrange("p (g t n) -> p g t n", g=2, t=4)
+        w2_words = [w2_stage[:, 1, 4 * D * g : 4 * D * (g + 1)].rearrange("p (n t) -> p n t", t=4) for g in range(2)]
         w2_codes = keep.tile([P, 2, D], U32, align_bytes=64)
         w2_planes = keep.tile([P, 2, D], U8, align_bytes=64)
 
-        def widen_w2(g):
-            for t in range(4):
-                nc.scalar.activation(
-                    out=w2_rows[:, g, t, :],
-                    in_=w2_bytes[:, g, t, :].bitcast(FP8),
-                    func=ACT.Copy,
-                    scale=w2_scale[:, g, t : t + 1],
-                )
+        def widen_w2(g, positions):
+            for t in positions:
+                dst, src, scale = w2_rows[:, g, t, :], w2_bytes[:, g, t, :].bitcast(FP8), w2_scale[:, g, t : t + 1]
+                if g == 0:
+                    nc.vector.tensor_scalar(out=dst, in0=src, scalar1=scale, scalar2=None, op0=ALU.mult)
+                else:
+                    nc.scalar.activation(out=dst, in_=src, func=ACT.Copy, scale=scale)
 
         def interleave_w2(g):
-            nc.scalar.copy(out=w2_words[g][:], in_=w2_rows[:, g].rearrange("p t n -> p n t"))
+            copy = (nc.vector.tensor_copy, nc.scalar.copy)[g]
+            copy(out=w2_words[g], in_=w2_rows[:, g].rearrange("p t n -> p n t"))
 
         def quantise_w2(g):
             nc.vector.quantize_mx(
                 out=w2_codes[:, g, :].bitcast(FP8X4),
                 scales=w2_planes[:, g, :],
-                in_=w2_words[g][:].rearrange("p n t -> p (n t)"),
+                in_=w2_words[g].rearrange("p n t -> p (n t)"),
             )
 
         st = {}
@@ -257,35 +259,51 @@ def tile_simplepredictor_t_kernel(
                 )
                 st["acc", i, g] = acc
 
-        def bias_and_gelu(i, g):
-            if g == 0:
-                st["v", i] = work.tile([P, F], F32, tag="v", name="v")
-                st["h", i] = work.tile([P, F], F32, tag="h", name="h")
-            cols = slice(HALF * g, HALF * g + HALF)
-            v = st["v", i][:, cols]
-            nc.vector.tensor_tensor(out=v, in0=st["acc", i, g][:], in1=b1_all[:, cols], op=ALU.add)
-            nc.scalar.activation(out=st["h", i][:, cols], in_=v, func=ACT.Gelu)
+        def add_b1(i):
+            v = work.tile([P, F], F32, tag="v", name="v")
+            for g in range(2):
+                cols = slice(HALF * g, HALF * g + HALF)
+                nc.vector.tensor_tensor(out=v[:, cols], in0=st["acc", i, g][:], in1=b1_all[:, cols], op=ALU.add)
+            st["v", i] = v
 
-        def half_statistics(i, g):
-            if g == 0:
-                st["half_stats", i] = work.tile([P, 2, 6], F32, tag="half_stats", name="half_stats")
-            nc.vector.bn_stats(out=st["half_stats", i][:, g, :], in_=st["h", i][:, HALF * g : HALF * g + HALF])
+        def gelu(i):
+            h = work.tile([P, F], F32, tag="h", name="h")
+            total = work.tile([P, 1], F32, tag="total", name="total")
+            nc.scalar.activation(out=h[:], in_=st["v", i][:], func=ACT.Gelu, accum_out=total[:])
+            st["h", i], st["total", i] = h, total
 
-        def statistics(i):
-            stats = work.tile([P, 2], F32, tag="stats", name="stats")
-            nc.vector.bn_aggr(out=stats[:], in_=st["half_stats", i][:].rearrange("p g s -> p (g s)"))
+        def mean_of_h(i):
+            mu = work.tile([P, 1], F32, tag="mu", name="mu")
+            nc.scalar.activation(out=mu[:], in_=st["total", i][:], func=ACT.Copy, scale=1.0 / F)
+            st["mu", i] = mu
+
+        def squares(i):
+            scaled_var = work.tile([P, 1], F32, tag="scaled_var", name="scaled_var")
+            nc.scalar.activation(
+                out=st["v", i][:],
+                in_=st["h", i][:],
+                func=ACT.Square,
+                scale=-float(F),
+                bias=st["total", i][:],
+                accum_out=scaled_var[:],
+            )
+            st["scaled_var", i] = scaled_var
+
+        def inverse_deviation(i):
             var_eps = work.tile([P, 1], F32, tag="var_eps", name="var_eps")
-            nc.gpsimd.tensor_scalar_add(var_eps[:], stats[:, 1:2], LN_EPS)
+            nc.scalar.activation(
+                out=var_eps[:], in_=st["scaled_var", i][:], func=ACT.Copy, scale=1.0 / F**3, bias=LN_EPS
+            )
             rstd = work.tile([P, 1], F32, tag="rstd", name="rstd")
             nc.gpsimd.tensor_tensor(out=rstd[:], in0=var_eps[:], in1=minus_half[:], op=ALU.pow)
-            st["stats", i], st["rstd", i] = stats, rstd
+            st["rstd", i] = rstd
 
         def centre(i):
             centred = work.tile([P, F], F32, tag="centred", name="centred")
             nc.vector.scalar_tensor_tensor(
                 out=centred[:],
                 in0=st["h", i][:],
-                scalar=st["stats", i][:, 0:1],
+                scalar=st["mu", i][:],
                 in1=gamma_all[:],
                 op0=ALU.subtract,
                 op1=ALU.mult,
@@ -342,20 +360,19 @@ def tile_simplepredictor_t_kernel(
             nc.vector.tensor_tensor(out=prediction[:], in0=st["acc2", i][:], in1=b2_all[:], op=ALU.add)
             st["prediction", i] = prediction
 
-        def fill_slots(i, slots, on_vector=()):
-            if slots[0] == 0:
-                st["slots", i] = outp.tile([P, T, D], F32, tag="slots", name="slots")
+        def fill_slots(i, slots, on_vector):
+            if ("slots", i) not in st:
+                st["slots", i] = big_tile([P, T, D], F32, "slots")
             for j in slots:
                 mask = valid[:, i, j : j + 1]
                 dst = st["slots", i][:, j, :]
-                if j in on_vector:
+                if on_vector:
                     nc.vector.tensor_scalar_mul(dst, st["prediction", i][:], mask)
                 else:
                     nc.scalar.activation(out=dst, in_=st["prediction", i][:], func=ACT.Copy, scale=mask)
 
-        def store_slots(i, slots):
-            part = slice(slots[0], slots[0] + len(slots))
-            nc.sync.dma_start(out=out[P * i : P * i + P, part, :], in_=st["slots", i][:, part, :])
+        def store_slots(i, first, end):
+            nc.sync.dma_start(out=out[P * i : P * i + P, first:end, :], in_=st["slots", i][:, first:end, :])
 
         nc.vector.tensor_reduce(out=count[:], in_=cmask[:], axis=X, op=ALU.add)
         nc.vector.tensor_scalar_max(count_or_1[:], count[:], 1.0)
@@ -363,137 +380,113 @@ def tile_simplepredictor_t_kernel(
         nc.vector.scalar_tensor_tensor(
             out=factor[:], in0=count[:], scalar=0.0, in1=reciprocal[:], op0=ALU.is_gt, op1=ALU.mult
         )
-        b1_all = spread_hidden(b1_cols, "b1_all")
         interleave_w1(0)
         interleave_w1(1)
+        b1_all = spread_hidden(b1_cols, "b1_all")
         spread_factor(0)
         pool(0, 0)
         spread_factor(1)
         pool(0, 1)
         pool(0, 2)
         pool(0, 3)
+        nc.vector.tensor_copy(out=sel1[:], in_=sel1_f32[:])
         quantise_w1(0)
         quantise_w1(1)
-        load_rows(4)
         scale_mean(0)
 
         target_n = keep.tile([P, 8], F32)
-        nc.vector.tensor_reduce(out=target_n[:], in_=tmask[:], axis=X, op=ALU.add)
-        nc.vector.tensor_copy(out=sel1[:], in_=sel1_f32[:])
-        quantise_mean(0)
-        multiply_w1(0)
         picked = keep.tile([P, 16, 8], BF16)
-        nc.vector.tensor_tensor(
-            out=picked[:],
-            in0=target_n[:].unsqueeze(1).to_broadcast([P, 16, 8]),
-            in1=mod16[:].unsqueeze(2).to_broadcast([P, 16, 8]),
-            op=ALU.mult,
-        )
-        widen_w2(0)
         n_of_row = keep.tile([P, NT], F32)
         valid = keep.tile([P, NT, T], F32)
 
-        for s in range(NT):
-            nxt = s + 1
-            if 0 < s < NT - 4:
-                load_rows(s + 4)
-            if s >= 2:
-                interleave_hn(s - 2)
-            if s >= 3:
-                fill_slots(s - 3, HIGH)
-                store_slots(s - 3, LOW + HIGH if s - 3 < FIRST_HALF_STORED else HIGH)
-            if nxt < NT:
-                if s == 0:
-                    pool(nxt, 0)
-                    pool(nxt, 1)
-                pool(nxt, 2)
-                if s != 2:
-                    pool(nxt, 3)
-            if s >= 1:
-                half_statistics(s - 1, 0)
-                half_statistics(s - 1, 1)
-            bias_and_gelu(s, 0)
-            if s >= 1:
-                statistics(s - 1)
-            if s == 2:
-                quantise_w2(1)
-            if s >= 2:
-                quantise_hn(s - 2)
-                multiply_w2(s - 2)
-            if s == 2:
-                pool(nxt, 3)
-            if 1 <= s < NT - 2:
-                pool(s + 2, 0)
-                pool(s + 2, 1)
-            bias_and_gelu(s, 1)
+        def live(i):
+            return 0 <= i < NT
 
+        for s in range(NT + 3):
+            hid, nrm, sec, fil, nxt = s, s - 1, s - 2, s - 3, s + 1
+            on_vec = VECTOR_SLOTS if live(hid) else 5
+            vec_slots, sca_slots = list(range(on_vec)), list(range(on_vec, T))
+
+            if live(nrm):
+                squares(nrm)
+            if live(fil):
+                fill_slots(fil, vec_slots[:1], True)
+            if live(hid):
+                quantise_mean(hid)
+                multiply_w1(hid)
+            if live(nxt):
+                pool(nxt, 0)
             if s == 0:
-                interleave_w2(0)
+                widen_w2(0, (0, 1))
+                widen_w2(1, (0, 1, 2, 3))
+            if live(fil):
+                fill_slots(fil, vec_slots[1:], True)
+                if fil >= FIRST_SPLIT_STORE:
+                    store_slots(fil, 0, on_vec)
+                fill_slots(fil, sca_slots[:1], False)
+            if live(nrm):
+                inverse_deviation(nrm)
+            if s == 1:
+                interleave_w2(1)
+            if live(fil):
+                fill_slots(fil, sca_slots[1:-1], False)
+            if live(sec):
+                quantise_hn(sec)
+                multiply_w2(sec)
+            if live(nrm):
+                centre(nrm)
+            if live(hid):
+                add_b1(hid)
+                gelu(hid)
+            if s == 0:
+                widen_w2(0, (2, 3))
                 gamma_all = spread_hidden(gamma_cols, "gamma_all")
                 beta_all = spread_hidden(beta_cols, "beta_all")
-                widen_w2(1)
+                interleave_w2(0)
+            if live(nxt):
+                pool(nxt, 1)
+                pool(nxt, 2)
+                pool(nxt, 3)
+            if live(fil):
+                fill_slots(fil, sca_slots[-1:], False)
+                store_slots(fil, on_vec if fil >= FIRST_SPLIT_STORE else 0, T)
+            if live(nrm):
+                normalise(nrm)
+                transpose_hn(nrm)
+            if s == 0:
+                quantise_w2(0)
+            if s == 1:
+                nc.vector.tensor_reduce(out=target_n[:], in_=tmask[:], axis=X, op=ALU.add)
+                nc.vector.tensor_tensor(
+                    out=picked[:],
+                    in0=target_n[:].unsqueeze(1).to_broadcast([P, 16, 8]),
+                    in1=mod16[:].unsqueeze(2).to_broadcast([P, 16, 8]),
+                    op=ALU.mult,
+                )
+                quantise_w2(1)
                 n_psum = psum.tile([P, NT], F32, tag="out", bufs=1, name="n_psum")
                 nc.tensor.matmul(
                     out=n_psum[:], lhsT=picked[:].rearrange("p q i -> p (q i)"), rhs=sel1[:], start=True, stop=True
                 )
-            if s == 1:
-                nc.vector.tensor_copy(out=n_of_row[:], in_=n_psum[:])
-                interleave_w2(1)
                 b2_all = keep.tile([P, D], BF16)
                 nc.scalar.copy(
-                    out=b2_all[:].rearrange("p (n i) -> p n i", i=4),
-                    in_=turn_vector(b2_cols, 4)[:].rearrange("p i n -> p n i"),
+                    out=b2_all[:].bitcast(F32).rearrange("p (n i) -> p n i", i=2),
+                    in_=turn_vector(b2_cols, 2)[:].rearrange("p i n -> p n i"),
                 )
-                quantise_w2(0)
-
-            if s >= 1:
-                centre(s - 1)
-            if s >= 2:
-                add_b2(s - 2)
-                fill_slots(s - 2, LOW)
-                if s - 2 >= FIRST_HALF_STORED:
-                    store_slots(s - 2, LOW)
-            if nxt < NT:
+            if live(sec):
+                add_b2(sec)
+            if live(hid):
+                mean_of_h(hid)
+            if live(nrm):
+                interleave_hn(nrm)
+            if live(nxt):
                 scale_mean(nxt)
             if s == 1:
+                nc.vector.tensor_copy(out=n_of_row[:], in_=n_psum[:])
+            if s == 2:
                 nc.vector.tensor_tensor(
                     out=valid[:],
                     in0=slot_index[:].unsqueeze(1).to_broadcast([P, NT, T]),
                     in1=n_of_row[:].unsqueeze(2).to_broadcast([P, NT, T]),
                     op=ALU.is_lt,
                 )
-            if s == 0:
-                pool(s + 2, 0)
-            if s >= 1:
-                normalise(s - 1)
-                transpose_hn(s - 1)
-            if nxt < NT:
-                quantise_mean(nxt)
-                multiply_w1(nxt)
-            if s == 0:
-                pool(s + 2, 1)
-
-        interleave_hn(LAST - 1)
-        fill_slots(LAST - 2, HIGH)
-        store_slots(LAST - 2, HIGH)
-        half_statistics(LAST, 0)
-        half_statistics(LAST, 1)
-        statistics(LAST)
-        centre(LAST)
-        quantise_hn(LAST - 1)
-        multiply_w2(LAST - 1)
-        normalise(LAST)
-        transpose_hn(LAST)
-        add_b2(LAST - 1)
-        interleave_hn(LAST)
-        fill_slots(LAST - 1, LOW, on_vector=(1, 2, 3))
-        store_slots(LAST - 1, LOW)
-        quantise_hn(LAST)
-        multiply_w2(LAST)
-        fill_slots(LAST - 1, HIGH, on_vector=(6, 7))
-        store_slots(LAST - 1, HIGH)
-        add_b2(LAST)
-        for j in range(0, T, 2):
-            pair = (j, j + 1)
-            fill_slots(LAST, pair, on_vector=pair if j == T - 2 else (j + 1,))
-            store_slots(LAST, pair)

@@ -393,100 +393,136 @@ def tile_simplepredictor_t_kernel(
         quantise_w1(0)
         quantise_w1(1)
         scale_mean(0)
+        pool(1, 0)
+        widen_w2(0, (0,))
+        quantise_mean(0)
+        multiply_w1(0)
+        widen_w2(1, (0, 1, 2, 3))
+        widen_w2(0, (1, 2, 3))
+        pool(1, 1)
+        pool(1, 2)
 
         target_n = keep.tile([P, 8], F32)
         picked = keep.tile([P, 16, 8], BF16)
         n_of_row = keep.tile([P, NT], F32)
         valid = keep.tile([P, NT, T], F32)
 
-        def live(i):
-            return 0 <= i < NT
+        def count_targets():
+            nc.vector.tensor_tensor(
+                out=picked[:],
+                in0=target_n[:].unsqueeze(1).to_broadcast([P, 16, 8]),
+                in1=mod16[:].unsqueeze(2).to_broadcast([P, 16, 8]),
+                op=ALU.mult,
+            )
+            n_psum = psum.tile([P, NT], F32, tag="out", bufs=1, name="n_psum")
+            nc.tensor.matmul(
+                out=n_psum[:], lhsT=picked[:].rearrange("p q i -> p (q i)"), rhs=sel1[:], start=True, stop=True
+            )
+            st["n_psum"] = n_psum
 
-        for s in range(NT + 3):
-            hid, nrm, sec, fil, nxt = s, s - 1, s - 2, s - 3, s + 1
-            on_vec = VECTOR_SLOTS if live(hid) else 5
-            vec_slots, sca_slots = list(range(on_vec)), list(range(on_vec, T))
+        def spread_b2():
+            dst = keep.tile([P, D], BF16, name="b2_all")
+            nc.scalar.copy(
+                out=dst[:].bitcast(F32).rearrange("p (n i) -> p n i", i=2),
+                in_=turn_vector(b2_cols, 2)[:].rearrange("p i n -> p n i"),
+            )
+            return dst
 
-            if live(nrm):
-                squares(nrm)
-            if live(fil):
-                fill_slots(fil, vec_slots[:1], True)
-            if live(hid):
-                quantise_mean(hid)
-                multiply_w1(hid)
-            if live(nxt):
-                pool(nxt, 0)
+        def when(i, stage, *args):
+            if 0 <= i < NT:
+                stage(i, *args)
+
+        for s in range(LAST):
+            when(s - 3, fill_slots, range(T - 2, T), False)
+            when(s - 3, store_slots, T // 2, T)
+            when(s, add_b1)
+            when(s + 1, pool, 3)
+            when(s - 2, add_b2)
+            when(s, gelu)
+            when(s - 2, fill_slots, range(1), False)
             if s == 0:
-                widen_w2(0, (0, 1))
-                widen_w2(1, (0, 1, 2, 3))
-            if live(fil):
-                fill_slots(fil, vec_slots[1:], True)
-                if fil >= FIRST_SPLIT_STORE:
-                    store_slots(fil, 0, on_vec)
-                fill_slots(fil, sca_slots[:1], False)
-            if live(nrm):
-                inverse_deviation(nrm)
-            if s == 1:
-                interleave_w2(1)
-            if live(fil):
-                fill_slots(fil, sca_slots[1:-1], False)
-            if live(sec):
-                quantise_hn(sec)
-                multiply_w2(sec)
-            if live(nrm):
-                centre(nrm)
-            if live(hid):
-                add_b1(hid)
-                gelu(hid)
-            if s == 0:
-                widen_w2(0, (2, 3))
                 gamma_all = spread_hidden(gamma_cols, "gamma_all")
-                beta_all = spread_hidden(beta_cols, "beta_all")
                 interleave_w2(0)
-            if live(nxt):
-                pool(nxt, 1)
-                pool(nxt, 2)
-                pool(nxt, 3)
-            if live(fil):
-                fill_slots(fil, sca_slots[-1:], False)
-                store_slots(fil, on_vec if fil >= FIRST_SPLIT_STORE else 0, T)
-            if live(nrm):
-                normalise(nrm)
-                transpose_hn(nrm)
+            if s == 1:
+                b2_all = spread_b2()
+            when(s, mean_of_h)
+            when(s, squares)
+            when(s + 2, pool, 0)
+            when(s - 1, normalise)
+            when(s - 1, transpose_hn)
+            when(s - 1, interleave_hn)
+            when(s + 1, scale_mean)
+            when(s - 2, fill_slots, range(1, 2), True)
             if s == 0:
                 quantise_w2(0)
+                beta_all = spread_hidden(beta_cols, "beta_all")
             if s == 1:
+                nc.vector.tensor_copy(out=n_of_row[:], in_=st["n_psum"][:])
+            when(s + 1, quantise_mean)
+            when(s + 2, pool, 1)
+            when(s + 1, multiply_w1)
+            when(s + 2, pool, 2)
+            when(s, centre)
+            when(s - 2, fill_slots, range(2, 3), True)
+            when(s - 2, fill_slots, range(3, 4), False)
+            when(s - 2, store_slots, 0, T // 2)
+            if s == 0:
                 nc.vector.tensor_reduce(out=target_n[:], in_=tmask[:], axis=X, op=ALU.add)
-                nc.vector.tensor_tensor(
-                    out=picked[:],
-                    in0=target_n[:].unsqueeze(1).to_broadcast([P, 16, 8]),
-                    in1=mod16[:].unsqueeze(2).to_broadcast([P, 16, 8]),
-                    op=ALU.mult,
-                )
-                quantise_w2(1)
-                n_psum = psum.tile([P, NT], F32, tag="out", bufs=1, name="n_psum")
-                nc.tensor.matmul(
-                    out=n_psum[:], lhsT=picked[:].rearrange("p q i -> p (q i)"), rhs=sel1[:], start=True, stop=True
-                )
-                b2_all = keep.tile([P, D], BF16)
-                nc.scalar.copy(
-                    out=b2_all[:].bitcast(F32).rearrange("p (n i) -> p n i", i=2),
-                    in_=turn_vector(b2_cols, 2)[:].rearrange("p i n -> p n i"),
-                )
-            if live(sec):
-                add_b2(sec)
-            if live(hid):
-                mean_of_h(hid)
-            if live(nrm):
-                interleave_hn(nrm)
-            if live(nxt):
-                scale_mean(nxt)
+                count_targets()
             if s == 1:
-                nc.vector.tensor_copy(out=n_of_row[:], in_=n_psum[:])
-            if s == 2:
+                quantise_w2(1)
                 nc.vector.tensor_tensor(
                     out=valid[:],
                     in0=slot_index[:].unsqueeze(1).to_broadcast([P, NT, T]),
                     in1=n_of_row[:].unsqueeze(2).to_broadcast([P, NT, T]),
                     op=ALU.is_lt,
                 )
+            when(s - 1, quantise_hn)
+            when(s - 1, multiply_w2)
+            when(s - 2, fill_slots, range(4, 5), True)
+            when(s - 2, fill_slots, range(5, 6), False)
+            when(s, inverse_deviation)
+            if s == 0:
+                interleave_w2(1)
+
+        fill_slots(LAST - 3, range(T - 2, T), False)
+        store_slots(LAST - 3, T // 2, T)
+        add_b1(LAST)
+        add_b2(LAST - 2)
+        gelu(LAST)
+        fill_slots(LAST - 2, range(1), False)
+        mean_of_h(LAST)
+        squares(LAST)
+        normalise(LAST - 1)
+        transpose_hn(LAST - 1)
+        interleave_hn(LAST - 1)
+        inverse_deviation(LAST)
+        fill_slots(LAST - 2, range(1, 4), True)
+        store_slots(LAST - 2, 0, T // 2)
+        centre(LAST)
+        quantise_hn(LAST - 1)
+        multiply_w2(LAST - 1)
+        fill_slots(LAST - 2, range(4, 5), True)
+        fill_slots(LAST - 2, range(5, 8), False)
+        store_slots(LAST - 2, T // 2, T)
+        normalise(LAST)
+        transpose_hn(LAST)
+        interleave_hn(LAST)
+        add_b2(LAST - 1)
+        fill_slots(LAST - 1, range(3), True)
+        fill_slots(LAST - 1, range(3, 4), False)
+        store_slots(LAST - 1, 0, T // 2)
+        quantise_hn(LAST)
+        multiply_w2(LAST)
+        fill_slots(LAST - 1, range(4, 6), True)
+        fill_slots(LAST - 1, range(6, 8), False)
+        store_slots(LAST - 1, T // 2, T)
+        add_b2(LAST)
+        fill_slots(LAST, range(0, 2), True)
+        fill_slots(LAST, range(2, 3), False)
+        store_slots(LAST, 0, 3)
+        fill_slots(LAST, range(3, 5), True)
+        fill_slots(LAST, range(5, 6), False)
+        store_slots(LAST, 3, 6)
+        fill_slots(LAST, range(6, 8), True)
+        store_slots(LAST, 6, 8)

@@ -12,19 +12,20 @@ FLOPS = 2 * B * D * F + 2 * B * F * D
 P = 128
 NT = B // P
 LAST = NT - 1
+WHOLE = (0, LAST)
 HALF = F // 2
 QUARTERS = 4
 BLOCKS = 4
 
-PAIRED_QUARTERS = 19
+PAIRED_QUARTERS = 32
 
-QUARTERS_PER_LOAD = (1, 1, 1, 2, 4, 4, 4, 4)
+QUARTERS_PER_LOAD = (1, 1, 1, 2, 2, 2, 2, 4)
 
 BIG_BUFFERS = NT + 2
 
 VECTOR_SLOTS = 3
 
-FIRST_SPLIT_STORE = NT - 3
+FIRST_SPLIT_STORE = NT - 4
 
 F32 = mybir.dt.float32
 BF16 = mybir.dt.bfloat16
@@ -78,6 +79,15 @@ def tile_simplepredictor_t_kernel(
         ctx = {}
 
         def load_rows(i):
+            if i in WHOLE:
+                ctx[i] = big_tile([P, QUARTERS, 4 * D], BF16, "ctx")
+                src = context_repr[P * i : P * i + P].rearrange("b (q l) d -> b q (l d)", q=QUARTERS)
+                for q in range(0, QUARTERS, QUARTERS_PER_LOAD[i]):
+                    part = slice(q, q + QUARTERS_PER_LOAD[i])
+                    nc.sync.dma_start(
+                        out=ctx[i][:, part].rearrange("b q x -> b (q x)"), in_=src[:, part].rearrange("b q x -> b (q x)")
+                    )
+                return
             ctx[i] = big_tile([P, QUARTERS, BLOCKS, D], BF16, "ctx")
             q = 0
             while q < QUARTERS:
@@ -144,7 +154,7 @@ def tile_simplepredictor_t_kernel(
             for i in range(4):
                 column = factor[:, 4 * k + i : 4 * k + i + 1]
                 nc.tensor.transpose(turned[:, i, :], column.to_broadcast([P, P]), ident_f32[:])
-            nc.vector.tensor_copy(
+            nc.scalar.copy(
                 out=factor_all[:].rearrange("p (n i) -> p n i", i=8)[:, :, 4 * k : 4 * k + 4],
                 in_=turned[:].rearrange("p i n -> p n i"),
             )
@@ -225,6 +235,28 @@ def tile_simplepredictor_t_kernel(
                             start=(e == 0),
                             stop=(e == r - 1),
                         )
+
+        def add_pairs(i, q):
+            if q == 0:
+                st["pairs", i] = big_tile([P, 4, QUARTERS, 2 * P], F32, "pairs")
+            x = ctx[i][:, q].rearrange("b (h c n t) -> b h c t n", h=2, n=4, t=4)
+            nc.vector.tensor_tensor(
+                out=st["pairs", i][:, :, q].rearrange("b t (c n) -> b c t n", n=4), in0=x[:, 0], in1=x[:, 1], op=ALU.add
+            )
+
+        def pool_pairs(i, t):
+            if t == 0:
+                st["sums", i] = psum.tile([P, 4, P], F32, tag="pool", name="sums")
+            words = st["pairs", i][:, t].rearrange("b q (j p) -> b (q j) p", p=P)
+            for j in range(L // 2):
+                nc.tensor.matmul(
+                    out=st["sums", i][:, t, :],
+                    lhsT=words[:, j],
+                    rhs=ident_f32[:],
+                    is_transpose=True,
+                    start=(j == 0),
+                    stop=(j == L // 2 - 1),
+                )
 
         def scale_mean(i):
             mean = work.tile([P, P, 4], BF16, align_bytes=64, tag="mean", name="mean")
@@ -382,23 +414,24 @@ def tile_simplepredictor_t_kernel(
         )
         interleave_w1(0)
         interleave_w1(1)
-        b1_all = spread_hidden(b1_cols, "b1_all")
         spread_factor(0)
-        pool(0, 0)
         spread_factor(1)
-        pool(0, 1)
-        pool(0, 2)
-        pool(0, 3)
+        b1_all = spread_hidden(b1_cols, "b1_all")
+        add_pairs(0, 0)
+        add_pairs(0, 1)
+        add_pairs(0, 2)
+        add_pairs(0, 3)
+        for t in range(4):
+            pool_pairs(0, t)
         nc.vector.tensor_copy(out=sel1[:], in_=sel1_f32[:])
         quantise_w1(0)
         quantise_w1(1)
+        widen_w2(1, (0, 1, 2, 3))
+        widen_w2(0, (0, 1, 2, 3))
         scale_mean(0)
         pool(1, 0)
-        widen_w2(0, (0,))
         quantise_mean(0)
         multiply_w1(0)
-        widen_w2(1, (0, 1, 2, 3))
-        widen_w2(0, (1, 2, 3))
         pool(1, 1)
         pool(1, 2)
 
@@ -433,39 +466,53 @@ def tile_simplepredictor_t_kernel(
                 stage(i, *args)
 
         for s in range(LAST):
-            when(s - 3, fill_slots, range(T - 2, T), False)
-            when(s - 3, store_slots, T // 2, T)
+            whole = s + 2 in WHOLE
+            plain = s + 2 < NT and not whole
+            when(s - 3, fill_slots, range(5, 7), False)
             when(s, add_b1)
-            when(s + 1, pool, 3)
-            when(s - 2, add_b2)
+            if s + 1 not in WHOLE:
+                pool(s + 1, 3)
+            if whole:
+                add_pairs(s + 2, 0)
             when(s, gelu)
-            when(s - 2, fill_slots, range(1), False)
+            when(s - 3, fill_slots, range(7, 8), False)
+            when(s - 3, store_slots, T // 2 if s - 3 >= FIRST_SPLIT_STORE else 0, T)
             if s == 0:
                 gamma_all = spread_hidden(gamma_cols, "gamma_all")
                 interleave_w2(0)
             if s == 1:
                 b2_all = spread_b2()
             when(s, mean_of_h)
-            when(s, squares)
-            when(s + 2, pool, 0)
             when(s - 1, normalise)
             when(s - 1, transpose_hn)
             when(s - 1, interleave_hn)
+            when(s, squares)
+            if plain:
+                pool(s + 2, 0)
+            when(s - 2, add_b2)
+            if whole:
+                add_pairs(s + 2, 1)
             when(s + 1, scale_mean)
-            when(s - 2, fill_slots, range(1, 2), True)
+            if whole:
+                add_pairs(s + 2, 2)
+            when(s - 2, fill_slots, range(1), not whole)
             if s == 0:
                 quantise_w2(0)
                 beta_all = spread_hidden(beta_cols, "beta_all")
             if s == 1:
                 nc.vector.tensor_copy(out=n_of_row[:], in_=st["n_psum"][:])
             when(s + 1, quantise_mean)
-            when(s + 2, pool, 1)
+            if whole:
+                add_pairs(s + 2, 3)
+            if plain:
+                pool(s + 2, 1)
             when(s + 1, multiply_w1)
-            when(s + 2, pool, 2)
+            if plain:
+                pool(s + 2, 2)
+            if whole:
+                pool_pairs(s + 2, 0)
+                pool_pairs(s + 2, 1)
             when(s, centre)
-            when(s - 2, fill_slots, range(2, 3), True)
-            when(s - 2, fill_slots, range(3, 4), False)
-            when(s - 2, store_slots, 0, T // 2)
             if s == 0:
                 nc.vector.tensor_reduce(out=target_n[:], in_=tmask[:], axis=X, op=ALU.add)
                 count_targets()
@@ -479,25 +526,31 @@ def tile_simplepredictor_t_kernel(
                 )
             when(s - 1, quantise_hn)
             when(s - 1, multiply_w2)
-            when(s - 2, fill_slots, range(4, 5), True)
-            when(s - 2, fill_slots, range(5, 6), False)
+            if whole:
+                pool_pairs(s + 2, 2)
+                pool_pairs(s + 2, 3)
+            when(s - 2, fill_slots, range(1, 3), not whole)
+            when(s - 2, fill_slots, range(3, 4), False)
+            if s - 2 >= FIRST_SPLIT_STORE:
+                store_slots(s - 2, 0, T // 2)
             when(s, inverse_deviation)
+            when(s - 2, fill_slots, range(4, 5), False)
             if s == 0:
                 interleave_w2(1)
 
-        fill_slots(LAST - 3, range(T - 2, T), False)
-        store_slots(LAST - 3, T // 2, T)
+        fill_slots(LAST - 3, range(5, 7), False)
         add_b1(LAST)
-        add_b2(LAST - 2)
         gelu(LAST)
-        fill_slots(LAST - 2, range(1), False)
+        fill_slots(LAST - 3, range(7, 8), False)
+        store_slots(LAST - 3, T // 2, T)
         mean_of_h(LAST)
         squares(LAST)
         normalise(LAST - 1)
         transpose_hn(LAST - 1)
         interleave_hn(LAST - 1)
         inverse_deviation(LAST)
-        fill_slots(LAST - 2, range(1, 4), True)
+        add_b2(LAST - 2)
+        fill_slots(LAST - 2, range(4), True)
         store_slots(LAST - 2, 0, T // 2)
         centre(LAST)
         quantise_hn(LAST - 1)

@@ -12,18 +12,22 @@ FLOPS = 2 * B * D * F + 2 * B * F * D
 P = 128
 NT = B // P
 LAST = NT - 1
-WHOLE = (0, LAST)
+WHOLE = (0, 6)
 HALF = F // 2
 QUARTERS = 4
 BLOCKS = 4
 
-PAIRED_QUARTERS = 32
+WIDE_QUARTERS = 1
 
-QUARTERS_PER_LOAD = (1, 1, 1, 2, 2, 2, 2, 4)
+QUARTERS_PER_LOAD = (1, 1, 1, 1, 2, 2, 2, 2)
 
-BIG_BUFFERS = NT + 2
+BIG_BUFFERS = 9
+
+FIRST_LOADS = 5
 
 VECTOR_SLOTS = 3
+
+PREDICTIONS = 4
 
 FIRST_SPLIT_STORE = NT - 4
 
@@ -39,7 +43,14 @@ X = mybir.AxisListType.X
 
 
 def rows_per_partition(i, quarter):
-    return 2 if QUARTERS * i + quarter < PAIRED_QUARTERS else 1
+    earlier = QUARTERS * len([k for k in range(i) if k not in WHOLE]) + quarter
+    return 4 if earlier < WIDE_QUARTERS else 2
+
+
+def slots_per_store(i):
+    if i == LAST:
+        return T // 2
+    return T // 2 if i >= FIRST_SPLIT_STORE else T
 
 
 def hidden_block(g, u):
@@ -54,70 +65,75 @@ def tile_simplepredictor_t_kernel(
     assert num_targets == T
     with ExitStack() as es:
         keep = es.enter_context(tc.tile_pool(name="keep", bufs=1))
-        big = es.enter_context(tc.tile_pool(name="big", bufs=BIG_BUFFERS))
+        big = es.enter_context(tc.tile_pool(name="big", bufs=1))
         work = es.enter_context(tc.tile_pool(name="work", bufs=2))
         psum = es.enter_context(tc.psum_pool(name="psum", bufs=2))
 
         es.enter_context(tc.manual_schedule())
 
-        def load_vector(queue, vec, per, name):
-            cols = keep.tile([P, per], BF16, name=name)
-            queue.dma_start(out=cols[:], in_=vec.rearrange("(p i) -> p i", i=per))
-            return cols
+        free = list(range(BIG_BUFFERS))
+        held = {}
 
-        def big_tile(shape, dtype, name):
-            return big.tile(shape, dtype, tag="big", align_bytes=64, name=name)
+        def big_tile(width, dtype, name, key):
+            held[key] = free[0]
+            free.remove(held[key])
+            return big.tile([P, width], dtype, tag="big%d" % held[key], align_bytes=64, name=name)
+
+        def give_back(key):
+            free.append(held[key])
 
         cmask = keep.tile([P, 8, L], BF16)
         nc.scalar.dma_start(out=cmask[:], in_=context_mask.rearrange("(p i) l -> p i l", i=8))
-        w1_stage = big_tile([P, 2, 4 * F], BF16, "w1_stage")
-        w1_rows = w1_stage[:, 0].rearrange("p (t c) -> p t c", t=4)
-        nc.sync.dma_start(out=w1_rows, in_=W1.rearrange("(p t) c -> p t c", t=4))
-        b1_cols = load_vector(nc.scalar, b1, 8, "b1_cols")
+        vectors = keep.tile([P, HALF], F32)
+        nc.vector.memset(vectors[:], 0.0)
+        w2_bytes = keep.tile([P, 2, 4, D], U8)
+        nc.sync.dma_start(
+            out=w2_bytes[:].rearrange("p g t n -> p g (t n)"), in_=W2_bytes.rearrange("(g p t) n -> p g (t n)", g=2, t=4)
+        )
+        nc.sync.dma_start(out=vectors[0:2, :], in_=W2_scale.rearrange("(g k) o -> g (k o)", g=2))
+        for row, vec in enumerate((b1, gamma, beta, b2), 2):
+            nc.sync.dma_start(
+                out=vectors[row : row + 1, :].bitcast(BF16)[:, : vec.shape[0]], in_=vec.rearrange("(o f) -> o f", o=1)
+            )
 
         rows = context_repr.rearrange("b l d -> (b l) d")
         ctx = {}
 
-        def load_rows(i):
+        def quarters(i, q, n):
+            return ctx[i][:, 4 * D * q : 4 * D * (q + n)]
+
+        def load_rows(i, first=0, end=QUARTERS):
+            if first == 0:
+                ctx[i] = big_tile(L * D, BF16, "ctx", ("ctx", i))
             if i in WHOLE:
-                ctx[i] = big_tile([P, QUARTERS, 4 * D], BF16, "ctx")
-                src = context_repr[P * i : P * i + P].rearrange("b (q l) d -> b q (l d)", q=QUARTERS)
-                for q in range(0, QUARTERS, QUARTERS_PER_LOAD[i]):
-                    part = slice(q, q + QUARTERS_PER_LOAD[i])
-                    nc.sync.dma_start(
-                        out=ctx[i][:, part].rearrange("b q x -> b (q x)"), in_=src[:, part].rearrange("b q x -> b (q x)")
-                    )
+                src = context_repr[P * i : P * i + P].rearrange("b l d -> b (l d)")
+                n = QUARTERS_PER_LOAD[i]
+                for q in range(first, end, n):
+                    nc.sync.dma_start(out=quarters(i, q, n), in_=src[:, 4 * D * q : 4 * D * (q + n)])
                 return
-            ctx[i] = big_tile([P, QUARTERS, BLOCKS, D], BF16, "ctx")
-            q = 0
-            while q < QUARTERS:
+            q = first
+            while q < end:
                 r = rows_per_partition(i, q)
                 n = 1
-                while n < QUARTERS_PER_LOAD[i] and q + n < QUARTERS and rows_per_partition(i, q + n) == r:
+                while n < QUARTERS_PER_LOAD[i] and q + n < end and rows_per_partition(i, q + n) == r:
                     n += 1
                 row0 = 512 * (QUARTERS * i + q)
                 nc.sync.dma_start(
-                    out=ctx[i][:, q : q + n].rearrange("p q (c r) d -> p (q c) (r d)", r=r),
+                    out=quarters(i, q, n).rearrange("p (c x) -> p c x", x=r * D),
                     in_=rows[row0 : row0 + 512 * n, :].rearrange("(c p r) d -> p c (r d)", p=P, r=r),
                 )
                 q += n
 
         load_rows(0)
-        w2_bytes = keep.tile([P, 2, 4, D], U8)
-        nc.sync.dma_start(
-            out=w2_bytes[:].rearrange("p g t n -> p g (t n)"), in_=W2_bytes.rearrange("(g p t) n -> p g (t n)", g=2, t=4)
-        )
-        w2_scale = keep.tile([P, 2, 4], F32)
-        nc.sync.dma_start(out=w2_scale[:], in_=W2_scale.rearrange("(g p t) o -> p g (t o)", g=2, t=4))
-        gamma_cols = load_vector(nc.sync, gamma, 8, "gamma_cols")
-        beta_cols = load_vector(nc.sync, beta, 8, "beta_cols")
+        w1_stage = big_tile(8 * F, BF16, "w1_stage", "w1")
+        w1_rows = w1_stage[:, : 4 * F].rearrange("p (t c) -> p t c", t=4)
+        nc.sync.dma_start(out=w1_rows, in_=W1.rearrange("(p t) c -> p t c", t=4))
         load_rows(1)
-        b2_cols = load_vector(nc.sync, b2, 4, "b2_cols")
         tmask = keep.tile([P, 8, L], BF16)
         nc.sync.dma_start(out=tmask[:], in_=target_mask.rearrange("(p i) l -> p i l", i=8))
-        w2_stage = big_tile([P, 2, 8 * D], BF16, "w2_stage")
-        for i in range(2, NT):
+        for i in range(2, FIRST_LOADS):
             load_rows(i)
+        w2_stage = big_tile(16 * D, BF16, "w2_stage", "w2")
 
         ident_f32 = keep.tile([P, P], F32)
         make_identity(nc, ident_f32[:])
@@ -128,18 +144,19 @@ def tile_simplepredictor_t_kernel(
             slot_index[:], pattern=[[1, T]], base=0, channel_multiplier=0, allow_small_or_imprecise_dtypes=True
         )
         table_in = keep.tile([P, 1], F32)
-        nc.gpsimd.memset(table_in[:], 0.0)
+        nc.vector.memset(table_in[:], 0.0)
         table_out = keep.tile([P, 1], F32)
         nc.scalar.activation(out=table_out[:], in_=table_in[:], func=ACT.Gelu)
 
-        sel2_f32 = keep.tile([P, 16], F32)
-        sel2 = keep.tile([P, 16], BF16)
-        nc.vector.tensor_reduce(out=sel2_f32[:], in_=ident_f32[:].rearrange("p (j q) -> p j q", q=8), axis=X, op=ALU.add)
-        nc.vector.tensor_copy(out=sel2[:], in_=sel2_f32[:])
-        sel1_f32 = keep.tile([P, 8], F32)
-        sel1 = keep.tile([P, 8], BF16)
-        nc.vector.tensor_reduce(out=sel1_f32[:], in_=ident_f32[:].rearrange("p (j q) -> p j q", q=16), axis=X, op=ALU.add)
-        pooling = {1: sel1, 2: sel2}
+        def selection(r):
+            wide = keep.tile([P, 8 * r], F32, name="selection%d_f32" % r)
+            sel = keep.tile([P, 8 * r], BF16, name="selection%d" % r)
+            nc.vector.tensor_reduce(
+                out=wide[:], in_=ident_f32[:].rearrange("p (j q) -> p j q", q=L // r), axis=X, op=ALU.add
+            )
+            return wide, sel
+
+        pooling = {r: selection(r) for r in (1, 2, 4)}
         mod16 = keep.tile([P, 16], F32)
         nc.vector.tensor_reduce(out=mod16[:], in_=ident_f32[:].rearrange("p (j q) -> p q j", q=16), axis=X, op=ALU.add)
 
@@ -159,24 +176,31 @@ def tile_simplepredictor_t_kernel(
                 in_=turned[:].rearrange("p i n -> p n i"),
             )
 
-        def turn_vector(cols, per):
-            turned = psum.tile([P, per, P], F32, tag="h", bufs=4, name="turned")
-            words = cols[:].bitcast(F32)
-            for i in range(per):
-                nc.tensor.transpose(turned[:, i, :], words[:, i : i + 1].to_broadcast([P, P]), ident_f32[:])
+        columns = keep.tile([P, 6, 4], F32)
+
+        def turn_rows():
+            turned = psum.tile([P, 4, P], F32, tag="h", bufs=4, name="turned")
+            for t in range(4):
+                nc.tensor.transpose(turned[:, t, :], vectors[:, t::4], ident_f32[:])
+            nc.scalar.copy(out=columns[:], in_=turned[:, :, :6].rearrange("p t row -> p row t"))
+
+        def turn_vector(row):
+            turned = psum.tile([P, 4, P], F32, tag="h", bufs=4, name="turned")
+            for t in range(4):
+                nc.tensor.transpose(turned[:, t, :], columns[:, row, t : t + 1].to_broadcast([P, P]), ident_f32[:])
             return turned
 
-        def spread_hidden(cols, name):
+        def spread_hidden(turned, name):
             dst = keep.tile([P, F], BF16, name=name)
             nc.scalar.copy(
                 out=dst[:].bitcast(F32).rearrange("p (g u n v) -> p g u n v", g=2, u=2, v=2),
-                in_=turn_vector(cols, 4)[:].rearrange("p (v u) (g n) -> p g u n v", u=2, g=2),
+                in_=turned[:].rearrange("p (v u) (g n) -> p g u n v", u=2, g=2),
             )
             return dst
 
         w1_codes = keep.tile([P, F], U32, align_bytes=64)
         w1_planes = keep.tile([P, F], U8, align_bytes=64)
-        w1_words = [w1_stage[:, 1, 4 * HALF * g : 4 * HALF * (g + 1)].rearrange("p (c t) -> p c t", t=4) for g in range(2)]
+        w1_words = [w1_stage[:, 4 * HALF * (2 + g) : 4 * HALF * (3 + g)].rearrange("p (c t) -> p c t", t=4) for g in range(2)]
 
         def interleave_w1(g):
             copy = (nc.vector.tensor_copy, nc.scalar.copy)[g]
@@ -192,22 +216,22 @@ def tile_simplepredictor_t_kernel(
                 in_=w1_words[g].rearrange("p c t -> p (c t)"),
             )
 
-        w2_rows = w2_stage[:, 0].rearrange("p (g t n) -> p g t n", g=2, t=4)
-        w2_words = [w2_stage[:, 1, 4 * D * g : 4 * D * (g + 1)].rearrange("p (n t) -> p n t", t=4) for g in range(2)]
+        w2_rows = w2_stage[:, : 8 * D].rearrange("p (g t n) -> p g t n", g=2, t=4)
+        w2_words = [w2_stage[:, 4 * D * (2 + g) : 4 * D * (3 + g)].rearrange("p (n t) -> p n t", t=4) for g in range(2)]
         w2_codes = keep.tile([P, 2, D], U32, align_bytes=64)
         w2_planes = keep.tile([P, 2, D], U8, align_bytes=64)
 
         def widen_w2(g, positions):
             for t in positions:
-                dst, src, scale = w2_rows[:, g, t, :], w2_bytes[:, g, t, :].bitcast(FP8), w2_scale[:, g, t : t + 1]
-                if g == 0:
-                    nc.vector.tensor_scalar(out=dst, in0=src, scalar1=scale, scalar2=None, op0=ALU.mult)
-                else:
-                    nc.scalar.activation(out=dst, in_=src, func=ACT.Copy, scale=scale)
+                nc.scalar.activation(
+                    out=w2_rows[:, g, t, :],
+                    in_=w2_bytes[:, g, t, :].bitcast(FP8),
+                    func=ACT.Copy,
+                    scale=columns[:, g, t : t + 1],
+                )
 
         def interleave_w2(g):
-            copy = (nc.vector.tensor_copy, nc.scalar.copy)[g]
-            copy(out=w2_words[g], in_=w2_rows[:, g].rearrange("p t n -> p n t"))
+            nc.vector.tensor_copy(out=w2_words[g], in_=w2_rows[:, g].rearrange("p t n -> p n t"))
 
         def quantise_w2(g):
             nc.vector.quantize_mx(
@@ -217,13 +241,14 @@ def tile_simplepredictor_t_kernel(
             )
 
         st = {}
+        pooled = [QUARTERS, 2] + [0] * (NT - 2)
 
         def pool(i, q):
             if q == 0:
                 st["sums", i] = psum.tile([P, 4, P], F32, tag="pool", name="sums")
             r = rows_per_partition(i, q)
             width = 8 * r
-            x = ctx[i][:, q].rearrange("p (c r) d -> p c (r d)", r=r)
+            x = quarters(i, q, 1).rearrange("p (c x) -> p c x", x=r * D)
             for c in range(BLOCKS // r):
                 b0 = 32 * q + width * c
                 for t in range(4):
@@ -231,32 +256,41 @@ def tile_simplepredictor_t_kernel(
                         nc.tensor.matmul(
                             out=st["sums", i][:, t, b0 : b0 + width],
                             lhsT=x[:, c, D * e + t : D * e + D : 4],
-                            rhs=pooling[r][:],
+                            rhs=pooling[r][1][:],
                             start=(e == 0),
                             stop=(e == r - 1),
                         )
+            if q == QUARTERS - 1:
+                give_back(("ctx", i))
 
         def add_pairs(i, q):
             if q == 0:
-                st["pairs", i] = big_tile([P, 4, QUARTERS, 2 * P], F32, "pairs")
-            x = ctx[i][:, q].rearrange("b (h c n t) -> b h c t n", h=2, n=4, t=4)
+                st["pairs", i] = big_tile(QUARTERS * F, F32, "pairs", ("pairs", i))
+            x = quarters(i, q, 1).rearrange("b (h c n t) -> b h c t n", h=2, n=4, t=4)
             nc.vector.tensor_tensor(
-                out=st["pairs", i][:, :, q].rearrange("b t (c n) -> b c t n", n=4), in0=x[:, 0], in1=x[:, 1], op=ALU.add
+                out=st["pairs", i][:, F * q : F * q + F].rearrange("b (t c n) -> b c t n", t=4, n=4),
+                in0=x[:, 0],
+                in1=x[:, 1],
+                op=ALU.add,
             )
+            if q == QUARTERS - 1:
+                give_back(("ctx", i))
 
         def pool_pairs(i, t):
             if t == 0:
                 st["sums", i] = psum.tile([P, 4, P], F32, tag="pool", name="sums")
-            words = st["pairs", i][:, t].rearrange("b q (j p) -> b (q j) p", p=P)
             for j in range(L // 2):
+                w0 = F * (j // 2) + 2 * P * t + P * (j % 2)
                 nc.tensor.matmul(
                     out=st["sums", i][:, t, :],
-                    lhsT=words[:, j],
+                    lhsT=st["pairs", i][:, w0 : w0 + P],
                     rhs=ident_f32[:],
                     is_transpose=True,
                     start=(j == 0),
                     stop=(j == L // 2 - 1),
                 )
+            if t == 3:
+                give_back(("pairs", i))
 
         def scale_mean(i):
             mean = work.tile([P, P, 4], BF16, align_bytes=64, tag="mean", name="mean")
@@ -276,8 +310,8 @@ def tile_simplepredictor_t_kernel(
             )
             st["mean_codes", i], st["mean_plane", i] = codes, plane
 
-        def multiply_w1(i):
-            for g in range(2):
+        def multiply_w1(i, halves=(0, 1)):
+            for g in halves:
                 cols = slice(HALF * g, HALF * g + HALF)
                 acc = psum.tile([P, HALF], F32, tag="h", bufs=4, name="acc")
                 nc.tensor.matmul_mx(
@@ -388,52 +422,73 @@ def tile_simplepredictor_t_kernel(
             st["acc2", i] = acc
 
         def add_b2(i):
-            prediction = work.tile([P, D], F32, tag="prediction", name="prediction")
+            prediction = work.tile([P, D], F32, tag="prediction", bufs=PREDICTIONS, name="prediction")
             nc.vector.tensor_tensor(out=prediction[:], in0=st["acc2", i][:], in1=b2_all[:], op=ALU.add)
             st["prediction", i] = prediction
+            waiting.extend((i, j) for j in range(T))
 
-        def fill_slots(i, slots, on_vector):
-            if ("slots", i) not in st:
-                st["slots", i] = big_tile([P, T, D], F32, "slots")
-            for j in slots:
+        waiting = []
+
+        def fill_slots(count, on_vector):
+            for i, j in waiting[:count]:
+                waiting.remove((i, j))
+                if j == 0:
+                    st["slots", i] = big_tile(T * D, F32, "slots", ("slots", i))
                 mask = valid[:, i, j : j + 1]
-                dst = st["slots", i][:, j, :]
+                dst = st["slots", i][:, D * j : D * j + D]
                 if on_vector:
                     nc.vector.tensor_scalar_mul(dst, st["prediction", i][:], mask)
                 else:
                     nc.scalar.activation(out=dst, in_=st["prediction", i][:], func=ACT.Copy, scale=mask)
-
-        def store_slots(i, first, end):
-            nc.sync.dma_start(out=out[P * i : P * i + P, first:end, :], in_=st["slots", i][:, first:end, :])
+                part = slots_per_store(i)
+                if (j + 1) % part == 0:
+                    nc.sync.dma_start(
+                        out=out[P * i : P * i + P, j + 1 - part : j + 1, :].rearrange("b j d -> b (j d)"),
+                        in_=st["slots", i][:, D * (j + 1 - part) : D * (j + 1)],
+                    )
 
         nc.vector.tensor_reduce(out=count[:], in_=cmask[:], axis=X, op=ALU.add)
+        nc.vector.tensor_copy(out=pooling[2][1][:], in_=pooling[2][0][:])
         nc.vector.tensor_scalar_max(count_or_1[:], count[:], 1.0)
+        nc.vector.tensor_copy(out=pooling[4][1][:], in_=pooling[4][0][:])
         nc.vector.reciprocal(reciprocal[:], count_or_1[:])
+        nc.vector.tensor_copy(out=pooling[1][1][:], in_=pooling[1][0][:])
         nc.vector.scalar_tensor_tensor(
             out=factor[:], in0=count[:], scalar=0.0, in1=reciprocal[:], op0=ALU.is_gt, op1=ALU.mult
         )
-        interleave_w1(0)
-        interleave_w1(1)
         spread_factor(0)
         spread_factor(1)
-        b1_all = spread_hidden(b1_cols, "b1_all")
-        add_pairs(0, 0)
-        add_pairs(0, 1)
-        add_pairs(0, 2)
-        add_pairs(0, 3)
+        turn_rows()
+        widen_w2(0, range(4))
+        b1_all = spread_hidden(turn_vector(2), "b1_all")
+        gamma_turned = turn_vector(3)
+        beta_turned = turn_vector(4)
+        widen_w2(1, range(2))
+        for q in range(QUARTERS):
+            add_pairs(0, q)
         for t in range(4):
             pool_pairs(0, t)
-        nc.vector.tensor_copy(out=sel1[:], in_=sel1_f32[:])
-        quantise_w1(0)
-        quantise_w1(1)
-        widen_w2(1, (0, 1, 2, 3))
-        widen_w2(0, (0, 1, 2, 3))
+        interleave_w2(0)
+        interleave_w1(0)
+        interleave_w1(1)
+        widen_w2(1, range(2, 4))
+        gamma_all = spread_hidden(gamma_turned, "gamma_all")
+        beta_all = spread_hidden(beta_turned, "beta_all")
         scale_mean(0)
-        pool(1, 0)
+        quantise_w1(0)
         quantise_mean(0)
-        multiply_w1(0)
+        pool(1, 0)
         pool(1, 1)
-        pool(1, 2)
+        multiply_w1(0, (0,))
+        quantise_w1(1)
+        give_back("w1")
+        multiply_w1(0, (1,))
+        load_rows(5, 0, 2)
+        load_rows(6, 0, 2)
+        load_rows(5, 2, 4)
+        load_rows(6, 2, 4)
+        load_rows(7)
+        quantise_w2(0)
 
         target_n = keep.tile([P, 8], F32)
         picked = keep.tile([P, 16, 8], BF16)
@@ -449,15 +504,15 @@ def tile_simplepredictor_t_kernel(
             )
             n_psum = psum.tile([P, NT], F32, tag="out", bufs=1, name="n_psum")
             nc.tensor.matmul(
-                out=n_psum[:], lhsT=picked[:].rearrange("p q i -> p (q i)"), rhs=sel1[:], start=True, stop=True
+                out=n_psum[:], lhsT=picked[:].rearrange("p q i -> p (q i)"), rhs=pooling[1][1][:], start=True, stop=True
             )
             st["n_psum"] = n_psum
 
-        def spread_b2():
+        def spread_b2(turned):
             dst = keep.tile([P, D], BF16, name="b2_all")
             nc.scalar.copy(
-                out=dst[:].bitcast(F32).rearrange("p (n i) -> p n i", i=2),
-                in_=turn_vector(b2_cols, 2)[:].rearrange("p i n -> p n i"),
+                out=dst[:].bitcast(F32).rearrange("p (n t) -> p n t", t=4),
+                in_=turned[:, :, : P // 2].rearrange("p t n -> p n t"),
             )
             return dst
 
@@ -465,59 +520,58 @@ def tile_simplepredictor_t_kernel(
             if 0 <= i < NT:
                 stage(i, *args)
 
+
+        def pool_until(i, last):
+            while i < NT and pooled[i] <= last:
+                (pool_pairs if i in WHOLE else pool)(i, pooled[i])
+                pooled[i] += 1
+
         for s in range(LAST):
-            whole = s + 2 in WHOLE
-            plain = s + 2 < NT and not whole
-            when(s - 3, fill_slots, range(5, 7), False)
+            pairs = [(w, q) for w in WHOLE for q in range(QUARTERS) if w > 0 and s == w - 2 - (q < 2)]
+            spare = 0 if pairs or s + 1 in WHOLE else VECTOR_SLOTS
+            fill_slots(2, False)
             when(s, add_b1)
-            if s + 1 not in WHOLE:
-                pool(s + 1, 3)
-            if whole:
-                add_pairs(s + 2, 0)
+            pool_until(s + 1, 3)
             when(s, gelu)
-            when(s - 3, fill_slots, range(7, 8), False)
-            when(s - 3, store_slots, T // 2 if s - 3 >= FIRST_SPLIT_STORE else 0, T)
+            fill_slots(1, False)
             if s == 0:
-                gamma_all = spread_hidden(gamma_cols, "gamma_all")
-                interleave_w2(0)
-            if s == 1:
-                b2_all = spread_b2()
+                interleave_w2(1)
             when(s, mean_of_h)
             when(s - 1, normalise)
             when(s - 1, transpose_hn)
             when(s - 1, interleave_hn)
             when(s, squares)
-            if plain:
-                pool(s + 2, 0)
-            when(s - 2, add_b2)
-            if whole:
-                add_pairs(s + 2, 1)
-            when(s + 1, scale_mean)
-            if whole:
-                add_pairs(s + 2, 2)
-            when(s - 2, fill_slots, range(1), not whole)
             if s == 0:
-                quantise_w2(0)
-                beta_all = spread_hidden(beta_cols, "beta_all")
+                nc.vector.tensor_reduce(out=target_n[:], in_=tmask[:], axis=X, op=ALU.add)
+            if s + 2 in WHOLE:
+                pool_until(s + 3, 1)
+            else:
+                pool_until(s + 2, 2 if s + 1 in WHOLE else 1)
+            if s == 0:
+                b2_turned = turn_vector(5)
+            when(s - 2, add_b2)
+            if s + 1 in WHOLE:
+                fill_slots(VECTOR_SLOTS, True)
+            when(s + 1, scale_mean)
+            fill_slots(min(spare, 1), True)
+            if pairs:
+                add_pairs(*pairs[0])
+            if s == 0:
+                quantise_w2(1)
+                give_back("w2")
             if s == 1:
                 nc.vector.tensor_copy(out=n_of_row[:], in_=st["n_psum"][:])
             when(s + 1, quantise_mean)
-            if whole:
-                add_pairs(s + 2, 3)
-            if plain:
-                pool(s + 2, 1)
             when(s + 1, multiply_w1)
-            if plain:
-                pool(s + 2, 2)
-            if whole:
-                pool_pairs(s + 2, 0)
-                pool_pairs(s + 2, 1)
+            if s + 2 in WHOLE:
+                add_pairs(*pairs[1])
+                pool_until(s + 2, 1)
+            else:
+                pool_until(s + 2, 3 if s + 1 in WHOLE else 2)
             when(s, centre)
             if s == 0:
-                nc.vector.tensor_reduce(out=target_n[:], in_=tmask[:], axis=X, op=ALU.add)
                 count_targets()
             if s == 1:
-                quantise_w2(1)
                 nc.vector.tensor_tensor(
                     out=valid[:],
                     in0=slot_index[:].unsqueeze(1).to_broadcast([P, NT, T]),
@@ -526,56 +580,42 @@ def tile_simplepredictor_t_kernel(
                 )
             when(s - 1, quantise_hn)
             when(s - 1, multiply_w2)
-            if whole:
-                pool_pairs(s + 2, 2)
-                pool_pairs(s + 2, 3)
-            when(s - 2, fill_slots, range(1, 3), not whole)
-            when(s - 2, fill_slots, range(3, 4), False)
-            if s - 2 >= FIRST_SPLIT_STORE:
-                store_slots(s - 2, 0, T // 2)
+            if s + 3 in WHOLE:
+                add_pairs(*pairs[1])
+            fill_slots(1, False)
             when(s, inverse_deviation)
-            when(s - 2, fill_slots, range(4, 5), False)
             if s == 0:
-                interleave_w2(1)
+                b2_all = spread_b2(b2_turned)
+            fill_slots(max(spare - 1, 0), True)
+            fill_slots(5 if pairs else 2, False)
 
-        fill_slots(LAST - 3, range(5, 7), False)
+        fill_slots(1, False)
         add_b1(LAST)
         gelu(LAST)
-        fill_slots(LAST - 3, range(7, 8), False)
-        store_slots(LAST - 3, T // 2, T)
-        mean_of_h(LAST)
-        squares(LAST)
         normalise(LAST - 1)
         transpose_hn(LAST - 1)
+        fill_slots(1, False)
+        mean_of_h(LAST)
+        squares(LAST)
+        add_b2(LAST - 2)
+        fill_slots(3, True)
+        centre(LAST)
         interleave_hn(LAST - 1)
         inverse_deviation(LAST)
-        add_b2(LAST - 2)
-        fill_slots(LAST - 2, range(4), True)
-        store_slots(LAST - 2, 0, T // 2)
-        centre(LAST)
+        fill_slots(1, True)
         quantise_hn(LAST - 1)
         multiply_w2(LAST - 1)
-        fill_slots(LAST - 2, range(4, 5), True)
-        fill_slots(LAST - 2, range(5, 8), False)
-        store_slots(LAST - 2, T // 2, T)
+        fill_slots(4, False)
         normalise(LAST)
         transpose_hn(LAST)
-        interleave_hn(LAST)
         add_b2(LAST - 1)
-        fill_slots(LAST - 1, range(3), True)
-        fill_slots(LAST - 1, range(3, 4), False)
-        store_slots(LAST - 1, 0, T // 2)
+        interleave_hn(LAST)
+        fill_slots(4, True)
         quantise_hn(LAST)
         multiply_w2(LAST)
-        fill_slots(LAST - 1, range(4, 6), True)
-        fill_slots(LAST - 1, range(6, 8), False)
-        store_slots(LAST - 1, T // 2, T)
+        fill_slots(2, False)
+        fill_slots(4, True)
         add_b2(LAST)
-        fill_slots(LAST, range(0, 2), True)
-        fill_slots(LAST, range(2, 3), False)
-        store_slots(LAST, 0, 3)
-        fill_slots(LAST, range(3, 5), True)
-        fill_slots(LAST, range(5, 6), False)
-        store_slots(LAST, 3, 6)
-        fill_slots(LAST, range(6, 8), True)
-        store_slots(LAST, 6, 8)
+        while waiting:
+            fill_slots(2, True)
+            fill_slots(1, False)

@@ -12,12 +12,12 @@ FLOPS = 2 * B * D * F + 2 * B * F * D
 P = 128
 NT = B // P
 LAST = NT - 1
-WHOLE = (0, 6)
+WHOLE = (0, 4, 7)
 HALF = F // 2
 QUARTERS = 4
 BLOCKS = 4
 
-WIDE_QUARTERS = 1
+WIDE_QUARTERS = 5
 
 QUARTERS_PER_LOAD = (1, 1, 1, 1, 2, 2, 2, 2)
 
@@ -25,11 +25,7 @@ BIG_BUFFERS = 9
 
 FIRST_LOADS = 5
 
-VECTOR_SLOTS = 3
-
-PREDICTIONS = 4
-
-FIRST_SPLIT_STORE = NT - 4
+FIRST_SPLIT_STORE = NT - 5
 
 F32 = mybir.dt.float32
 BF16 = mybir.dt.bfloat16
@@ -131,8 +127,10 @@ def tile_simplepredictor_t_kernel(
         load_rows(1)
         tmask = keep.tile([P, 8, L], BF16)
         nc.sync.dma_start(out=tmask[:], in_=target_mask.rearrange("(p i) l -> p i l", i=8))
-        for i in range(2, FIRST_LOADS):
-            load_rows(i)
+        load_rows(2)
+        load_rows(4, 0, 2)
+        load_rows(3)
+        load_rows(4, 2, 4)
         w2_stage = big_tile(16 * D, BF16, "w2_stage", "w2")
 
         ident_f32 = keep.tile([P, P], F32)
@@ -167,7 +165,7 @@ def tile_simplepredictor_t_kernel(
         factor_all = keep.tile([P, B], F32)
 
         def spread_factor(k):
-            turned = psum.tile([P, 4, P], F32, tag="h", bufs=4, name="turned")
+            turned = psum.tile([P, 4, P], F32, tag="h", bufs=3, name="turned")
             for i in range(4):
                 column = factor[:, 4 * k + i : 4 * k + i + 1]
                 nc.tensor.transpose(turned[:, i, :], column.to_broadcast([P, P]), ident_f32[:])
@@ -179,13 +177,13 @@ def tile_simplepredictor_t_kernel(
         columns = keep.tile([P, 6, 4], F32)
 
         def turn_rows():
-            turned = psum.tile([P, 4, P], F32, tag="h", bufs=4, name="turned")
+            turned = psum.tile([P, 4, P], F32, tag="h", bufs=3, name="turned")
             for t in range(4):
                 nc.tensor.transpose(turned[:, t, :], vectors[:, t::4], ident_f32[:])
             nc.scalar.copy(out=columns[:], in_=turned[:, :, :6].rearrange("p t row -> p row t"))
 
-        def turn_vector(row):
-            turned = psum.tile([P, 4, P], F32, tag="h", bufs=4, name="turned")
+        def turn_vector(row, tag="h", bufs=3):
+            turned = psum.tile([P, 4, P], F32, tag=tag, bufs=bufs, name="turned")
             for t in range(4):
                 nc.tensor.transpose(turned[:, t, :], columns[:, row, t : t + 1].to_broadcast([P, P]), ident_f32[:])
             return turned
@@ -230,8 +228,8 @@ def tile_simplepredictor_t_kernel(
                     scale=columns[:, g, t : t + 1],
                 )
 
-        def interleave_w2(g):
-            nc.vector.tensor_copy(out=w2_words[g], in_=w2_rows[:, g].rearrange("p t n -> p n t"))
+        def interleave_w2(g, cols, copy):
+            copy(out=w2_words[g][:, cols], in_=w2_rows[:, g, :, cols].rearrange("p t n -> p n t"))
 
         def quantise_w2(g):
             nc.vector.quantize_mx(
@@ -245,7 +243,7 @@ def tile_simplepredictor_t_kernel(
 
         def pool(i, q):
             if q == 0:
-                st["sums", i] = psum.tile([P, 4, P], F32, tag="pool", name="sums")
+                st["sums", i] = psum.tile([P, 4, P], F32, tag="pool", bufs=3, name="sums")
             r = rows_per_partition(i, q)
             width = 8 * r
             x = quarters(i, q, 1).rearrange("p (c x) -> p c x", x=r * D)
@@ -276,20 +274,21 @@ def tile_simplepredictor_t_kernel(
             if q == QUARTERS - 1:
                 give_back(("ctx", i))
 
-        def pool_pairs(i, t):
-            if t == 0:
-                st["sums", i] = psum.tile([P, 4, P], F32, tag="pool", name="sums")
-            for j in range(L // 2):
-                w0 = F * (j // 2) + 2 * P * t + P * (j % 2)
-                nc.tensor.matmul(
-                    out=st["sums", i][:, t, :],
-                    lhsT=st["pairs", i][:, w0 : w0 + P],
-                    rhs=ident_f32[:],
-                    is_transpose=True,
-                    start=(j == 0),
-                    stop=(j == L // 2 - 1),
-                )
-            if t == 3:
+        def pool_pairs(i, q):
+            if q == 0:
+                st["sums", i] = psum.tile([P, 4, P], F32, tag="pool", bufs=3, name="sums")
+            for t in range(4):
+                for j in range(2):
+                    w0 = F * q + 2 * P * t + P * j
+                    nc.tensor.matmul(
+                        out=st["sums", i][:, t, :],
+                        lhsT=st["pairs", i][:, w0 : w0 + P],
+                        rhs=ident_f32[:],
+                        is_transpose=True,
+                        start=(q, t, j) == (0, 0, 0),
+                        stop=(q, t, j) == (QUARTERS - 1, 3, 1),
+                    )
+            if q == QUARTERS - 1:
                 give_back(("pairs", i))
 
         def scale_mean(i):
@@ -313,7 +312,7 @@ def tile_simplepredictor_t_kernel(
         def multiply_w1(i, halves=(0, 1)):
             for g in halves:
                 cols = slice(HALF * g, HALF * g + HALF)
-                acc = psum.tile([P, HALF], F32, tag="h", bufs=4, name="acc")
+                acc = psum.tile([P, HALF], F32, tag="h", bufs=3, name="acc")
                 nc.tensor.matmul_mx(
                     out=acc[:],
                     lhsT=st["mean_codes", i][:].bitcast(FP8X4),
@@ -421,25 +420,37 @@ def tile_simplepredictor_t_kernel(
                 )
             st["acc2", i] = acc
 
+        def mask_b2(i, on_vector=True):
+            masked = work.tile([P, D], BF16, tag="b2_masked", name="b2_masked")
+            if on_vector:
+                nc.vector.tensor_scalar_mul(masked[:], b2_all[:], valid[:, i, 0:1])
+            else:
+                nc.scalar.activation(out=masked[:], in_=b2_all[:], func=ACT.Copy, scale=valid[:, i, 0:1])
+            st["b2_masked", i] = masked
+
         def add_b2(i):
-            prediction = work.tile([P, D], F32, tag="prediction", bufs=PREDICTIONS, name="prediction")
-            nc.vector.tensor_tensor(out=prediction[:], in0=st["acc2", i][:], in1=b2_all[:], op=ALU.add)
-            st["prediction", i] = prediction
-            waiting.extend((i, j) for j in range(T))
+            st["slots", i] = big_tile(T * D, F32, "slots", ("slots", i))
+            nc.vector.scalar_tensor_tensor(
+                out=st["slots", i][:, :D],
+                in0=st["acc2", i][:],
+                scalar=valid[:, i, 0:1],
+                in1=st["b2_masked", i][:],
+                op0=ALU.mult,
+                op1=ALU.add,
+            )
+            waiting.extend((i, j) for j in range(1, T))
 
         waiting = []
 
         def fill_slots(count, on_vector):
             for i, j in waiting[:count]:
                 waiting.remove((i, j))
-                if j == 0:
-                    st["slots", i] = big_tile(T * D, F32, "slots", ("slots", i))
                 mask = valid[:, i, j : j + 1]
                 dst = st["slots", i][:, D * j : D * j + D]
                 if on_vector:
-                    nc.vector.tensor_scalar_mul(dst, st["prediction", i][:], mask)
+                    nc.vector.tensor_scalar_mul(dst, st["slots", i][:, :D], mask)
                 else:
-                    nc.scalar.activation(out=dst, in_=st["prediction", i][:], func=ACT.Copy, scale=mask)
+                    nc.scalar.activation(out=dst, in_=st["slots", i][:, :D], func=ACT.Copy, scale=mask)
                 part = slots_per_store(i)
                 if (j + 1) % part == 0:
                     nc.sync.dma_start(
@@ -461,19 +472,19 @@ def tile_simplepredictor_t_kernel(
         turn_rows()
         widen_w2(0, range(4))
         b1_all = spread_hidden(turn_vector(2), "b1_all")
-        gamma_turned = turn_vector(3)
-        beta_turned = turn_vector(4)
+        gamma_turned = turn_vector(3, "out", 1)
+        beta_turned = turn_vector(4, "turned_hn", 1)
         widen_w2(1, range(2))
         for q in range(QUARTERS):
             add_pairs(0, q)
-        for t in range(4):
-            pool_pairs(0, t)
-        interleave_w2(0)
+            pool_pairs(0, q)
+        interleave_w2(0, slice(0, D), nc.vector.tensor_copy)
         interleave_w1(0)
         interleave_w1(1)
         widen_w2(1, range(2, 4))
         gamma_all = spread_hidden(gamma_turned, "gamma_all")
         beta_all = spread_hidden(beta_turned, "beta_all")
+        interleave_w2(1, slice(0, D // 2), nc.scalar.copy)
         scale_mean(0)
         quantise_w1(0)
         quantise_mean(0)
@@ -483,11 +494,8 @@ def tile_simplepredictor_t_kernel(
         quantise_w1(1)
         give_back("w1")
         multiply_w1(0, (1,))
-        load_rows(5, 0, 2)
-        load_rows(6, 0, 2)
-        load_rows(5, 2, 4)
-        load_rows(6, 2, 4)
-        load_rows(7)
+        for i in range(FIRST_LOADS, NT):
+            load_rows(i)
         quantise_w2(0)
 
         target_n = keep.tile([P, 8], F32)
@@ -527,48 +535,53 @@ def tile_simplepredictor_t_kernel(
                 pooled[i] += 1
 
         for s in range(LAST):
-            pairs = [(w, q) for w in WHOLE for q in range(QUARTERS) if w > 0 and s == w - 2 - (q < 2)]
-            spare = 0 if pairs or s + 1 in WHOLE else VECTOR_SLOTS
-            fill_slots(2, False)
-            when(s, add_b1)
+            first, middle, final = (s + 3 in WHOLE), (s + 2 in WHOLE), (s + 1 in WHOLE)
+            spare = 0 if middle else 1
+            fill_slots(1, False)
+            add_b1(s)
+            if final:
+                add_pairs(s + 1, 3)
             pool_until(s + 1, 3)
-            when(s, gelu)
+            if s == 1:
+                b2_turned = turn_vector(5)
+            gelu(s)
             fill_slots(1, False)
             if s == 0:
-                interleave_w2(1)
-            when(s, mean_of_h)
+                interleave_w2(1, slice(D // 2, D), nc.vector.tensor_copy)
+            mean_of_h(s)
             when(s - 1, normalise)
             when(s - 1, transpose_hn)
+            squares(s)
+            if final:
+                fill_slots(0, False)
             when(s - 1, interleave_hn)
-            when(s, squares)
+            if s == 1:
+                b2_all = spread_b2(b2_turned)
             if s == 0:
                 nc.vector.tensor_reduce(out=target_n[:], in_=tmask[:], axis=X, op=ALU.add)
-            if s + 2 in WHOLE:
-                pool_until(s + 3, 1)
+            if middle:
+                pool_until(s + 2, 0)
+                pool_until(s + 3, -1)
             else:
-                pool_until(s + 2, 2 if s + 1 in WHOLE else 1)
-            if s == 0:
-                b2_turned = turn_vector(5)
+                pool_until(s + 2, 0 if s == 1 else 1)
             when(s - 2, add_b2)
-            if s + 1 in WHOLE:
-                fill_slots(VECTOR_SLOTS, True)
-            when(s + 1, scale_mean)
-            fill_slots(min(spare, 1), True)
-            if pairs:
-                add_pairs(*pairs[0])
+            if middle:
+                add_pairs(s + 2, 1)
+            scale_mean(s + 1)
+            if first:
+                add_pairs(s + 3, 0)
             if s == 0:
                 quantise_w2(1)
                 give_back("w2")
             if s == 1:
                 nc.vector.tensor_copy(out=n_of_row[:], in_=st["n_psum"][:])
-            when(s + 1, quantise_mean)
-            when(s + 1, multiply_w1)
-            if s + 2 in WHOLE:
-                add_pairs(*pairs[1])
-                pool_until(s + 2, 1)
-            else:
-                pool_until(s + 2, 3 if s + 1 in WHOLE else 2)
-            when(s, centre)
+            if s > 2:
+                mask_b2(s - 1)
+            quantise_mean(s + 1)
+            multiply_w1(s + 1)
+            pool_until(s + 2, 1 if middle or s == 1 else 2)
+            fill_slots(min(spare, 1), True)
+            centre(s)
             if s == 0:
                 count_targets()
             if s == 1:
@@ -580,14 +593,17 @@ def tile_simplepredictor_t_kernel(
                 )
             when(s - 1, quantise_hn)
             when(s - 1, multiply_w2)
-            if s + 3 in WHOLE:
-                add_pairs(*pairs[1])
+            if middle:
+                add_pairs(s + 2, 2)
+                pool_until(s + 3, 0)
+                pool_until(s + 2, 2)
             fill_slots(1, False)
-            when(s, inverse_deviation)
-            if s == 0:
-                b2_all = spread_b2(b2_turned)
+            inverse_deviation(s)
+            if s == 1:
+                mask_b2(0, False)
+                mask_b2(1, False)
             fill_slots(max(spare - 1, 0), True)
-            fill_slots(5 if pairs else 2, False)
+            fill_slots(4, False)
 
         fill_slots(1, False)
         add_b1(LAST)
@@ -598,6 +614,7 @@ def tile_simplepredictor_t_kernel(
         mean_of_h(LAST)
         squares(LAST)
         add_b2(LAST - 2)
+        mask_b2(LAST - 1)
         fill_slots(3, True)
         centre(LAST)
         interleave_hn(LAST - 1)
@@ -605,7 +622,8 @@ def tile_simplepredictor_t_kernel(
         fill_slots(1, True)
         quantise_hn(LAST - 1)
         multiply_w2(LAST - 1)
-        fill_slots(4, False)
+        mask_b2(LAST)
+        fill_slots(3, False)
         normalise(LAST)
         transpose_hn(LAST)
         add_b2(LAST - 1)

@@ -13,6 +13,7 @@ P = 128
 NT = B // P
 LAST = NT - 1
 WHOLE = (0, 4, 7)
+WIDENED = (4, 0)
 HALF = F // 2
 QUARTERS = 4
 BLOCKS = 4
@@ -43,10 +44,11 @@ def rows_per_partition(i, quarter):
     return 4 if earlier < WIDE_QUARTERS else 2
 
 
-def slots_per_store(i):
-    if i == LAST:
-        return T // 2
-    return T // 2 if i >= FIRST_SPLIT_STORE else T
+def stores(i):
+    if i < FIRST_SPLIT_STORE:
+        return ((0, T),)
+    cut = 4 if i == LAST else T // 2
+    return ((0, cut), (cut, T))
 
 
 def hidden_block(g, u):
@@ -229,7 +231,10 @@ def tile_simplepredictor_t_kernel(
                 )
 
         def interleave_w2(g, cols, copy):
-            copy(out=w2_words[g][:, cols], in_=w2_rows[:, g, :, cols].rearrange("p t n -> p n t"))
+            copy(
+                out=w2_words[g][:, cols].rearrange("p (c i) t -> p c t i", i=4),
+                in_=w2_rows[:, g, :, cols].rearrange("p t (c i) -> p c t i", i=4),
+            )
 
         def quantise_w2(g):
             nc.vector.quantize_mx(
@@ -243,7 +248,7 @@ def tile_simplepredictor_t_kernel(
 
         def pool(i, q):
             if q == 0:
-                st["sums", i] = psum.tile([P, 4, P], F32, tag="pool", bufs=3, name="sums")
+                st["sums", i] = psum.tile([P, P, 4], F32, tag="pool", bufs=3, name="sums")
             r = rows_per_partition(i, q)
             width = 8 * r
             x = quarters(i, q, 1).rearrange("p (c x) -> p c x", x=r * D)
@@ -252,7 +257,7 @@ def tile_simplepredictor_t_kernel(
                 for t in range(4):
                     for e in range(r):
                         nc.tensor.matmul(
-                            out=st["sums", i][:, t, b0 : b0 + width],
+                            out=st["sums", i][:, b0 : b0 + width, t],
                             lhsT=x[:, c, D * e + t : D * e + D : 4],
                             rhs=pooling[r][1][:],
                             start=(e == 0),
@@ -262,7 +267,7 @@ def tile_simplepredictor_t_kernel(
                 give_back(("ctx", i))
 
         def add_pairs(i, q):
-            if q == 0:
+            if ("pairs", i) not in st:
                 st["pairs", i] = big_tile(QUARTERS * F, F32, "pairs", ("pairs", i))
             x = quarters(i, q, 1).rearrange("b (h c n t) -> b h c t n", h=2, n=4, t=4)
             nc.vector.tensor_tensor(
@@ -274,20 +279,31 @@ def tile_simplepredictor_t_kernel(
             if q == QUARTERS - 1:
                 give_back(("ctx", i))
 
+        def widen_rows(i, q, part):
+            if part == 0:
+                st["wide", i, q] = big_tile(QUARTERS * F, F32, "wide", ("wide", i, q))
+            nc.scalar.copy(
+                out=st["wide", i, q][:, D * part : D * part + D].rearrange("b (t c n) -> b c t n", t=4, n=4),
+                in_=quarters(i, q, 1)[:, D * part : D * part + D].rearrange("b (c n t) -> b c t n", n=4, t=4),
+            )
+
         def pool_pairs(i, q):
             if q == 0:
                 st["sums", i] = psum.tile([P, 4, P], F32, tag="pool", bufs=3, name="sums")
+            wide = (i, q) == WIDENED
             for t in range(4):
-                for j in range(2):
-                    w0 = F * q + 2 * P * t + P * j
+                for j in range(4 if wide else 2):
+                    w0 = D * j + P * t if wide else F * q + 2 * P * t + P * j
                     nc.tensor.matmul(
                         out=st["sums", i][:, t, :],
-                        lhsT=st["pairs", i][:, w0 : w0 + P],
+                        lhsT=(st["wide", i, q] if wide else st["pairs", i])[:, w0 : w0 + P],
                         rhs=ident_f32[:],
                         is_transpose=True,
                         start=(q, t, j) == (0, 0, 0),
                         stop=(q, t, j) == (QUARTERS - 1, 3, 1),
                     )
+            if wide:
+                give_back(("wide", i, q))
             if q == QUARTERS - 1:
                 give_back(("pairs", i))
 
@@ -295,7 +311,7 @@ def tile_simplepredictor_t_kernel(
             mean = work.tile([P, P, 4], BF16, align_bytes=64, tag="mean", name="mean")
             nc.vector.tensor_tensor(
                 out=mean[:],
-                in0=st["sums", i][:].rearrange("p t b -> p b t"),
+                in0=st["sums", i][:].rearrange("p t b -> p b t") if i in WHOLE else st["sums", i][:],
                 in1=factor_all[:, P * i : P * i + P].unsqueeze(2).to_broadcast([P, P, 4]),
                 op=ALU.mult,
             )
@@ -375,42 +391,54 @@ def tile_simplepredictor_t_kernel(
             )
             st["centred", i] = centred
 
-        def normalise(i):
-            hn = work.tile([P, F], BF16, tag="hn", name="hn")
+        def normalise(i, first=0, end=2):
+            if first == 0:
+                st["hn", i] = work.tile([P, F], BF16, tag="hn", name="hn")
+            cols = slice(HALF * first, HALF * end)
             nc.vector.scalar_tensor_tensor(
-                out=hn[:], in0=st["centred", i][:], scalar=st["rstd", i][:], in1=beta_all[:], op0=ALU.mult, op1=ALU.add
+                out=st["hn", i][:, cols],
+                in0=st["centred", i][:, cols],
+                scalar=st["rstd", i][:],
+                in1=beta_all[:, cols],
+                op0=ALU.mult,
+                op1=ALU.add,
             )
-            st["hn", i] = hn
 
-        def transpose_hn(i):
-            turned = psum.tile([P, 2, 2, P], F32, tag="turned_hn", bufs=1, name="turned_hn")
+        def transpose_hn(i, first=0, end=2, tag="turned_hn", bufs=1):
+            turned = psum.tile([P, end - first, 2, P], F32, tag=tag, bufs=bufs, name="turned_hn")
             words = st["hn", i][:].bitcast(F32)
-            for g in range(2):
+            for g in range(first, end):
                 for u in range(2):
                     w0 = 256 * g + 128 * u
-                    nc.tensor.transpose(turned[:, g, u, :], words[:, w0 : w0 + 128], ident_f32[:])
-            st["turned_hn", i] = turned
+                    nc.tensor.transpose(turned[:, g - first, u, :], words[:, w0 : w0 + 128], ident_f32[:])
+            st["turned_hn", i, first] = turned
 
-        def interleave_hn(i):
-            hn_words = work.tile([P, 2 * P * 4], BF16, align_bytes=64, tag="hn_words", name="hn_words")
+        def interleave_hn(i, first=0, end=2):
+            if first == 0:
+                st["hn_words", i] = work.tile([P, 2 * P * 4], BF16, align_bytes=64, tag="hn_words", name="hn_words")
             nc.scalar.copy(
-                out=hn_words[:].bitcast(F32).rearrange("p (g b u) -> p g b u", g=2, u=2),
-                in_=st["turned_hn", i][:].rearrange("p g u b -> p g b u"),
+                out=st["hn_words", i][:, HALF * first : HALF * end].bitcast(F32).rearrange("p (g b u) -> p g b u", b=P, u=2),
+                in_=st["turned_hn", i, first][:].rearrange("p g u b -> p g b u"),
             )
-            st["hn_words", i] = hn_words
 
-        def quantise_hn(i):
-            codes = work.tile([P, 2 * P], U32, align_bytes=64, tag="hn_codes", name="hn_codes")
-            plane = work.tile([P, 2 * P], U8, align_bytes=64, tag="hn_plane", name="hn_plane")
-            nc.vector.quantize_mx(out=codes[:].bitcast(FP8X4), scales=plane[:], in_=st["hn_words", i][:])
-            st["hn_codes", i], st["hn_plane", i] = codes, plane
+        def quantise_hn(i, first=0, end=2):
+            if first == 0:
+                st["hn_codes", i] = work.tile([P, 2 * P], U32, align_bytes=64, tag="hn_codes", name="hn_codes")
+                st["hn_plane", i] = work.tile([P, 2 * P], U8, align_bytes=64, tag="hn_plane", name="hn_plane")
+            part = slice(P * first, P * end)
+            nc.vector.quantize_mx(
+                out=st["hn_codes", i][:, part].bitcast(FP8X4),
+                scales=st["hn_plane", i][:, part],
+                in_=st["hn_words", i][:, HALF * first : HALF * end],
+            )
 
-        def multiply_w2(i):
-            acc = psum.tile([P, D], F32, tag="out", bufs=1, name="acc2")
-            for g in range(2):
+        def multiply_w2(i, first=0, end=2):
+            if first == 0:
+                st["acc2", i] = psum.tile([P, D], F32, tag="out", bufs=1, name="acc2")
+            for g in range(first, end):
                 part = slice(P * g, P * g + P)
                 nc.tensor.matmul_mx(
-                    out=acc[:],
+                    out=st["acc2", i][:],
                     lhsT=st["hn_codes", i][:, part].bitcast(FP8X4),
                     lhsT_scale=st["hn_plane", i][:, part],
                     rhs=w2_codes[:, g, :].bitcast(FP8X4),
@@ -418,7 +446,6 @@ def tile_simplepredictor_t_kernel(
                     start=(g == 0),
                     stop=(g == 1),
                 )
-            st["acc2", i] = acc
 
         def mask_b2(i, on_vector=True):
             masked = work.tile([P, D], BF16, tag="b2_masked", name="b2_masked")
@@ -451,12 +478,12 @@ def tile_simplepredictor_t_kernel(
                     nc.vector.tensor_scalar_mul(dst, st["slots", i][:, :D], mask)
                 else:
                     nc.scalar.activation(out=dst, in_=st["slots", i][:, :D], func=ACT.Copy, scale=mask)
-                part = slots_per_store(i)
-                if (j + 1) % part == 0:
-                    nc.sync.dma_start(
-                        out=out[P * i : P * i + P, j + 1 - part : j + 1, :].rearrange("b j d -> b (j d)"),
-                        in_=st["slots", i][:, D * (j + 1 - part) : D * (j + 1)],
-                    )
+                for first, end in stores(i):
+                    if j + 1 == end:
+                        nc.sync.dma_start(
+                            out=out[P * i : P * i + P, first:end, :].rearrange("b j d -> b (j d)"),
+                            in_=st["slots", i][:, D * first : D * end],
+                        )
 
         nc.vector.tensor_reduce(out=count[:], in_=cmask[:], axis=X, op=ALU.add)
         nc.vector.tensor_copy(out=pooling[2][1][:], in_=pooling[2][0][:])
@@ -541,6 +568,7 @@ def tile_simplepredictor_t_kernel(
             add_b1(s)
             if final:
                 add_pairs(s + 1, 3)
+                add_b2(s - 2)
             pool_until(s + 1, 3)
             if s == 1:
                 b2_turned = turn_vector(5)
@@ -553,7 +581,7 @@ def tile_simplepredictor_t_kernel(
             when(s - 1, transpose_hn)
             squares(s)
             if final:
-                fill_slots(0, False)
+                fill_slots(1, False)
             when(s - 1, interleave_hn)
             if s == 1:
                 b2_all = spread_b2(b2_turned)
@@ -564,18 +592,19 @@ def tile_simplepredictor_t_kernel(
                 pool_until(s + 3, -1)
             else:
                 pool_until(s + 2, 0 if s == 1 else 1)
-            when(s - 2, add_b2)
+            if not final:
+                when(s - 2, add_b2)
             if middle:
                 add_pairs(s + 2, 1)
             scale_mean(s + 1)
-            if first:
+            if first and (s + 3, 0) != WIDENED:
                 add_pairs(s + 3, 0)
             if s == 0:
                 quantise_w2(1)
                 give_back("w2")
             if s == 1:
                 nc.vector.tensor_copy(out=n_of_row[:], in_=st["n_psum"][:])
-            if s > 2:
+            if s > 1:
                 mask_b2(s - 1)
             quantise_mean(s + 1)
             multiply_w1(s + 1)
@@ -600,8 +629,9 @@ def tile_simplepredictor_t_kernel(
             fill_slots(1, False)
             inverse_deviation(s)
             if s == 1:
-                mask_b2(0, False)
-                mask_b2(1, False)
+                mask_b2(0)
+                for part in range(4):
+                    widen_rows(*WIDENED, part)
             fill_slots(max(spare - 1, 0), True)
             fill_slots(4, False)
 
@@ -612,27 +642,35 @@ def tile_simplepredictor_t_kernel(
         transpose_hn(LAST - 1)
         fill_slots(1, False)
         mean_of_h(LAST)
+        interleave_hn(LAST - 1)
         squares(LAST)
         add_b2(LAST - 2)
         mask_b2(LAST - 1)
-        fill_slots(3, True)
-        centre(LAST)
-        interleave_hn(LAST - 1)
-        inverse_deviation(LAST)
-        fill_slots(1, True)
+        fill_slots(4, True)
         quantise_hn(LAST - 1)
         multiply_w2(LAST - 1)
-        mask_b2(LAST)
-        fill_slots(3, False)
-        normalise(LAST)
-        transpose_hn(LAST)
+        centre(LAST)
+        fill_slots(1, False)
+        inverse_deviation(LAST)
+        fill_slots(1, True)
+        fill_slots(1, False)
         add_b2(LAST - 1)
-        interleave_hn(LAST)
-        fill_slots(4, True)
-        quantise_hn(LAST)
-        multiply_w2(LAST)
         fill_slots(2, False)
-        fill_slots(4, True)
+        normalise(LAST, 0, 1)
+        transpose_hn(LAST, 0, 1)
+        normalise(LAST, 1, 2)
+        transpose_hn(LAST, 1, 2, "pool", 3)
+        interleave_hn(LAST, 0, 1)
+        interleave_hn(LAST, 1, 2)
+        mask_b2(LAST)
+        fill_slots(2, True)
+        quantise_hn(LAST, 0, 1)
+        multiply_w2(LAST, 0, 1)
+        fill_slots(1, True)
+        quantise_hn(LAST, 1, 2)
+        multiply_w2(LAST, 1, 2)
+        fill_slots(1, False)
+        fill_slots(1, True)
         add_b2(LAST)
         while waiting:
             fill_slots(2, True)

@@ -12,21 +12,25 @@ FLOPS = 2 * B * D * F + 2 * B * F * D
 P = 128
 NT = B // P
 LAST = NT - 1
-WHOLE = (0, 4, 7)
-WIDENED = (4, 0)
 HALF = F // 2
 QUARTERS = 4
-BLOCKS = 4
 
-WIDE_QUARTERS = 5
+MIDDLE = 4
+WHOLE = (0, MIDDLE)
 
-QUARTERS_PER_LOAD = (1, 1, 1, 1, 2, 2, 2, 2)
+WIDE_QUARTERS = 1
+
+FIRST_BY_HALVES = 4
 
 BIG_BUFFERS = 9
 
-FIRST_LOADS = 5
+VECTOR_SLOTS = 2
 
-FIRST_SPLIT_STORE = NT - 5
+SUM_BANKS = 3
+HIDDEN_BANKS = 3
+
+ROW_B1, ROW_GAMMA, ROW_BETA, ROW_B2 = 2, 3, 4, 5
+VECTOR_ROWS = 6
 
 F32 = mybir.dt.float32
 BF16 = mybir.dt.bfloat16
@@ -42,13 +46,6 @@ X = mybir.AxisListType.X
 def rows_per_partition(i, quarter):
     earlier = QUARTERS * len([k for k in range(i) if k not in WHOLE]) + quarter
     return 4 if earlier < WIDE_QUARTERS else 2
-
-
-def stores(i):
-    if i < FIRST_SPLIT_STORE:
-        return ((0, T),)
-    cut = 4 if i == LAST else T // 2
-    return ((0, cut), (cut, T))
 
 
 def hidden_block(g, u):
@@ -89,7 +86,7 @@ def tile_simplepredictor_t_kernel(
             out=w2_bytes[:].rearrange("p g t n -> p g (t n)"), in_=W2_bytes.rearrange("(g p t) n -> p g (t n)", g=2, t=4)
         )
         nc.sync.dma_start(out=vectors[0:2, :], in_=W2_scale.rearrange("(g k) o -> g (k o)", g=2))
-        for row, vec in enumerate((b1, gamma, beta, b2), 2):
+        for row, vec in enumerate((b1, gamma, beta, b2), ROW_B1):
             nc.sync.dma_start(
                 out=vectors[row : row + 1, :].bitcast(BF16)[:, : vec.shape[0]], in_=vec.rearrange("(o f) -> o f", o=1)
             )
@@ -103,24 +100,18 @@ def tile_simplepredictor_t_kernel(
         def load_rows(i, first=0, end=QUARTERS):
             if first == 0:
                 ctx[i] = big_tile(L * D, BF16, "ctx", ("ctx", i))
-            if i in WHOLE:
-                src = context_repr[P * i : P * i + P].rearrange("b l d -> b (l d)")
-                n = QUARTERS_PER_LOAD[i]
-                for q in range(first, end, n):
+            n = 1 if i < FIRST_BY_HALVES else 2
+            for q in range(first, end, n):
+                if i in WHOLE:
+                    src = context_repr[P * i : P * i + P].rearrange("b l d -> b (l d)")
                     nc.sync.dma_start(out=quarters(i, q, n), in_=src[:, 4 * D * q : 4 * D * (q + n)])
-                return
-            q = first
-            while q < end:
-                r = rows_per_partition(i, q)
-                n = 1
-                while n < QUARTERS_PER_LOAD[i] and q + n < end and rows_per_partition(i, q + n) == r:
-                    n += 1
-                row0 = 512 * (QUARTERS * i + q)
-                nc.sync.dma_start(
-                    out=quarters(i, q, n).rearrange("p (c x) -> p c x", x=r * D),
-                    in_=rows[row0 : row0 + 512 * n, :].rearrange("(c p r) d -> p c (r d)", p=P, r=r),
-                )
-                q += n
+                else:
+                    r = rows_per_partition(i, q)
+                    row0 = 512 * (QUARTERS * i + q)
+                    nc.sync.dma_start(
+                        out=quarters(i, q, n).rearrange("p (c x) -> p c x", x=r * D),
+                        in_=rows[row0 : row0 + 512 * n, :].rearrange("(c p r) d -> p c (r d)", p=P, r=r),
+                    )
 
         load_rows(0)
         w1_stage = big_tile(8 * F, BF16, "w1_stage", "w1")
@@ -129,10 +120,11 @@ def tile_simplepredictor_t_kernel(
         load_rows(1)
         tmask = keep.tile([P, 8, L], BF16)
         nc.sync.dma_start(out=tmask[:], in_=target_mask.rearrange("(p i) l -> p i l", i=8))
-        load_rows(2)
-        load_rows(4, 0, 2)
-        load_rows(3)
-        load_rows(4, 2, 4)
+        for i in range(2, MIDDLE - 1):
+            load_rows(i)
+        load_rows(MIDDLE, 0, 2)
+        load_rows(MIDDLE - 1)
+        load_rows(MIDDLE, 2, QUARTERS)
         w2_stage = big_tile(16 * D, BF16, "w2_stage", "w2")
 
         ident_f32 = keep.tile([P, P], F32)
@@ -149,12 +141,12 @@ def tile_simplepredictor_t_kernel(
         nc.scalar.activation(out=table_out[:], in_=table_in[:], func=ACT.Gelu)
 
         def selection(r):
-            wide = keep.tile([P, 8 * r], F32, name="selection%d_f32" % r)
+            sel_f32 = keep.tile([P, 8 * r], F32, name="selection%d_f32" % r)
             sel = keep.tile([P, 8 * r], BF16, name="selection%d" % r)
             nc.vector.tensor_reduce(
-                out=wide[:], in_=ident_f32[:].rearrange("p (j q) -> p j q", q=L // r), axis=X, op=ALU.add
+                out=sel_f32[:], in_=ident_f32[:].rearrange("p (j q) -> p j q", q=L // r), axis=X, op=ALU.add
             )
-            return wide, sel
+            return sel_f32, sel
 
         pooling = {r: selection(r) for r in (1, 2, 4)}
         mod16 = keep.tile([P, 16], F32)
@@ -167,7 +159,7 @@ def tile_simplepredictor_t_kernel(
         factor_all = keep.tile([P, B], F32)
 
         def spread_factor(k):
-            turned = psum.tile([P, 4, P], F32, tag="h", bufs=3, name="turned")
+            turned = psum.tile([P, 4, P], F32, tag="hidden", bufs=HIDDEN_BANKS, name="turned")
             for i in range(4):
                 column = factor[:, 4 * k + i : 4 * k + i + 1]
                 nc.tensor.transpose(turned[:, i, :], column.to_broadcast([P, P]), ident_f32[:])
@@ -176,15 +168,15 @@ def tile_simplepredictor_t_kernel(
                 in_=turned[:].rearrange("p i n -> p n i"),
             )
 
-        columns = keep.tile([P, 6, 4], F32)
+        columns = keep.tile([P, VECTOR_ROWS, 4], F32)
 
         def turn_rows():
-            turned = psum.tile([P, 4, P], F32, tag="h", bufs=3, name="turned")
+            turned = psum.tile([P, 4, P], F32, tag="hidden", bufs=HIDDEN_BANKS, name="turned")
             for t in range(4):
                 nc.tensor.transpose(turned[:, t, :], vectors[:, t::4], ident_f32[:])
-            nc.scalar.copy(out=columns[:], in_=turned[:, :, :6].rearrange("p t row -> p row t"))
+            nc.scalar.copy(out=columns[:], in_=turned[:, :, :VECTOR_ROWS].rearrange("p t row -> p row t"))
 
-        def turn_vector(row, tag="h", bufs=3):
+        def turn_vector(row, tag="hidden", bufs=HIDDEN_BANKS):
             turned = psum.tile([P, 4, P], F32, tag=tag, bufs=bufs, name="turned")
             for t in range(4):
                 nc.tensor.transpose(turned[:, t, :], columns[:, row, t : t + 1].to_broadcast([P, P]), ident_f32[:])
@@ -200,7 +192,9 @@ def tile_simplepredictor_t_kernel(
 
         w1_codes = keep.tile([P, F], U32, align_bytes=64)
         w1_planes = keep.tile([P, F], U8, align_bytes=64)
-        w1_words = [w1_stage[:, 4 * HALF * (2 + g) : 4 * HALF * (3 + g)].rearrange("p (c t) -> p c t", t=4) for g in range(2)]
+        w1_words = [
+            w1_stage[:, 4 * HALF * (2 + g) : 4 * HALF * (3 + g)].rearrange("p (c t) -> p c t", t=4) for g in range(2)
+        ]
 
         def interleave_w1(g):
             copy = (nc.vector.tensor_copy, nc.scalar.copy)[g]
@@ -244,15 +238,15 @@ def tile_simplepredictor_t_kernel(
             )
 
         st = {}
-        pooled = [QUARTERS, 2] + [0] * (NT - 2)
+        pooled = [0] * NT
 
         def pool(i, q):
             if q == 0:
-                st["sums", i] = psum.tile([P, P, 4], F32, tag="pool", bufs=3, name="sums")
+                st["sums", i] = psum.tile([P, P, 4], F32, tag="pool", bufs=SUM_BANKS, name="sums")
             r = rows_per_partition(i, q)
             width = 8 * r
             x = quarters(i, q, 1).rearrange("p (c x) -> p c x", x=r * D)
-            for c in range(BLOCKS // r):
+            for c in range(4 // r):
                 b0 = 32 * q + width * c
                 for t in range(4):
                     for e in range(r):
@@ -279,33 +273,42 @@ def tile_simplepredictor_t_kernel(
             if q == QUARTERS - 1:
                 give_back(("ctx", i))
 
-        def widen_rows(i, q, part):
-            if part == 0:
-                st["wide", i, q] = big_tile(QUARTERS * F, F32, "wide", ("wide", i, q))
-            nc.scalar.copy(
-                out=st["wide", i, q][:, D * part : D * part + D].rearrange("b (t c n) -> b c t n", t=4, n=4),
-                in_=quarters(i, q, 1)[:, D * part : D * part + D].rearrange("b (c n t) -> b c t n", n=4, t=4),
-            )
+        def widen_first_quarter(i):
+            st["wide", i] = big_tile(QUARTERS * F, F32, "wide", ("wide", i))
+            for j in range(4):
+                nc.scalar.copy(
+                    out=st["wide", i][:, D * j : D * j + D].rearrange("b (t c n) -> b c t n", t=4, n=4),
+                    in_=quarters(i, 0, 1)[:, D * j : D * j + D].rearrange("b (c n t) -> b c t n", n=4, t=4),
+                )
 
-        def pool_pairs(i, q):
+        def pool_whole(i, q):
             if q == 0:
-                st["sums", i] = psum.tile([P, 4, P], F32, tag="pool", bufs=3, name="sums")
-            wide = (i, q) == WIDENED
+                st["sums", i] = psum.tile([P, 4, P], F32, tag="pool", bufs=SUM_BANKS, name="sums")
+            widened = q == 0 and ("wide", i) in st
             for t in range(4):
-                for j in range(4 if wide else 2):
-                    w0 = D * j + P * t if wide else F * q + 2 * P * t + P * j
+                if widened:
+                    addends = [st["wide", i][:, D * j + P * t : D * j + P * t + P] for j in range(4)]
+                else:
+                    w0 = F * q + 2 * P * t
+                    addends = [st["pairs", i][:, w0 + P * j : w0 + P * j + P] for j in range(2)]
+                for j, addend in enumerate(addends):
                     nc.tensor.matmul(
                         out=st["sums", i][:, t, :],
-                        lhsT=(st["wide", i, q] if wide else st["pairs", i])[:, w0 : w0 + P],
+                        lhsT=addend,
                         rhs=ident_f32[:],
                         is_transpose=True,
                         start=(q, t, j) == (0, 0, 0),
                         stop=(q, t, j) == (QUARTERS - 1, 3, 1),
                     )
-            if wide:
-                give_back(("wide", i, q))
+            if widened:
+                give_back(("wide", i))
             if q == QUARTERS - 1:
                 give_back(("pairs", i))
+
+        def pool_until(i, last):
+            while i < NT and pooled[i] <= last:
+                (pool_whole if i in WHOLE else pool)(i, pooled[i])
+                pooled[i] += 1
 
         def scale_mean(i):
             mean = work.tile([P, P, 4], BF16, align_bytes=64, tag="mean", name="mean")
@@ -328,7 +331,7 @@ def tile_simplepredictor_t_kernel(
         def multiply_w1(i, halves=(0, 1)):
             for g in halves:
                 cols = slice(HALF * g, HALF * g + HALF)
-                acc = psum.tile([P, HALF], F32, tag="h", bufs=3, name="acc")
+                acc = psum.tile([P, HALF], F32, tag="hidden", bufs=HIDDEN_BANKS, name="acc")
                 nc.tensor.matmul_mx(
                     out=acc[:],
                     lhsT=st["mean_codes", i][:].bitcast(FP8X4),
@@ -391,54 +394,42 @@ def tile_simplepredictor_t_kernel(
             )
             st["centred", i] = centred
 
-        def normalise(i, first=0, end=2):
-            if first == 0:
-                st["hn", i] = work.tile([P, F], BF16, tag="hn", name="hn")
-            cols = slice(HALF * first, HALF * end)
+        def normalise(i):
+            hn = work.tile([P, F], BF16, tag="hn", name="hn")
             nc.vector.scalar_tensor_tensor(
-                out=st["hn", i][:, cols],
-                in0=st["centred", i][:, cols],
-                scalar=st["rstd", i][:],
-                in1=beta_all[:, cols],
-                op0=ALU.mult,
-                op1=ALU.add,
+                out=hn[:], in0=st["centred", i][:], scalar=st["rstd", i][:], in1=beta_all[:], op0=ALU.mult, op1=ALU.add
             )
+            st["hn", i] = hn
 
-        def transpose_hn(i, first=0, end=2, tag="turned_hn", bufs=1):
-            turned = psum.tile([P, end - first, 2, P], F32, tag=tag, bufs=bufs, name="turned_hn")
+        def transpose_hn(i):
+            turned = psum.tile([P, 2, 2, P], F32, tag="turned_hn", bufs=1, name="turned_hn")
             words = st["hn", i][:].bitcast(F32)
-            for g in range(first, end):
+            for g in range(2):
                 for u in range(2):
                     w0 = 256 * g + 128 * u
-                    nc.tensor.transpose(turned[:, g - first, u, :], words[:, w0 : w0 + 128], ident_f32[:])
-            st["turned_hn", i, first] = turned
+                    nc.tensor.transpose(turned[:, g, u, :], words[:, w0 : w0 + 128], ident_f32[:])
+            st["turned_hn", i] = turned
 
-        def interleave_hn(i, first=0, end=2):
-            if first == 0:
-                st["hn_words", i] = work.tile([P, 2 * P * 4], BF16, align_bytes=64, tag="hn_words", name="hn_words")
+        def interleave_hn(i):
+            hn_words = work.tile([P, 2 * P * 4], BF16, align_bytes=64, tag="hn_words", name="hn_words")
             nc.scalar.copy(
-                out=st["hn_words", i][:, HALF * first : HALF * end].bitcast(F32).rearrange("p (g b u) -> p g b u", b=P, u=2),
-                in_=st["turned_hn", i, first][:].rearrange("p g u b -> p g b u"),
+                out=hn_words[:].bitcast(F32).rearrange("p (g b u) -> p g b u", g=2, u=2),
+                in_=st["turned_hn", i][:].rearrange("p g u b -> p g b u"),
             )
+            st["hn_words", i] = hn_words
 
-        def quantise_hn(i, first=0, end=2):
-            if first == 0:
-                st["hn_codes", i] = work.tile([P, 2 * P], U32, align_bytes=64, tag="hn_codes", name="hn_codes")
-                st["hn_plane", i] = work.tile([P, 2 * P], U8, align_bytes=64, tag="hn_plane", name="hn_plane")
-            part = slice(P * first, P * end)
-            nc.vector.quantize_mx(
-                out=st["hn_codes", i][:, part].bitcast(FP8X4),
-                scales=st["hn_plane", i][:, part],
-                in_=st["hn_words", i][:, HALF * first : HALF * end],
-            )
+        def quantise_hn(i):
+            codes = work.tile([P, 2 * P], U32, align_bytes=64, tag="hn_codes", name="hn_codes")
+            plane = work.tile([P, 2 * P], U8, align_bytes=64, tag="hn_plane", name="hn_plane")
+            nc.vector.quantize_mx(out=codes[:].bitcast(FP8X4), scales=plane[:], in_=st["hn_words", i][:])
+            st["hn_codes", i], st["hn_plane", i] = codes, plane
 
-        def multiply_w2(i, first=0, end=2):
-            if first == 0:
-                st["acc2", i] = psum.tile([P, D], F32, tag="out", bufs=1, name="acc2")
-            for g in range(first, end):
+        def multiply_w2(i):
+            acc = psum.tile([P, D], F32, tag="out", bufs=1, name="acc2")
+            for g in range(2):
                 part = slice(P * g, P * g + P)
                 nc.tensor.matmul_mx(
-                    out=st["acc2", i][:],
+                    out=acc[:],
                     lhsT=st["hn_codes", i][:, part].bitcast(FP8X4),
                     lhsT_scale=st["hn_plane", i][:, part],
                     rhs=w2_codes[:, g, :].bitcast(FP8X4),
@@ -446,16 +437,16 @@ def tile_simplepredictor_t_kernel(
                     start=(g == 0),
                     stop=(g == 1),
                 )
+            st["acc2", i] = acc
 
-        def mask_b2(i, on_vector=True):
+        def mask_b2(i):
             masked = work.tile([P, D], BF16, tag="b2_masked", name="b2_masked")
-            if on_vector:
-                nc.vector.tensor_scalar_mul(masked[:], b2_all[:], valid[:, i, 0:1])
-            else:
-                nc.scalar.activation(out=masked[:], in_=b2_all[:], func=ACT.Copy, scale=valid[:, i, 0:1])
+            nc.vector.tensor_scalar_mul(masked[:], b2_all[:], valid[:, i, 0:1])
             st["b2_masked", i] = masked
 
-        def add_b2(i):
+        waiting = []
+
+        def first_slot(i):
             st["slots", i] = big_tile(T * D, F32, "slots", ("slots", i))
             nc.vector.scalar_tensor_tensor(
                 out=st["slots", i][:, :D],
@@ -467,10 +458,8 @@ def tile_simplepredictor_t_kernel(
             )
             waiting.extend((i, j) for j in range(1, T))
 
-        waiting = []
-
-        def fill_slots(count, on_vector):
-            for i, j in waiting[:count]:
+        def fill_slots(number, on_vector):
+            for i, j in waiting[:number]:
                 waiting.remove((i, j))
                 mask = valid[:, i, j : j + 1]
                 dst = st["slots", i][:, D * j : D * j + D]
@@ -478,52 +467,10 @@ def tile_simplepredictor_t_kernel(
                     nc.vector.tensor_scalar_mul(dst, st["slots", i][:, :D], mask)
                 else:
                     nc.scalar.activation(out=dst, in_=st["slots", i][:, :D], func=ACT.Copy, scale=mask)
-                for first, end in stores(i):
-                    if j + 1 == end:
-                        nc.sync.dma_start(
-                            out=out[P * i : P * i + P, first:end, :].rearrange("b j d -> b (j d)"),
-                            in_=st["slots", i][:, D * first : D * end],
-                        )
-
-        nc.vector.tensor_reduce(out=count[:], in_=cmask[:], axis=X, op=ALU.add)
-        nc.vector.tensor_copy(out=pooling[2][1][:], in_=pooling[2][0][:])
-        nc.vector.tensor_scalar_max(count_or_1[:], count[:], 1.0)
-        nc.vector.tensor_copy(out=pooling[4][1][:], in_=pooling[4][0][:])
-        nc.vector.reciprocal(reciprocal[:], count_or_1[:])
-        nc.vector.tensor_copy(out=pooling[1][1][:], in_=pooling[1][0][:])
-        nc.vector.scalar_tensor_tensor(
-            out=factor[:], in0=count[:], scalar=0.0, in1=reciprocal[:], op0=ALU.is_gt, op1=ALU.mult
-        )
-        spread_factor(0)
-        spread_factor(1)
-        turn_rows()
-        widen_w2(0, range(4))
-        b1_all = spread_hidden(turn_vector(2), "b1_all")
-        gamma_turned = turn_vector(3, "out", 1)
-        beta_turned = turn_vector(4, "turned_hn", 1)
-        widen_w2(1, range(2))
-        for q in range(QUARTERS):
-            add_pairs(0, q)
-            pool_pairs(0, q)
-        interleave_w2(0, slice(0, D), nc.vector.tensor_copy)
-        interleave_w1(0)
-        interleave_w1(1)
-        widen_w2(1, range(2, 4))
-        gamma_all = spread_hidden(gamma_turned, "gamma_all")
-        beta_all = spread_hidden(beta_turned, "beta_all")
-        interleave_w2(1, slice(0, D // 2), nc.scalar.copy)
-        scale_mean(0)
-        quantise_w1(0)
-        quantise_mean(0)
-        pool(1, 0)
-        pool(1, 1)
-        multiply_w1(0, (0,))
-        quantise_w1(1)
-        give_back("w1")
-        multiply_w1(0, (1,))
-        for i in range(FIRST_LOADS, NT):
-            load_rows(i)
-        quantise_w2(0)
+                if j == T - 1:
+                    nc.sync.dma_start(
+                        out=out[P * i : P * i + P].rearrange("b j d -> b (j d)"), in_=st["slots", i][:]
+                    )
 
         target_n = keep.tile([P, 8], F32)
         picked = keep.tile([P, 16, 8], BF16)
@@ -551,127 +498,147 @@ def tile_simplepredictor_t_kernel(
             )
             return dst
 
-        def when(i, stage, *args):
-            if 0 <= i < NT:
-                stage(i, *args)
+        def valid_slots():
+            nc.vector.tensor_tensor(
+                out=valid[:],
+                in0=slot_index[:].unsqueeze(1).to_broadcast([P, NT, T]),
+                in1=n_of_row[:].unsqueeze(2).to_broadcast([P, NT, T]),
+                op=ALU.is_lt,
+            )
 
+        def when(i, stage):
+            if i >= 0:
+                stage(i)
 
-        def pool_until(i, last):
-            while i < NT and pooled[i] <= last:
-                (pool_pairs if i in WHOLE else pool)(i, pooled[i])
-                pooled[i] += 1
+        nc.vector.tensor_reduce(out=count[:], in_=cmask[:], axis=X, op=ALU.add)
+        nc.vector.tensor_copy(out=pooling[2][1][:], in_=pooling[2][0][:])
+        nc.vector.tensor_scalar_max(count_or_1[:], count[:], 1.0)
+        nc.vector.tensor_copy(out=pooling[4][1][:], in_=pooling[4][0][:])
+        nc.vector.reciprocal(reciprocal[:], count_or_1[:])
+        nc.vector.tensor_copy(out=pooling[1][1][:], in_=pooling[1][0][:])
+        nc.vector.scalar_tensor_tensor(
+            out=factor[:], in0=count[:], scalar=0.0, in1=reciprocal[:], op0=ALU.is_gt, op1=ALU.mult
+        )
+        spread_factor(0)
+        spread_factor(1)
+        turn_rows()
+        widen_w2(0, range(4))
+        b1_all = spread_hidden(turn_vector(ROW_B1), "b1_all")
+        gamma_turned = turn_vector(ROW_GAMMA, "out", 1)
+        beta_turned = turn_vector(ROW_BETA, "turned_hn", 1)
+        widen_w2(1, range(2))
+        for q in range(QUARTERS):
+            add_pairs(0, q)
+            pool_until(0, q)
+        interleave_w2(0, slice(0, D), nc.vector.tensor_copy)
+        interleave_w1(0)
+        interleave_w1(1)
+        widen_w2(1, range(2, 4))
+        gamma_all = spread_hidden(gamma_turned, "gamma_all")
+        beta_all = spread_hidden(beta_turned, "beta_all")
+        interleave_w2(1, slice(0, D // 2), nc.scalar.copy)
+        scale_mean(0)
+        quantise_w1(0)
+        quantise_mean(0)
+        pool_until(1, 1)
+        multiply_w1(0, (0,))
+        quantise_w1(1)
+        give_back("w1")
+        multiply_w1(0, (1,))
+        for i in range(MIDDLE + 1, NT):
+            load_rows(i)
+        quantise_w2(0)
 
         for s in range(LAST):
-            first, middle, final = (s + 3 in WHOLE), (s + 2 in WHOLE), (s + 1 in WHOLE)
-            spare = 0 if middle else 1
-            fill_slots(1, False)
+            two_pairs, last_pair = (s + 2 == MIDDLE), (s + 1 == MIDDLE)
+            vector_slots = 0 if two_pairs else VECTOR_SLOTS - last_pair
             add_b1(s)
-            if final:
-                add_pairs(s + 1, 3)
-                add_b2(s - 2)
+            if last_pair:
+                add_pairs(MIDDLE, 3)
+                first_slot(s - 2)
             pool_until(s + 1, 3)
             if s == 1:
-                b2_turned = turn_vector(5)
+                b2_turned = turn_vector(ROW_B2)
             gelu(s)
-            fill_slots(1, False)
             if s == 0:
                 interleave_w2(1, slice(D // 2, D), nc.vector.tensor_copy)
             mean_of_h(s)
             when(s - 1, normalise)
             when(s - 1, transpose_hn)
             squares(s)
-            if final:
+            if last_pair:
                 fill_slots(1, False)
             when(s - 1, interleave_hn)
-            if s == 1:
-                b2_all = spread_b2(b2_turned)
             if s == 0:
                 nc.vector.tensor_reduce(out=target_n[:], in_=tmask[:], axis=X, op=ALU.add)
-            if middle:
-                pool_until(s + 2, 0)
-                pool_until(s + 3, -1)
-            else:
-                pool_until(s + 2, 0 if s == 1 else 1)
-            if not final:
-                when(s - 2, add_b2)
-            if middle:
-                add_pairs(s + 2, 1)
+            if s == 1:
+                b2_all = spread_b2(b2_turned)
+            behind = two_pairs or s + 3 == MIDDLE
+            pool_until(s + 2, 1 - behind)
+            if not last_pair:
+                when(s - 2, first_slot)
+            if two_pairs:
+                add_pairs(MIDDLE, 1)
             scale_mean(s + 1)
-            if first and (s + 3, 0) != WIDENED:
-                add_pairs(s + 3, 0)
             if s == 0:
                 quantise_w2(1)
                 give_back("w2")
-            if s == 1:
+            elif s == 1:
                 nc.vector.tensor_copy(out=n_of_row[:], in_=st["n_psum"][:])
-            if s > 1:
+            else:
                 mask_b2(s - 1)
             quantise_mean(s + 1)
             multiply_w1(s + 1)
-            pool_until(s + 2, 1 if middle or s == 1 else 2)
-            fill_slots(min(spare, 1), True)
+            pool_until(s + 2, 2 - behind)
+            fill_slots(min(vector_slots, 1), True)
             centre(s)
             if s == 0:
                 count_targets()
             if s == 1:
-                nc.vector.tensor_tensor(
-                    out=valid[:],
-                    in0=slot_index[:].unsqueeze(1).to_broadcast([P, NT, T]),
-                    in1=n_of_row[:].unsqueeze(2).to_broadcast([P, NT, T]),
-                    op=ALU.is_lt,
-                )
+                valid_slots()
             when(s - 1, quantise_hn)
             when(s - 1, multiply_w2)
-            if middle:
-                add_pairs(s + 2, 2)
-                pool_until(s + 3, 0)
-                pool_until(s + 2, 2)
+            if two_pairs:
+                add_pairs(MIDDLE, 2)
+                pool_until(MIDDLE + 1, 0)
+                pool_until(MIDDLE, 2)
             fill_slots(1, False)
             inverse_deviation(s)
             if s == 1:
                 mask_b2(0)
-                for part in range(4):
-                    widen_rows(*WIDENED, part)
-            fill_slots(max(spare - 1, 0), True)
-            fill_slots(4, False)
+            if s + 3 == MIDDLE:
+                widen_first_quarter(MIDDLE)
+            fill_slots(max(vector_slots - 1, 0), True)
+            fill_slots(len(waiting), False)
 
-        fill_slots(1, False)
         add_b1(LAST)
         gelu(LAST)
         normalise(LAST - 1)
         transpose_hn(LAST - 1)
-        fill_slots(1, False)
         mean_of_h(LAST)
         interleave_hn(LAST - 1)
         squares(LAST)
-        add_b2(LAST - 2)
+        first_slot(LAST - 2)
         mask_b2(LAST - 1)
-        fill_slots(4, True)
+        fill_slots(T // 2, True)
         quantise_hn(LAST - 1)
         multiply_w2(LAST - 1)
         centre(LAST)
         fill_slots(1, False)
         inverse_deviation(LAST)
         fill_slots(1, True)
-        fill_slots(1, False)
-        add_b2(LAST - 1)
+        fill_slots(len(waiting), False)
+        first_slot(LAST - 1)
+        normalise(LAST)
+        transpose_hn(LAST)
         fill_slots(2, False)
-        normalise(LAST, 0, 1)
-        transpose_hn(LAST, 0, 1)
-        normalise(LAST, 1, 2)
-        transpose_hn(LAST, 1, 2, "pool", 3)
-        interleave_hn(LAST, 0, 1)
-        interleave_hn(LAST, 1, 2)
+        interleave_hn(LAST)
         mask_b2(LAST)
-        fill_slots(2, True)
-        quantise_hn(LAST, 0, 1)
-        multiply_w2(LAST, 0, 1)
-        fill_slots(1, True)
-        quantise_hn(LAST, 1, 2)
-        multiply_w2(LAST, 1, 2)
-        fill_slots(1, False)
-        fill_slots(1, True)
-        add_b2(LAST)
+        fill_slots(T // 2, True)
+        quantise_hn(LAST)
+        multiply_w2(LAST)
+        fill_slots(len(waiting), False)
+        first_slot(LAST)
         while waiting:
             fill_slots(2, True)
             fill_slots(1, False)

@@ -135,10 +135,6 @@ def tile_simplepredictor_t_kernel(
         nc.gpsimd.iota(
             slot_index[:], pattern=[[1, T]], base=0, channel_multiplier=0, allow_small_or_imprecise_dtypes=True
         )
-        table_in = keep.tile([P, 1], F32)
-        nc.vector.memset(table_in[:], 0.0)
-        table_out = keep.tile([P, 1], F32)
-        nc.scalar.activation(out=table_out[:], in_=table_in[:], func=ACT.Gelu)
 
         def selection(r):
             sel_f32 = keep.tile([P, 8 * r], F32, name="selection%d_f32" % r)

@@ -15,19 +15,15 @@ LAST = NT - 1
 HALF = F // 2
 QUARTERS = 4
 
-MIDDLE = 4
-WHOLE = (0, MIDDLE)
+WHOLE = (0, 3, 5, 7)
 
-WIDE_QUARTERS = 1
+WIDE_QUARTERS = 9
 
-FIRST_BY_HALVES = 4
+FIRST_BY_HALVES = 3
 
-BIG_BUFFERS = 9
+BIG_BUFFERS = 8
 
-VECTOR_SLOTS = 2
-
-SUM_BANKS = 3
-HIDDEN_BANKS = 3
+GPSIMD_SLOTS = 5
 
 ROW_B1, ROW_GAMMA, ROW_BETA, ROW_B2 = 2, 3, 4, 5
 VECTOR_ROWS = 6
@@ -81,16 +77,6 @@ def tile_simplepredictor_t_kernel(
         nc.scalar.dma_start(out=cmask[:], in_=context_mask.rearrange("(p i) l -> p i l", i=8))
         vectors = keep.tile([P, HALF], F32)
         nc.vector.memset(vectors[:], 0.0)
-        w2_bytes = keep.tile([P, 2, 4, D], U8)
-        nc.sync.dma_start(
-            out=w2_bytes[:].rearrange("p g t n -> p g (t n)"), in_=W2_bytes.rearrange("(g p t) n -> p g (t n)", g=2, t=4)
-        )
-        nc.sync.dma_start(out=vectors[0:2, :], in_=W2_scale.rearrange("(g k) o -> g (k o)", g=2))
-        for row, vec in enumerate((b1, gamma, beta, b2), ROW_B1):
-            nc.sync.dma_start(
-                out=vectors[row : row + 1, :].bitcast(BF16)[:, : vec.shape[0]], in_=vec.rearrange("(o f) -> o f", o=1)
-            )
-
         rows = context_repr.rearrange("b l d -> (b l) d")
         ctx = {}
 
@@ -100,8 +86,10 @@ def tile_simplepredictor_t_kernel(
         def load_rows(i, first=0, end=QUARTERS):
             if first == 0:
                 ctx[i] = big_tile(L * D, BF16, "ctx", ("ctx", i))
-            n = 1 if i < FIRST_BY_HALVES else 2
-            for q in range(first, end, n):
+            q = first
+            while q < end:
+                alike = i in WHOLE or q % 2 == 0 and rows_per_partition(i, q) == rows_per_partition(i, q + 1)
+                n = 2 if i >= FIRST_BY_HALVES and alike else 1
                 if i in WHOLE:
                     src = context_repr[P * i : P * i + P].rearrange("b l d -> b (l d)")
                     nc.sync.dma_start(out=quarters(i, q, n), in_=src[:, 4 * D * q : 4 * D * (q + n)])
@@ -112,19 +100,32 @@ def tile_simplepredictor_t_kernel(
                         out=quarters(i, q, n).rearrange("p (c x) -> p c x", x=r * D),
                         in_=rows[row0 : row0 + 512 * n, :].rearrange("(c p r) d -> p c (r d)", p=P, r=r),
                     )
+                q = q + n
 
-        load_rows(0)
+        load_rows(0, 0, 1)
+        nc.sync.dma_start(out=vectors[0:2, :], in_=W2_scale.rearrange("(g k) o -> g (k o)", g=2))
+        for row, vec in enumerate((b1, gamma, beta, b2), ROW_B1):
+            nc.sync.dma_start(
+                out=vectors[row : row + 1, :].bitcast(BF16)[:, : vec.shape[0]], in_=vec.rearrange("(o f) -> o f", o=1)
+            )
+        w2_bytes = keep.tile([P, 2, 4, D], U8)
+        nc.sync.dma_start(
+            out=w2_bytes[:].rearrange("p g t n -> p g (t n)"), in_=W2_bytes.rearrange("(g p t) n -> p g (t n)", g=2, t=4)
+        )
+        load_rows(0, 1, QUARTERS)
         w1_stage = big_tile(8 * F, BF16, "w1_stage", "w1")
         w1_rows = w1_stage[:, : 4 * F].rearrange("p (t c) -> p t c", t=4)
         nc.sync.dma_start(out=w1_rows, in_=W1.rearrange("(p t) c -> p t c", t=4))
         load_rows(1)
         tmask = keep.tile([P, 8, L], BF16)
         nc.sync.dma_start(out=tmask[:], in_=target_mask.rearrange("(p i) l -> p i l", i=8))
-        for i in range(2, MIDDLE - 1):
-            load_rows(i)
-        load_rows(MIDDLE, 0, 2)
-        load_rows(MIDDLE - 1)
-        load_rows(MIDDLE, 2, QUARTERS)
+        load_rows(3, 0, 2)
+        load_rows(2)
+        load_rows(3, 2, 4)
+        load_rows(5, 0, 2)
+        load_rows(4, 0, 2)
+        load_rows(5, 2, 4)
+        load_rows(4, 2, 4)
         w2_stage = big_tile(16 * D, BF16, "w2_stage", "w2")
 
         ident_f32 = keep.tile([P, P], F32)
@@ -155,36 +156,36 @@ def tile_simplepredictor_t_kernel(
         factor_all = keep.tile([P, B], F32)
 
         def spread_factor(k):
-            turned = psum.tile([P, 4, P], F32, tag="hidden", bufs=HIDDEN_BANKS, name="turned")
+            turned = psum.tile([P, 4, P], F32, tag=("out", "turned_hn")[k], bufs=1, name="turned")
             for i in range(4):
                 column = factor[:, 4 * k + i : 4 * k + i + 1]
                 nc.tensor.transpose(turned[:, i, :], column.to_broadcast([P, P]), ident_f32[:])
+            st["factor", k] = turned
+
+        def copy_factor(k):
+            turned = st["factor", k]
             nc.scalar.copy(
                 out=factor_all[:].rearrange("p (n i) -> p n i", i=8)[:, :, 4 * k : 4 * k + 4],
                 in_=turned[:].rearrange("p i n -> p n i"),
             )
 
+        scale_columns = keep.tile([P, 2, 4], F32)
         columns = keep.tile([P, VECTOR_ROWS, 4], F32)
 
-        def turn_rows():
-            turned = psum.tile([P, 4, P], F32, tag="hidden", bufs=HIDDEN_BANKS, name="turned")
-            for t in range(4):
-                nc.tensor.transpose(turned[:, t, :], vectors[:, t::4], ident_f32[:])
-            nc.scalar.copy(out=columns[:], in_=turned[:, :, :VECTOR_ROWS].rearrange("p t row -> p row t"))
+        def turn_rows(dst, picks):
+            turned = psum.tile([P, 4, P], F32, tag="hidden", name="turned")
+            for c, pick in enumerate(picks):
+                nc.tensor.transpose(turned[:, c, :], vectors[:, pick], ident_f32[:])
+            nc.scalar.copy(out=dst[:], in_=turned[:, :, : dst.shape[1]].rearrange("p c row -> p row c"))
 
-        def turn_vector(row, tag="hidden", bufs=HIDDEN_BANKS):
-            turned = psum.tile([P, 4, P], F32, tag=tag, bufs=bufs, name="turned")
-            for t in range(4):
-                nc.tensor.transpose(turned[:, t, :], columns[:, row, t : t + 1].to_broadcast([P, P]), ident_f32[:])
+        def turn_vector(row, tag, bufs, parts=4):
+            turned = psum.tile([P, parts, P], F32, tag=tag, bufs=bufs, name="turned")
+            for c in range(parts):
+                nc.tensor.transpose(turned[:, c, :], columns[:, row, c : c + 1].to_broadcast([P, P]), ident_f32[:])
             return turned
 
-        def spread_hidden(turned, name):
-            dst = keep.tile([P, F], BF16, name=name)
-            nc.scalar.copy(
-                out=dst[:].bitcast(F32).rearrange("p (g u n v) -> p g u n v", g=2, u=2, v=2),
-                in_=turned[:].rearrange("p (v u) (g n) -> p g u n v", u=2, g=2),
-            )
-            return dst
+        def as_entries(turned):
+            return turned[:].rearrange("p c m -> p (c m)").bitcast(BF16)
 
         w1_codes = keep.tile([P, F], U32, align_bytes=64)
         w1_planes = keep.tile([P, F], U8, align_bytes=64)
@@ -217,7 +218,7 @@ def tile_simplepredictor_t_kernel(
                     out=w2_rows[:, g, t, :],
                     in_=w2_bytes[:, g, t, :].bitcast(FP8),
                     func=ACT.Copy,
-                    scale=columns[:, g, t : t + 1],
+                    scale=scale_columns[:, g, t : t + 1],
                 )
 
         def interleave_w2(g, cols, copy):
@@ -238,7 +239,7 @@ def tile_simplepredictor_t_kernel(
 
         def pool(i, q):
             if q == 0:
-                st["sums", i] = psum.tile([P, P, 4], F32, tag="pool", bufs=SUM_BANKS, name="sums")
+                st["sums", i] = psum.tile([P, P, 4], F32, tag="pool", name="sums")
             r = rows_per_partition(i, q)
             width = 8 * r
             x = quarters(i, q, 1).rearrange("p (c x) -> p c x", x=r * D)
@@ -257,36 +258,53 @@ def tile_simplepredictor_t_kernel(
                 give_back(("ctx", i))
 
         def add_pairs(i, q):
-            if ("pairs", i) not in st:
-                st["pairs", i] = big_tile(QUARTERS * F, F32, "pairs", ("pairs", i))
+            pairs = work.tile([P, F], F32, tag="pairs", bufs=4, name="pairs")
             x = quarters(i, q, 1).rearrange("b (h c n t) -> b h c t n", h=2, n=4, t=4)
             nc.vector.tensor_tensor(
-                out=st["pairs", i][:, F * q : F * q + F].rearrange("b (t c n) -> b c t n", t=4, n=4),
-                in0=x[:, 0],
-                in1=x[:, 1],
-                op=ALU.add,
+                out=pairs[:].rearrange("b (t c n) -> b c t n", t=4, n=4), in0=x[:, 0], in1=x[:, 1], op=ALU.add
             )
-            if q == QUARTERS - 1:
+            st["addends", i, q] = [[pairs[:, 2 * P * t + P * j : 2 * P * t + P * j + P] for j in range(2)] for t in range(4)]
+            taken(i)
+
+        def add_pair(i, q, j, engine, tag="pair", bufs=6):
+            pair = work.tile([P, D], F32, tag=tag, bufs=bufs, align_bytes=64, name="pair")
+            x = quarters(i, q, 1).rearrange("b (h j c n t) -> b h j c t n", h=2, j=2, n=4, t=4)
+            engine.tensor_tensor(
+                out=pair[:].rearrange("b (t c n) -> b c t n", t=4, n=4), in0=x[:, 0, j], in1=x[:, 1, j], op=ALU.add
+            )
+            st["pair", i, q, j] = pair
+            if j == 1:
+                st["addends", i, q] = [[st["pair", i, q, e][:, P * t : P * t + P] for e in range(2)] for t in range(4)]
+                taken(i)
+
+        def taken(i):
+            st["taken", i] = st.get(("taken", i), 0) + 1
+            if st["taken", i] == QUARTERS:
                 give_back(("ctx", i))
 
-        def widen_first_quarter(i):
-            st["wide", i] = big_tile(QUARTERS * F, F32, "wide", ("wide", i))
-            for j in range(4):
+        def ready(i):
+            q = -1
+            while q < 3 and (i not in WHOLE or ("addends", i, q + 1) in st):
+                q += 1
+            return q
+
+        def widen(i, q, positions=range(4)):
+            if ("wide", i, q) not in st:
+                st["wide", i, q] = work.tile([P, 4 * D], F32, tag="wide", bufs=1, name="wide")
+            wide = st["wide", i, q]
+            for j in positions:
                 nc.scalar.copy(
-                    out=st["wide", i][:, D * j : D * j + D].rearrange("b (t c n) -> b c t n", t=4, n=4),
-                    in_=quarters(i, 0, 1)[:, D * j : D * j + D].rearrange("b (c n t) -> b c t n", n=4, t=4),
+                    out=wide[:, D * j : D * j + D].rearrange("b (t c n) -> b c t n", t=4, n=4),
+                    in_=quarters(i, q, 1)[:, D * j : D * j + D].rearrange("b (c n t) -> b c t n", n=4, t=4),
                 )
+            if 3 in positions:
+                st["addends", i, q] = [[wide[:, D * j + P * t : D * j + P * t + P] for j in range(4)] for t in range(4)]
+                taken(i)
 
         def pool_whole(i, q):
             if q == 0:
-                st["sums", i] = psum.tile([P, 4, P], F32, tag="pool", bufs=SUM_BANKS, name="sums")
-            widened = q == 0 and ("wide", i) in st
-            for t in range(4):
-                if widened:
-                    addends = [st["wide", i][:, D * j + P * t : D * j + P * t + P] for j in range(4)]
-                else:
-                    w0 = F * q + 2 * P * t
-                    addends = [st["pairs", i][:, w0 + P * j : w0 + P * j + P] for j in range(2)]
+                st["sums", i] = psum.tile([P, 4, P], F32, tag="pool", name="sums")
+            for t, addends in enumerate(st["addends", i, q]):
                 for j, addend in enumerate(addends):
                     nc.tensor.matmul(
                         out=st["sums", i][:, t, :],
@@ -294,12 +312,8 @@ def tile_simplepredictor_t_kernel(
                         rhs=ident_f32[:],
                         is_transpose=True,
                         start=(q, t, j) == (0, 0, 0),
-                        stop=(q, t, j) == (QUARTERS - 1, 3, 1),
+                        stop=(q, t, j) == (QUARTERS - 1, 3, len(addends) - 1),
                     )
-            if widened:
-                give_back(("wide", i))
-            if q == QUARTERS - 1:
-                give_back(("pairs", i))
 
         def pool_until(i, last):
             while i < NT and pooled[i] <= last:
@@ -327,7 +341,7 @@ def tile_simplepredictor_t_kernel(
         def multiply_w1(i, halves=(0, 1)):
             for g in halves:
                 cols = slice(HALF * g, HALF * g + HALF)
-                acc = psum.tile([P, HALF], F32, tag="hidden", bufs=HIDDEN_BANKS, name="acc")
+                acc = psum.tile([P, HALF], F32, tag="hidden", name="acc")
                 nc.tensor.matmul_mx(
                     out=acc[:],
                     lhsT=st["mean_codes", i][:].bitcast(FP8X4),
@@ -384,7 +398,7 @@ def tile_simplepredictor_t_kernel(
                 out=centred[:],
                 in0=st["h", i][:],
                 scalar=st["mu", i][:],
-                in1=gamma_all[:],
+                in1=as_entries(gamma_turned),
                 op0=ALU.subtract,
                 op1=ALU.mult,
             )
@@ -393,7 +407,7 @@ def tile_simplepredictor_t_kernel(
         def normalise(i):
             hn = work.tile([P, F], BF16, tag="hn", name="hn")
             nc.vector.scalar_tensor_tensor(
-                out=hn[:], in0=st["centred", i][:], scalar=st["rstd", i][:], in1=beta_all[:], op0=ALU.mult, op1=ALU.add
+                out=hn[:], in0=st["centred", i][:], scalar=st["rstd", i][:], in1=as_entries(beta_turned), op0=ALU.mult, op1=ALU.add
             )
             st["hn", i] = hn
 
@@ -407,7 +421,7 @@ def tile_simplepredictor_t_kernel(
             st["turned_hn", i] = turned
 
         def interleave_hn(i):
-            hn_words = work.tile([P, 2 * P * 4], BF16, align_bytes=64, tag="hn_words", name="hn_words")
+            hn_words = work.tile([P, 2 * P * 4], BF16, align_bytes=64, tag="words%d" % (i % 2), bufs=1, name="hn_words")
             nc.scalar.copy(
                 out=hn_words[:].bitcast(F32).rearrange("p (g b u) -> p g b u", g=2, u=2),
                 in_=st["turned_hn", i][:].rearrange("p g u b -> p g b u"),
@@ -454,18 +468,24 @@ def tile_simplepredictor_t_kernel(
             )
             waiting.extend((i, j) for j in range(1, T))
 
-        def fill_slots(number, on_vector):
+        def fill_slots(number, engine):
             for i, j in waiting[:number]:
                 waiting.remove((i, j))
                 mask = valid[:, i, j : j + 1]
                 dst = st["slots", i][:, D * j : D * j + D]
-                if on_vector:
+                if engine == "vector":
                     nc.vector.tensor_scalar_mul(dst, st["slots", i][:, :D], mask)
+                elif engine == "gpsimd":
+                    nc.gpsimd.tensor_scalar(
+                        out=dst, in0=st["slots", i][:, :D], scalar1=mask, scalar2=0.0, op0=ALU.mult, op1=ALU.add
+                    )
                 else:
                     nc.scalar.activation(out=dst, in_=st["slots", i][:, :D], func=ACT.Copy, scale=mask)
-                if j == T - 1:
+                parts = 2 if i >= 3 else 1
+                if (j + 1) % (T // parts) == 0:
+                    cols = slice(D * (j + 1 - T // parts), D * (j + 1))
                     nc.sync.dma_start(
-                        out=out[P * i : P * i + P].rearrange("b j d -> b (j d)"), in_=st["slots", i][:]
+                        out=out[P * i : P * i + P].rearrange("b j d -> b (j d)")[:, cols], in_=st["slots", i][:, cols]
                     )
 
         target_n = keep.tile([P, 8], F32)
@@ -486,11 +506,15 @@ def tile_simplepredictor_t_kernel(
             )
             st["n_psum"] = n_psum
 
+        def spread_b1(turned):
+            dst = keep.tile([P, F], BF16, name="b1_all")
+            nc.scalar.copy(out=dst[:].bitcast(F32), in_=turned[:].rearrange("p c m -> p (c m)"))
+            return dst
+
         def spread_b2(turned):
             dst = keep.tile([P, D], BF16, name="b2_all")
             nc.scalar.copy(
-                out=dst[:].bitcast(F32).rearrange("p (n t) -> p n t", t=4),
-                in_=turned[:, :, : P // 2].rearrange("p t n -> p n t"),
+                out=dst[:].bitcast(F32).rearrange("p (m u) -> p m u", u=2), in_=turned[:].rearrange("p u m -> p m u")
             )
             return dst
 
@@ -515,23 +539,28 @@ def tile_simplepredictor_t_kernel(
         nc.vector.scalar_tensor_tensor(
             out=factor[:], in0=count[:], scalar=0.0, in1=reciprocal[:], op0=ALU.is_gt, op1=ALU.mult
         )
+        turn_rows(scale_columns, [slice(t, HALF, 4) for t in range(4)])
+        turn_rows(columns, [slice(256 * g + u, 256 * g + 256, 2) for g in range(2) for u in range(2)])
         spread_factor(0)
         spread_factor(1)
-        turn_rows()
+        b1_turned = turn_vector(ROW_B1, "hidden", 2)
+        b2_turned = turn_vector(ROW_B2, "hidden", 2, 2)
         widen_w2(0, range(4))
-        b1_all = spread_hidden(turn_vector(ROW_B1), "b1_all")
-        gamma_turned = turn_vector(ROW_GAMMA, "out", 1)
-        beta_turned = turn_vector(ROW_BETA, "turned_hn", 1)
+        copy_factor(0)
+        copy_factor(1)
+        b1_all = spread_b1(b1_turned)
+        b2_all = spread_b2(b2_turned)
         widen_w2(1, range(2))
         for q in range(QUARTERS):
             add_pairs(0, q)
             pool_until(0, q)
-        interleave_w2(0, slice(0, D), nc.vector.tensor_copy)
+            if q == 2:
+                interleave_w2(0, slice(0, D), nc.vector.tensor_copy)
+        gamma_turned = turn_vector(ROW_GAMMA, "gamma", 1)
+        beta_turned = turn_vector(ROW_BETA, "beta", 1)
         interleave_w1(0)
         interleave_w1(1)
         widen_w2(1, range(2, 4))
-        gamma_all = spread_hidden(gamma_turned, "gamma_all")
-        beta_all = spread_hidden(beta_turned, "beta_all")
         interleave_w2(1, slice(0, D // 2), nc.scalar.copy)
         scale_mean(0)
         quantise_w1(0)
@@ -541,100 +570,121 @@ def tile_simplepredictor_t_kernel(
         quantise_w1(1)
         give_back("w1")
         multiply_w1(0, (1,))
-        for i in range(MIDDLE + 1, NT):
+        for i in range(6, NT):
             load_rows(i)
         quantise_w2(0)
 
+        VP = {1: [(3, 2)]}
+        SW = {1: [(3, 3)]}
+        VP0 = {0: [(3, 1)]}
+        LAG = (2, 3, 4, 5)
+        PA = {2: [(4, 0)], 3: [(5, 0)], 4: [(6, 0)], 5: [(7, 0)]}
+        PB = {1: [(3, 1)], 2: [(4, 1)], 4: [(6, 1)], 3: [(5, 1)], 5: [(7, 1)]}
+        PC = {0: [(2, 1)], 2: [(4, 2)], 3: [(5, 2)], 4: [(6, 2)], 5: [(7, 2)]}
+        VS = {}
         for s in range(LAST):
-            two_pairs, last_pair = (s + 2 == MIDDLE), (s + 1 == MIDDLE)
-            vector_slots = 0 if two_pairs else VECTOR_SLOTS - last_pair
+            rich = s in LAG
+            ahead, q = s + 3 - s % 2, 2 * (s % 2)
             add_b1(s)
-            if last_pair:
-                add_pairs(MIDDLE, 3)
-                first_slot(s - 2)
-            pool_until(s + 1, 3)
+            if rich:
+                add_pair(ahead, q, 0, nc.gpsimd, "words%d" % (s % 2), 1)
+                add_pair(ahead, q, 1, nc.gpsimd)
+                add_pair(ahead, q + 1, 0, nc.gpsimd)
             if s == 1:
-                b2_turned = turn_vector(ROW_B2)
+                add_pair(3, 0, 0, nc.gpsimd)
+                add_pair(3, 0, 1, nc.gpsimd)
+            when(s - 2, first_slot)
+            if not rich:
+                fill_slots(2, "gpsimd")
             gelu(s)
+            fill_slots(1, "scalar")
+            mean_of_h(s)
+            pool_until(s + 1, 3)
+            for i, r in PA.get(s, ()):
+                pool_until(i, r)
             if s == 0:
                 interleave_w2(1, slice(D // 2, D), nc.vector.tensor_copy)
-            mean_of_h(s)
+                nc.vector.tensor_reduce(out=target_n[:], in_=tmask[:], axis=X, op=ALU.add)
             when(s - 1, normalise)
             when(s - 1, transpose_hn)
-            squares(s)
-            if last_pair:
-                fill_slots(1, False)
+            fill_slots(1, "scalar")
+            if not rich:
+                fill_slots(1, "gpsimd")
             when(s - 1, interleave_hn)
-            if s == 0:
-                nc.vector.tensor_reduce(out=target_n[:], in_=tmask[:], axis=X, op=ALU.add)
             if s == 1:
-                b2_all = spread_b2(b2_turned)
-            behind = two_pairs or s + 3 == MIDDLE
-            pool_until(s + 2, 1 - behind)
-            if not last_pair:
-                when(s - 2, first_slot)
-            if two_pairs:
-                add_pairs(MIDDLE, 1)
+                widen(3, 3, range(2))
+            squares(s)
+            if s == 1:
+                widen(3, 3, (2,))
+            for i, r in PB.get(s, ()):
+                pool_until(i, r)
             scale_mean(s + 1)
             if s == 0:
                 quantise_w2(1)
                 give_back("w2")
-            elif s == 1:
-                nc.vector.tensor_copy(out=n_of_row[:], in_=st["n_psum"][:])
-            else:
-                mask_b2(s - 1)
-            quantise_mean(s + 1)
-            multiply_w1(s + 1)
-            pool_until(s + 2, 2 - behind)
-            fill_slots(min(vector_slots, 1), True)
-            centre(s)
-            if s == 0:
+                quantise_mean(1)
+                multiply_w1(1)
                 count_targets()
+            for i, r in VP0.get(s, ()):
+                add_pairs(i, r)
+            if s == 1:
+                nc.vector.tensor_copy(out=n_of_row[:], in_=st["n_psum"][:])
+            centre(s)
+            if s > 0:
+                quantise_mean(s + 1)
+                multiply_w1(s + 1)
+            for i, r in PC.get(s, ()):
+                pool_until(i, r)
             if s == 1:
                 valid_slots()
-            when(s - 1, quantise_hn)
-            when(s - 1, multiply_w2)
-            if two_pairs:
-                add_pairs(MIDDLE, 2)
-                pool_until(MIDDLE + 1, 0)
-                pool_until(MIDDLE, 2)
-            fill_slots(1, False)
-            inverse_deviation(s)
+            if s > 1:
+                mask_b2(s - 1)
+            fill_slots(1 if rich else 2, "vector")
+            if rich:
+                add_pair(ahead, q + 1, 1, nc.vector)
+            for i, r in VP.get(s, ()):
+                add_pairs(i, r)
             if s == 1:
                 mask_b2(0)
-            if s + 3 == MIDDLE:
-                widen_first_quarter(MIDDLE)
-            fill_slots(max(vector_slots - 1, 0), True)
-            fill_slots(len(waiting), False)
+            when(s - 1, quantise_hn)
+            when(s - 1, multiply_w2)
+            fill_slots(1, "scalar")
+            inverse_deviation(s)
+            fill_slots(len(waiting), "scalar")
+            for i, r in SW.get(s, ()):
+                widen(i, r, (3,))
 
         add_b1(LAST)
+        fill_slots(len(waiting), "gpsimd")
+        first_slot(LAST - 2)
+        fill_slots(2, "gpsimd")
         gelu(LAST)
+        fill_slots(1, "scalar")
+        fill_slots(1, "gpsimd")
+        mean_of_h(LAST)
         normalise(LAST - 1)
         transpose_hn(LAST - 1)
-        mean_of_h(LAST)
-        interleave_hn(LAST - 1)
         squares(LAST)
-        first_slot(LAST - 2)
+        interleave_hn(LAST - 1)
+        centre(LAST)
+        inverse_deviation(LAST)
         mask_b2(LAST - 1)
-        fill_slots(T // 2, True)
+        fill_slots(2, "vector")
+        fill_slots(1, "scalar")
         quantise_hn(LAST - 1)
         multiply_w2(LAST - 1)
-        centre(LAST)
-        fill_slots(1, False)
-        inverse_deviation(LAST)
-        fill_slots(1, True)
-        fill_slots(len(waiting), False)
-        first_slot(LAST - 1)
         normalise(LAST)
         transpose_hn(LAST)
-        fill_slots(2, False)
+        first_slot(LAST - 1)
+        fill_slots(1, "scalar")
         interleave_hn(LAST)
         mask_b2(LAST)
-        fill_slots(T // 2, True)
+        fill_slots(4, "vector")
         quantise_hn(LAST)
         multiply_w2(LAST)
-        fill_slots(len(waiting), False)
+        fill_slots(1, "scalar")
+        fill_slots(1, "vector")
         first_slot(LAST)
         while waiting:
-            fill_slots(2, True)
-            fill_slots(1, False)
+            fill_slots(2, "vector")
+            fill_slots(1, "scalar")

@@ -15,11 +15,11 @@ LAST = NT - 1
 HALF = F // 2
 QUARTERS = 4
 
-WHOLE = (0, 3, 5, 7)
+WHOLE = (0, 5, 7)
 
-WIDE_QUARTERS = 9
+WIDE_QUARTERS = 5
 
-FIRST_BY_HALVES = 3
+FIRST_BY_HALVES = 4
 
 BIG_BUFFERS = 8
 
@@ -88,7 +88,7 @@ def tile_simplepredictor_t_kernel(
                 ctx[i] = big_tile(L * D, BF16, "ctx", ("ctx", i))
             q = first
             while q < end:
-                alike = i in WHOLE or q % 2 == 0 and rows_per_partition(i, q) == rows_per_partition(i, q + 1)
+                alike = q + 1 < end and (i in WHOLE or q % 2 == 0 and rows_per_partition(i, q) == rows_per_partition(i, q + 1))
                 n = 2 if i >= FIRST_BY_HALVES and alike else 1
                 if i in WHOLE:
                     src = context_repr[P * i : P * i + P].rearrange("b l d -> b (l d)")
@@ -119,13 +119,13 @@ def tile_simplepredictor_t_kernel(
         load_rows(1)
         tmask = keep.tile([P, 8, L], BF16)
         nc.sync.dma_start(out=tmask[:], in_=target_mask.rearrange("(p i) l -> p i l", i=8))
-        load_rows(3, 0, 2)
         load_rows(2)
-        load_rows(3, 2, 4)
+        load_rows(3)
         load_rows(5, 0, 2)
         load_rows(4, 0, 2)
-        load_rows(5, 2, 4)
+        load_rows(5, 2, 3)
         load_rows(4, 2, 4)
+        load_rows(5, 3, 4)
         w2_stage = big_tile(16 * D, BF16, "w2_stage", "w2")
 
         ident_f32 = keep.tile([P, P], F32)
@@ -257,16 +257,16 @@ def tile_simplepredictor_t_kernel(
             if q == QUARTERS - 1:
                 give_back(("ctx", i))
 
-        def add_pairs(i, q):
-            pairs = work.tile([P, F], F32, tag="pairs", bufs=4, name="pairs")
+        def add_pairs(i, q, engine=nc.vector, tag="pairs", bufs=4):
+            pairs = work.tile([P, F], F32, tag=tag, bufs=bufs, align_bytes=64, name="pairs")
             x = quarters(i, q, 1).rearrange("b (h c n t) -> b h c t n", h=2, n=4, t=4)
-            nc.vector.tensor_tensor(
+            engine.tensor_tensor(
                 out=pairs[:].rearrange("b (t c n) -> b c t n", t=4, n=4), in0=x[:, 0], in1=x[:, 1], op=ALU.add
             )
             st["addends", i, q] = [[pairs[:, 2 * P * t + P * j : 2 * P * t + P * j + P] for j in range(2)] for t in range(4)]
             taken(i)
 
-        def add_pair(i, q, j, engine, tag="pair", bufs=6):
+        def add_pair(i, q, j, engine, tag="pair", bufs=4):
             pair = work.tile([P, D], F32, tag=tag, bufs=bufs, align_bytes=64, name="pair")
             x = quarters(i, q, 1).rearrange("b (h j c n t) -> b h j c t n", h=2, j=2, n=4, t=4)
             engine.tensor_tensor(
@@ -421,7 +421,7 @@ def tile_simplepredictor_t_kernel(
             st["turned_hn", i] = turned
 
         def interleave_hn(i):
-            hn_words = work.tile([P, 2 * P * 4], BF16, align_bytes=64, tag="words%d" % (i % 2), bufs=1, name="hn_words")
+            hn_words = work.tile([P, 2 * P * 4], BF16, align_bytes=64, tag="words%d" % (i % 3), bufs=1, name="hn_words")
             nc.scalar.copy(
                 out=hn_words[:].bitcast(F32).rearrange("p (g b u) -> p g b u", g=2, u=2),
                 in_=st["turned_hn", i][:].rearrange("p g u b -> p g b u"),
@@ -481,7 +481,7 @@ def tile_simplepredictor_t_kernel(
                     )
                 else:
                     nc.scalar.activation(out=dst, in_=st["slots", i][:, :D], func=ACT.Copy, scale=mask)
-                parts = 2 if i >= 3 else 1
+                parts = 2 if i >= 4 else 1
                 if (j + 1) % (T // parts) == 0:
                     cols = slice(D * (j + 1 - T // parts), D * (j + 1))
                     nc.sync.dma_start(
@@ -570,52 +570,47 @@ def tile_simplepredictor_t_kernel(
         quantise_w1(1)
         give_back("w1")
         multiply_w1(0, (1,))
-        for i in range(6, NT):
-            load_rows(i)
+        for first in (0, 2):
+            for i in range(6, NT):
+                load_rows(i, first, first + 2)
         quantise_w2(0)
 
-        VP = {1: [(3, 2)]}
-        SW = {1: [(3, 3)]}
-        VP0 = {0: [(3, 1)]}
+        VP = {2: [(5, 1)], 3: [(5, 3)], 4: [(7, 1)], 5: [(7, 3)]}
+        SW = {}
+        VP0 = {}
         LAG = (2, 3, 4, 5)
-        PA = {2: [(4, 0)], 3: [(5, 0)], 4: [(6, 0)], 5: [(7, 0)]}
-        PB = {1: [(3, 1)], 2: [(4, 1)], 4: [(6, 1)], 3: [(5, 1)], 5: [(7, 1)]}
-        PC = {0: [(2, 1)], 2: [(4, 2)], 3: [(5, 2)], 4: [(6, 2)], 5: [(7, 2)]}
+        PA = {}
+        PB = {1: [(3, 1)], 2: [(4, 1)], 3: [(5, 1)], 4: [(6, 1)], 5: [(7, 1)]}
+        PC = {0: [(2, 1)], 1: [(3, 2)], 3: [(5, 2)], 4: [(6, 2)], 5: [(7, 2)]}
         VS = {}
+        GP = {2: [(5, 0)], 3: [(5, 2)], 4: [(7, 0)], 5: [(7, 2)]}
         for s in range(LAST):
-            rich = s in LAG
-            ahead, q = s + 3 - s % 2, 2 * (s % 2)
+            gated = s + 1 in GP
             add_b1(s)
-            if rich:
-                add_pair(ahead, q, 0, nc.gpsimd, "words%d" % (s % 2), 1)
-                add_pair(ahead, q, 1, nc.gpsimd)
-                add_pair(ahead, q + 1, 0, nc.gpsimd)
-            if s == 1:
-                add_pair(3, 0, 0, nc.gpsimd)
-                add_pair(3, 0, 1, nc.gpsimd)
-            when(s - 2, first_slot)
-            if not rich:
-                fill_slots(2, "gpsimd")
+            for i, r in GP.get(s, ()):
+                add_pairs(i, r, nc.gpsimd, "words%d" % ((s - 2) % 3), 1)
             gelu(s)
-            fill_slots(1, "scalar")
             mean_of_h(s)
             pool_until(s + 1, 3)
-            for i, r in PA.get(s, ()):
-                pool_until(i, r)
             if s == 0:
                 interleave_w2(1, slice(D // 2, D), nc.vector.tensor_copy)
                 nc.vector.tensor_reduce(out=target_n[:], in_=tmask[:], axis=X, op=ALU.add)
-            when(s - 1, normalise)
-            when(s - 1, transpose_hn)
-            fill_slots(1, "scalar")
-            if not rich:
+            if s in GP:
+                squares(s)
+                when(s - 1, normalise)
+                when(s - 1, transpose_hn)
+                when(s - 2, first_slot)
+                when(s - 1, interleave_hn)
+            else:
+                when(s - 2, first_slot)
                 fill_slots(1, "gpsimd")
-            when(s - 1, interleave_hn)
-            if s == 1:
-                widen(3, 3, range(2))
-            squares(s)
-            if s == 1:
-                widen(3, 3, (2,))
+                fill_slots(1, "scalar")
+                fill_slots(1, "gpsimd")
+                fill_slots(1, "scalar")
+                when(s - 1, normalise)
+                when(s - 1, transpose_hn)
+                when(s - 1, interleave_hn)
+                squares(s)
             for i, r in PB.get(s, ()):
                 pool_until(i, r)
             scale_mean(s + 1)
@@ -625,43 +620,42 @@ def tile_simplepredictor_t_kernel(
                 quantise_mean(1)
                 multiply_w1(1)
                 count_targets()
-            for i, r in VP0.get(s, ()):
-                add_pairs(i, r)
             if s == 1:
                 nc.vector.tensor_copy(out=n_of_row[:], in_=st["n_psum"][:])
             centre(s)
             if s > 0:
                 quantise_mean(s + 1)
                 multiply_w1(s + 1)
-            for i, r in PC.get(s, ()):
-                pool_until(i, r)
             if s == 1:
                 valid_slots()
             if s > 1:
                 mask_b2(s - 1)
-            fill_slots(1 if rich else 2, "vector")
-            if rich:
-                add_pair(ahead, q + 1, 1, nc.vector)
+            if not gated:
+                when(s - 1, quantise_hn)
+                when(s - 1, multiply_w2)
+            for i, r in PC.get(s, ()):
+                pool_until(i, r)
+            fill_slots(1 if s in VP else 2, "vector")
             for i, r in VP.get(s, ()):
                 add_pairs(i, r)
             if s == 1:
                 mask_b2(0)
-            when(s - 1, quantise_hn)
-            when(s - 1, multiply_w2)
             fill_slots(1, "scalar")
             inverse_deviation(s)
+            if gated:
+                when(s - 1, quantise_hn)
+                when(s - 1, multiply_w2)
             fill_slots(len(waiting), "scalar")
             for i, r in SW.get(s, ()):
-                widen(i, r, (3,))
+                widen(i, r)
 
         add_b1(LAST)
-        fill_slots(len(waiting), "gpsimd")
-        first_slot(LAST - 2)
-        fill_slots(2, "gpsimd")
         gelu(LAST)
+        mean_of_h(LAST)
+        first_slot(LAST - 2)
+        fill_slots(1, "gpsimd")
         fill_slots(1, "scalar")
         fill_slots(1, "gpsimd")
-        mean_of_h(LAST)
         normalise(LAST - 1)
         transpose_hn(LAST - 1)
         squares(LAST)
@@ -670,15 +664,16 @@ def tile_simplepredictor_t_kernel(
         inverse_deviation(LAST)
         mask_b2(LAST - 1)
         fill_slots(2, "vector")
-        fill_slots(1, "scalar")
         quantise_hn(LAST - 1)
         multiply_w2(LAST - 1)
+        fill_slots(1, "scalar")
+        fill_slots(1, "vector")
         normalise(LAST)
         transpose_hn(LAST)
         first_slot(LAST - 1)
+        mask_b2(LAST)
         fill_slots(1, "scalar")
         interleave_hn(LAST)
-        mask_b2(LAST)
         fill_slots(4, "vector")
         quantise_hn(LAST)
         multiply_w2(LAST)

@@ -19,11 +19,15 @@ WHOLE = (0, 5, 7)
 
 WIDE_QUARTERS = 5
 
-FIRST_BY_HALVES = 4
+FIRST_BY_HALVES = 2
+
+FIRST_STORED_IN_HALVES = 4
 
 BIG_BUFFERS = 8
 
-GPSIMD_SLOTS = 5
+PAIR_BUFFERS = 4
+
+WORD_BUFFERS = 3
 
 ROW_B1, ROW_GAMMA, ROW_BETA, ROW_B2 = 2, 3, 4, 5
 VECTOR_ROWS = 6
@@ -77,6 +81,7 @@ def tile_simplepredictor_t_kernel(
         nc.scalar.dma_start(out=cmask[:], in_=context_mask.rearrange("(p i) l -> p i l", i=8))
         vectors = keep.tile([P, HALF], F32)
         nc.vector.memset(vectors[:], 0.0)
+
         rows = context_repr.rearrange("b l d -> (b l) d")
         ctx = {}
 
@@ -88,8 +93,8 @@ def tile_simplepredictor_t_kernel(
                 ctx[i] = big_tile(L * D, BF16, "ctx", ("ctx", i))
             q = first
             while q < end:
-                alike = q + 1 < end and (i in WHOLE or q % 2 == 0 and rows_per_partition(i, q) == rows_per_partition(i, q + 1))
-                n = 2 if i >= FIRST_BY_HALVES and alike else 1
+                alike = i in WHOLE or rows_per_partition(i, q) == rows_per_partition(i, q + 1)
+                n = 2 if i >= FIRST_BY_HALVES and q % 2 == 0 and q + 2 <= end and alike else 1
                 if i in WHOLE:
                     src = context_repr[P * i : P * i + P].rearrange("b l d -> b (l d)")
                     nc.sync.dma_start(out=quarters(i, q, n), in_=src[:, 4 * D * q : 4 * D * (q + n)])
@@ -124,8 +129,8 @@ def tile_simplepredictor_t_kernel(
         load_rows(5, 0, 2)
         load_rows(4, 0, 2)
         load_rows(5, 2, 3)
-        load_rows(4, 2, 4)
-        load_rows(5, 3, 4)
+        load_rows(4, 2)
+        load_rows(5, 3)
         w2_stage = big_tile(16 * D, BF16, "w2_stage", "w2")
 
         ident_f32 = keep.tile([P, P], F32)
@@ -155,15 +160,14 @@ def tile_simplepredictor_t_kernel(
         factor = keep.tile([P, 8], F32)
         factor_all = keep.tile([P, B], F32)
 
-        def spread_factor(k):
-            turned = psum.tile([P, 4, P], F32, tag=("out", "turned_hn")[k], bufs=1, name="turned")
+        def turn_factor(k, tag):
+            turned = psum.tile([P, 4, P], F32, tag=tag, bufs=1, name="turned")
             for i in range(4):
                 column = factor[:, 4 * k + i : 4 * k + i + 1]
                 nc.tensor.transpose(turned[:, i, :], column.to_broadcast([P, P]), ident_f32[:])
-            st["factor", k] = turned
+            return turned
 
-        def copy_factor(k):
-            turned = st["factor", k]
+        def spread_factor(k, turned):
             nc.scalar.copy(
                 out=factor_all[:].rearrange("p (n i) -> p n i", i=8)[:, :, 4 * k : 4 * k + 4],
                 in_=turned[:].rearrange("p i n -> p n i"),
@@ -257,66 +261,33 @@ def tile_simplepredictor_t_kernel(
             if q == QUARTERS - 1:
                 give_back(("ctx", i))
 
-        def add_pairs(i, q, engine=nc.vector, tag="pairs", bufs=4):
+        def add_pairs(i, q, engine=nc.vector, tag="pairs", bufs=PAIR_BUFFERS):
             pairs = work.tile([P, F], F32, tag=tag, bufs=bufs, align_bytes=64, name="pairs")
             x = quarters(i, q, 1).rearrange("b (h c n t) -> b h c t n", h=2, n=4, t=4)
             engine.tensor_tensor(
                 out=pairs[:].rearrange("b (t c n) -> b c t n", t=4, n=4), in0=x[:, 0], in1=x[:, 1], op=ALU.add
             )
-            st["addends", i, q] = [[pairs[:, 2 * P * t + P * j : 2 * P * t + P * j + P] for j in range(2)] for t in range(4)]
-            taken(i)
-
-        def add_pair(i, q, j, engine, tag="pair", bufs=4):
-            pair = work.tile([P, D], F32, tag=tag, bufs=bufs, align_bytes=64, name="pair")
-            x = quarters(i, q, 1).rearrange("b (h j c n t) -> b h j c t n", h=2, j=2, n=4, t=4)
-            engine.tensor_tensor(
-                out=pair[:].rearrange("b (t c n) -> b c t n", t=4, n=4), in0=x[:, 0, j], in1=x[:, 1, j], op=ALU.add
-            )
-            st["pair", i, q, j] = pair
-            if j == 1:
-                st["addends", i, q] = [[st["pair", i, q, e][:, P * t : P * t + P] for e in range(2)] for t in range(4)]
-                taken(i)
-
-        def taken(i):
-            st["taken", i] = st.get(("taken", i), 0) + 1
-            if st["taken", i] == QUARTERS:
+            st["pairs", i, q] = pairs
+            if q == QUARTERS - 1:
                 give_back(("ctx", i))
-
-        def ready(i):
-            q = -1
-            while q < 3 and (i not in WHOLE or ("addends", i, q + 1) in st):
-                q += 1
-            return q
-
-        def widen(i, q, positions=range(4)):
-            if ("wide", i, q) not in st:
-                st["wide", i, q] = work.tile([P, 4 * D], F32, tag="wide", bufs=1, name="wide")
-            wide = st["wide", i, q]
-            for j in positions:
-                nc.scalar.copy(
-                    out=wide[:, D * j : D * j + D].rearrange("b (t c n) -> b c t n", t=4, n=4),
-                    in_=quarters(i, q, 1)[:, D * j : D * j + D].rearrange("b (c n t) -> b c t n", n=4, t=4),
-                )
-            if 3 in positions:
-                st["addends", i, q] = [[wide[:, D * j + P * t : D * j + P * t + P] for j in range(4)] for t in range(4)]
-                taken(i)
 
         def pool_whole(i, q):
             if q == 0:
                 st["sums", i] = psum.tile([P, 4, P], F32, tag="pool", name="sums")
-            for t, addends in enumerate(st["addends", i, q]):
-                for j, addend in enumerate(addends):
+            for t in range(4):
+                for j in range(2):
+                    w0 = 2 * P * t + P * j
                     nc.tensor.matmul(
                         out=st["sums", i][:, t, :],
-                        lhsT=addend,
+                        lhsT=st["pairs", i, q][:, w0 : w0 + P],
                         rhs=ident_f32[:],
                         is_transpose=True,
                         start=(q, t, j) == (0, 0, 0),
-                        stop=(q, t, j) == (QUARTERS - 1, 3, len(addends) - 1),
+                        stop=(q, t, j) == (QUARTERS - 1, 3, 1),
                     )
 
         def pool_until(i, last):
-            while i < NT and pooled[i] <= last:
+            while pooled[i] <= last:
                 (pool_whole if i in WHOLE else pool)(i, pooled[i])
                 pooled[i] += 1
 
@@ -420,8 +391,11 @@ def tile_simplepredictor_t_kernel(
                     nc.tensor.transpose(turned[:, g, u, :], words[:, w0 : w0 + 128], ident_f32[:])
             st["turned_hn", i] = turned
 
+        def words_tag(i):
+            return "words%d" % (i % WORD_BUFFERS)
+
         def interleave_hn(i):
-            hn_words = work.tile([P, 2 * P * 4], BF16, align_bytes=64, tag="words%d" % (i % 3), bufs=1, name="hn_words")
+            hn_words = work.tile([P, 2 * P * 4], BF16, align_bytes=64, tag=words_tag(i), bufs=1, name="hn_words")
             nc.scalar.copy(
                 out=hn_words[:].bitcast(F32).rearrange("p (g b u) -> p g b u", g=2, u=2),
                 in_=st["turned_hn", i][:].rearrange("p g u b -> p g b u"),
@@ -472,18 +446,17 @@ def tile_simplepredictor_t_kernel(
             for i, j in waiting[:number]:
                 waiting.remove((i, j))
                 mask = valid[:, i, j : j + 1]
+                src = st["slots", i][:, :D]
                 dst = st["slots", i][:, D * j : D * j + D]
                 if engine == "vector":
-                    nc.vector.tensor_scalar_mul(dst, st["slots", i][:, :D], mask)
+                    nc.vector.tensor_scalar_mul(dst, src, mask)
                 elif engine == "gpsimd":
-                    nc.gpsimd.tensor_scalar(
-                        out=dst, in0=st["slots", i][:, :D], scalar1=mask, scalar2=0.0, op0=ALU.mult, op1=ALU.add
-                    )
+                    nc.gpsimd.tensor_scalar(out=dst, in0=src, scalar1=mask, scalar2=0.0, op0=ALU.mult, op1=ALU.add)
                 else:
-                    nc.scalar.activation(out=dst, in_=st["slots", i][:, :D], func=ACT.Copy, scale=mask)
-                parts = 2 if i >= 4 else 1
-                if (j + 1) % (T // parts) == 0:
-                    cols = slice(D * (j + 1 - T // parts), D * (j + 1))
+                    nc.scalar.activation(out=dst, in_=src, func=ACT.Copy, scale=mask)
+                together = T if i < FIRST_STORED_IN_HALVES else T // 2
+                if (j + 1) % together == 0:
+                    cols = slice(D * (j + 1 - together), D * (j + 1))
                     nc.sync.dma_start(
                         out=out[P * i : P * i + P].rearrange("b j d -> b (j d)")[:, cols], in_=st["slots", i][:, cols]
                     )
@@ -526,10 +499,6 @@ def tile_simplepredictor_t_kernel(
                 op=ALU.is_lt,
             )
 
-        def when(i, stage):
-            if i >= 0:
-                stage(i)
-
         nc.vector.tensor_reduce(out=count[:], in_=cmask[:], axis=X, op=ALU.add)
         nc.vector.tensor_copy(out=pooling[2][1][:], in_=pooling[2][0][:])
         nc.vector.tensor_scalar_max(count_or_1[:], count[:], 1.0)
@@ -540,24 +509,21 @@ def tile_simplepredictor_t_kernel(
             out=factor[:], in0=count[:], scalar=0.0, in1=reciprocal[:], op0=ALU.is_gt, op1=ALU.mult
         )
         turn_rows(scale_columns, [slice(t, HALF, 4) for t in range(4)])
+        widen_w2(0, range(2))
         turn_rows(columns, [slice(256 * g + u, 256 * g + 256, 2) for g in range(2) for u in range(2)])
-        spread_factor(0)
-        spread_factor(1)
+        factor_turned = [turn_factor(0, "out"), turn_factor(1, "turned_hn")]
         b1_turned = turn_vector(ROW_B1, "hidden", 2)
-        b2_turned = turn_vector(ROW_B2, "hidden", 2, 2)
-        widen_w2(0, range(4))
-        copy_factor(0)
-        copy_factor(1)
+        b2_turned = turn_vector(ROW_B2, "hidden", 2, parts=2)
+        widen_w2(0, range(2, 4))
+        for k in range(2):
+            spread_factor(k, factor_turned[k])
         b1_all = spread_b1(b1_turned)
         b2_all = spread_b2(b2_turned)
         widen_w2(1, range(2))
         for q in range(QUARTERS):
             add_pairs(0, q)
             pool_until(0, q)
-            if q == 2:
-                interleave_w2(0, slice(0, D), nc.vector.tensor_copy)
-        gamma_turned = turn_vector(ROW_GAMMA, "gamma", 1)
-        beta_turned = turn_vector(ROW_BETA, "beta", 1)
+        interleave_w2(0, slice(0, D), nc.vector.tensor_copy)
         interleave_w1(0)
         interleave_w1(1)
         widen_w2(1, range(2, 4))
@@ -571,114 +537,136 @@ def tile_simplepredictor_t_kernel(
         give_back("w1")
         multiply_w1(0, (1,))
         for first in (0, 2):
-            for i in range(6, NT):
+            for i in (LAST - 1, LAST):
                 load_rows(i, first, first + 2)
         quantise_w2(0)
 
-        VP = {2: [(5, 1)], 3: [(5, 3)], 4: [(7, 1)], 5: [(7, 3)]}
-        SW = {}
-        VP0 = {}
-        LAG = (2, 3, 4, 5)
-        PA = {}
-        PB = {1: [(3, 1)], 2: [(4, 1)], 3: [(5, 1)], 4: [(6, 1)], 5: [(7, 1)]}
-        PC = {0: [(2, 1)], 1: [(3, 2)], 3: [(5, 2)], 4: [(6, 2)], 5: [(7, 2)]}
-        VS = {}
-        GP = {2: [(5, 0)], 3: [(5, 2)], 4: [(7, 0)], 5: [(7, 2)]}
-        for s in range(LAST):
-            gated = s + 1 in GP
+
+        add_b1(0)
+        gelu(0)
+        mean_of_h(0)
+        pool_until(1, 3)
+        gamma_turned = turn_vector(ROW_GAMMA, "gamma", 1)
+        beta_turned = turn_vector(ROW_BETA, "beta", 1)
+        interleave_w2(1, slice(D // 2, D), nc.vector.tensor_copy)
+        nc.vector.tensor_reduce(out=target_n[:], in_=tmask[:], axis=X, op=ALU.add)
+        squares(0)
+        scale_mean(1)
+        quantise_w2(1)
+        give_back("w2")
+        quantise_mean(1)
+        multiply_w1(1)
+        count_targets()
+        centre(0)
+        pool_until(2, 1)
+        inverse_deviation(0)
+
+        add_b1(1)
+        gelu(1)
+        mean_of_h(1)
+        pool_until(2, 3)
+        normalise(0)
+        transpose_hn(0)
+        interleave_hn(0)
+        squares(1)
+        pool_until(3, 1)
+        scale_mean(2)
+        nc.vector.tensor_copy(out=n_of_row[:], in_=st["n_psum"][:])
+        centre(1)
+        quantise_mean(2)
+        multiply_w1(2)
+        valid_slots()
+        pool_until(3, 2)
+        mask_b2(0)
+        inverse_deviation(1)
+        quantise_hn(0)
+        multiply_w2(0)
+
+        for s in range(2, LAST - 1):
+            ahead, q = s + 3 - s % 2, 2 * (s % 2)
             add_b1(s)
-            for i, r in GP.get(s, ()):
-                add_pairs(i, r, nc.gpsimd, "words%d" % ((s - 2) % 3), 1)
+            add_pairs(ahead, q, nc.gpsimd, words_tag(s - 2), 1)
             gelu(s)
             mean_of_h(s)
             pool_until(s + 1, 3)
-            if s == 0:
-                interleave_w2(1, slice(D // 2, D), nc.vector.tensor_copy)
-                nc.vector.tensor_reduce(out=target_n[:], in_=tmask[:], axis=X, op=ALU.add)
-            if s in GP:
-                squares(s)
-                when(s - 1, normalise)
-                when(s - 1, transpose_hn)
-                when(s - 2, first_slot)
-                when(s - 1, interleave_hn)
-            else:
-                when(s - 2, first_slot)
-                fill_slots(1, "gpsimd")
-                fill_slots(1, "scalar")
-                fill_slots(1, "gpsimd")
-                fill_slots(1, "scalar")
-                when(s - 1, normalise)
-                when(s - 1, transpose_hn)
-                when(s - 1, interleave_hn)
-                squares(s)
-            for i, r in PB.get(s, ()):
-                pool_until(i, r)
+            squares(s)
+            normalise(s - 1)
+            transpose_hn(s - 1)
+            first_slot(s - 2)
+            interleave_hn(s - 1)
+            pool_until(s + 2, 1)
             scale_mean(s + 1)
-            if s == 0:
-                quantise_w2(1)
-                give_back("w2")
-                quantise_mean(1)
-                multiply_w1(1)
-                count_targets()
-            if s == 1:
-                nc.vector.tensor_copy(out=n_of_row[:], in_=st["n_psum"][:])
             centre(s)
-            if s > 0:
-                quantise_mean(s + 1)
-                multiply_w1(s + 1)
-            if s == 1:
-                valid_slots()
-            if s > 1:
-                mask_b2(s - 1)
-            if not gated:
-                when(s - 1, quantise_hn)
-                when(s - 1, multiply_w2)
-            for i, r in PC.get(s, ()):
-                pool_until(i, r)
-            fill_slots(1 if s in VP else 2, "vector")
-            for i, r in VP.get(s, ()):
-                add_pairs(i, r)
-            if s == 1:
-                mask_b2(0)
+            quantise_mean(s + 1)
+            multiply_w1(s + 1)
+            mask_b2(s - 1)
+            last = s == LAST - 2
+            if last:
+                quantise_hn(s - 1)
+                multiply_w2(s - 1)
+            if s > 2:
+                pool_until(s + 2, 2)
+            fill_slots(1, "vector")
+            add_pairs(ahead, q + 1)
             fill_slots(1, "scalar")
             inverse_deviation(s)
-            if gated:
-                when(s - 1, quantise_hn)
-                when(s - 1, multiply_w2)
+            if not last:
+                quantise_hn(s - 1)
+                multiply_w2(s - 1)
             fill_slots(len(waiting), "scalar")
-            for i, r in SW.get(s, ()):
-                widen(i, r)
+
+        s = LAST - 1
+        add_b1(s)
+        gelu(s)
+        mean_of_h(s)
+        pool_until(LAST, 3)
+        first_slot(s - 2)
+        for engine in ("gpsimd", "scalar", "gpsimd", "scalar"):
+            fill_slots(1, engine)
+        normalise(s - 1)
+        transpose_hn(s - 1)
+        interleave_hn(s - 1)
+        squares(s)
+        scale_mean(LAST)
+        centre(s)
+        quantise_mean(LAST)
+        multiply_w1(LAST)
+        mask_b2(s - 1)
+        quantise_hn(s - 1)
+        multiply_w2(s - 1)
+        fill_slots(2, "vector")
+        fill_slots(1, "scalar")
+        inverse_deviation(s)
 
         add_b1(LAST)
         gelu(LAST)
-        mean_of_h(LAST)
         first_slot(LAST - 2)
-        fill_slots(1, "gpsimd")
-        fill_slots(1, "scalar")
-        fill_slots(1, "gpsimd")
+        for engine in ("gpsimd", "scalar", "gpsimd"):
+            fill_slots(1, engine)
+        mean_of_h(LAST)
+        squares(LAST)
         normalise(LAST - 1)
         transpose_hn(LAST - 1)
-        squares(LAST)
+        inverse_deviation(LAST)
         interleave_hn(LAST - 1)
         centre(LAST)
-        inverse_deviation(LAST)
         mask_b2(LAST - 1)
         fill_slots(2, "vector")
         quantise_hn(LAST - 1)
         multiply_w2(LAST - 1)
-        fill_slots(1, "scalar")
-        fill_slots(1, "vector")
+        fill_slots(len(waiting), "scalar")
         normalise(LAST)
         transpose_hn(LAST)
         first_slot(LAST - 1)
         mask_b2(LAST)
+        fill_slots(2, "vector")
         fill_slots(1, "scalar")
         interleave_hn(LAST)
-        fill_slots(4, "vector")
+        fill_slots(1, "vector")
         quantise_hn(LAST)
         multiply_w2(LAST)
         fill_slots(1, "scalar")
-        fill_slots(1, "vector")
+        fill_slots(len(waiting), "vector")
         first_slot(LAST)
         while waiting:
             fill_slots(2, "vector")

@@ -23,14 +23,16 @@ FIRST_BY_HALVES = 2
 
 FIRST_STORED_IN_HALVES = 4
 
+LAST_PARTS = (0, T // 2, T)
+
 BIG_BUFFERS = 8
 
 PAIR_BUFFERS = 4
 
 WORD_BUFFERS = 3
 
-ROW_B1, ROW_GAMMA, ROW_BETA, ROW_B2 = 2, 3, 4, 5
-VECTOR_ROWS = 6
+ROW_B1, ROW_GAMMA, ROW_BETA, ROW_B2 = 0, 1, 2, 3
+VECTOR_ROWS = 4
 
 F32 = mybir.dt.float32
 BF16 = mybir.dt.bfloat16
@@ -78,8 +80,10 @@ def tile_simplepredictor_t_kernel(
             free.append(held[key])
 
         cmask = keep.tile([P, 8, L], BF16)
-        nc.scalar.dma_start(out=cmask[:], in_=context_mask.rearrange("(p i) l -> p i l", i=8))
-        vectors = keep.tile([P, HALF], F32)
+        nc.sync.dma_start(out=cmask[:], in_=context_mask.rearrange("(p i) l -> p i l", i=8))
+        scale_rows = keep.tile([P, HALF], F32)
+        nc.vector.memset(scale_rows[:], 0.0)
+        vectors = keep.tile([P, HALF // 2], F32)
         nc.vector.memset(vectors[:], 0.0)
 
         rows = context_repr.rearrange("b l d -> (b l) d")
@@ -88,59 +92,52 @@ def tile_simplepredictor_t_kernel(
         def quarters(i, q, n):
             return ctx[i][:, 4 * D * q : 4 * D * (q + n)]
 
-        def load_rows(i, first=0, end=QUARTERS):
-            if first == 0:
+        def load_rows(i, first, end):
+            if i not in ctx:
                 ctx[i] = big_tile(L * D, BF16, "ctx", ("ctx", i))
-            q = first
-            while q < end:
-                alike = i in WHOLE or rows_per_partition(i, q) == rows_per_partition(i, q + 1)
-                n = 2 if i >= FIRST_BY_HALVES and q % 2 == 0 and q + 2 <= end and alike else 1
-                if i in WHOLE:
-                    src = context_repr[P * i : P * i + P].rearrange("b l d -> b (l d)")
-                    nc.sync.dma_start(out=quarters(i, q, n), in_=src[:, 4 * D * q : 4 * D * (q + n)])
-                else:
-                    r = rows_per_partition(i, q)
-                    row0 = 512 * (QUARTERS * i + q)
-                    nc.sync.dma_start(
-                        out=quarters(i, q, n).rearrange("p (c x) -> p c x", x=r * D),
-                        in_=rows[row0 : row0 + 512 * n, :].rearrange("(c p r) d -> p c (r d)", p=P, r=r),
-                    )
-                q = q + n
+            if i in WHOLE:
+                src = context_repr[P * i : P * i + P].rearrange("b l d -> b (l d)")
+                nc.sync.dma_start(out=ctx[i][:, D * first : D * end], in_=src[:, D * first : D * end])
+            else:
+                n = end - first
+                r = rows_per_partition(i, first)
+                assert all(rows_per_partition(i, q) == r for q in range(first, end))
+                row0 = 512 * (QUARTERS * i + first)
+                nc.sync.dma_start(
+                    out=quarters(i, first, n).rearrange("p (c x) -> p c x", x=r * D),
+                    in_=rows[row0 : row0 + 512 * n, :].rearrange("(c p r) d -> p c (r d)", p=P, r=r),
+                )
 
-        load_rows(0, 0, 1)
-        nc.sync.dma_start(out=vectors[0:2, :], in_=W2_scale.rearrange("(g k) o -> g (k o)", g=2))
-        for row, vec in enumerate((b1, gamma, beta, b2), ROW_B1):
-            nc.sync.dma_start(
-                out=vectors[row : row + 1, :].bitcast(BF16)[:, : vec.shape[0]], in_=vec.rearrange("(o f) -> o f", o=1)
-            )
+        load_rows(0, 0, 4)
         w2_bytes = keep.tile([P, 2, 4, D], U8)
         nc.sync.dma_start(
             out=w2_bytes[:].rearrange("p g t n -> p g (t n)"), in_=W2_bytes.rearrange("(g p t) n -> p g (t n)", g=2, t=4)
         )
-        load_rows(0, 1, QUARTERS)
+        nc.sync.dma_start(out=scale_rows[0 : P : P // 2, :], in_=W2_scale.rearrange("(g k) o -> g (k o)", g=2))
+        load_rows(0, 4, 8)
+        load_rows(0, 8, 12)
+        load_rows(0, 12, 16)
         w1_stage = big_tile(8 * F, BF16, "w1_stage", "w1")
         w1_rows = w1_stage[:, : 4 * F].rearrange("p (t c) -> p t c", t=4)
         nc.sync.dma_start(out=w1_rows, in_=W1.rearrange("(p t) c -> p t c", t=4))
-        load_rows(1)
+        for row, vec in enumerate((b1, gamma, beta)):
+            nc.sync.dma_start(out=vectors[row : P : P // 2, :].bitcast(BF16), in_=vec.rearrange("(g f) -> g f", g=2))
+        nc.sync.dma_start(out=vectors[ROW_B2 : ROW_B2 + 1, :].bitcast(BF16), in_=b2.rearrange("(o f) -> o f", o=1))
+        load_rows(1, 0, 2)
+        load_rows(1, 2, 4)
         tmask = keep.tile([P, 8, L], BF16)
         nc.sync.dma_start(out=tmask[:], in_=target_mask.rearrange("(p i) l -> p i l", i=8))
-        load_rows(2)
-        load_rows(3)
-        load_rows(5, 0, 2)
-        load_rows(4, 0, 2)
-        load_rows(5, 2, 3)
-        load_rows(4, 2)
-        load_rows(5, 3)
+        for i, first, end in ((2, 0, 1), (5, 0, 4), (2, 1, 2), (2, 2, 4), (5, 4, 8), (3, 0, 2), (3, 2, 4), (5, 8, 16), (4, 0, 2), (4, 2, 4)):
+            load_rows(i, first, end)
         w2_stage = big_tile(16 * D, BF16, "w2_stage", "w2")
 
         ident_f32 = keep.tile([P, P], F32)
         make_identity(nc, ident_f32[:])
         minus_half = keep.tile([P, 1], F32)
-        nc.gpsimd.memset(minus_half[:], -0.5)
+        nc.vector.memset(minus_half[:], -0.5)
         slot_index = keep.tile([P, T], F32)
-        nc.gpsimd.iota(
-            slot_index[:], pattern=[[1, T]], base=0, channel_multiplier=0, allow_small_or_imprecise_dtypes=True
-        )
+        for j in range(T):
+            nc.vector.memset(slot_index[:, j : j + 1], float(j))
 
         def selection(r):
             sel_f32 = keep.tile([P, 8 * r], F32, name="selection%d_f32" % r)
@@ -150,9 +147,17 @@ def tile_simplepredictor_t_kernel(
             )
             return sel_f32, sel
 
-        pooling = {r: selection(r) for r in (1, 2, 4)}
+        pooling = {}
         mod16 = keep.tile([P, 16], F32)
-        nc.vector.tensor_reduce(out=mod16[:], in_=ident_f32[:].rearrange("p (j q) -> p q j", q=16), axis=X, op=ALU.add)
+
+        def make_selections():
+            for r in (1, 2, 4):
+                pooling[r] = selection(r)
+            nc.vector.tensor_reduce(
+                out=mod16[:], in_=ident_f32[:].rearrange("p (j q) -> p q j", q=16), axis=X, op=ALU.add
+            )
+            for r in (1, 2, 4):
+                nc.vector.tensor_copy(out=pooling[r][1][:], in_=pooling[r][0][:])
 
         count = keep.tile([P, 8], F32)
         count_or_1 = keep.tile([P, 8], F32)
@@ -174,22 +179,27 @@ def tile_simplepredictor_t_kernel(
             )
 
         scale_columns = keep.tile([P, 2, 4], F32)
-        columns = keep.tile([P, VECTOR_ROWS, 4], F32)
+        columns = keep.tile([P, VECTOR_ROWS, 2, 2], F32)
 
-        def turn_rows(dst, picks):
-            turned = psum.tile([P, 4, P], F32, tag="hidden", name="turned")
-            for c, pick in enumerate(picks):
-                nc.tensor.transpose(turned[:, c, :], vectors[:, pick], ident_f32[:])
-            nc.scalar.copy(out=dst[:], in_=turned[:, :, : dst.shape[1]].rearrange("p c row -> p row c"))
+        def turn_rows(src, step, width):
+            turned = psum.tile([P, step, P], F32, tag="hidden", name="turned")
+            for c in range(step):
+                nc.tensor.transpose(turned[:, c, :], src[:, c : width : step], ident_f32[:])
+            return turned[:].rearrange("p c (g row) -> p row g c", g=2)
 
-        def turn_vector(row, tag, bufs, parts=4):
-            turned = psum.tile([P, parts, P], F32, tag=tag, bufs=bufs, name="turned")
-            for c in range(parts):
-                nc.tensor.transpose(turned[:, c, :], columns[:, row, c : c + 1].to_broadcast([P, P]), ident_f32[:])
+        def keep_columns(dst, turned):
+            nc.scalar.copy(out=dst, in_=turned)
+
+        def turn_vector(row, tag, bufs, halves=2):
+            turned = psum.tile([P, halves, 2, P], F32, tag=tag, bufs=bufs, name="turned")
+            for g in range(halves):
+                for u in range(2):
+                    column = columns[:, row, g, u : u + 1]
+                    nc.tensor.transpose(turned[:, g, u, :], column.to_broadcast([P, P]), ident_f32[:])
             return turned
 
         def as_entries(turned):
-            return turned[:].rearrange("p c m -> p (c m)").bitcast(BF16)
+            return turned[:].rearrange("p g u m -> p (g u m)").bitcast(BF16)
 
         w1_codes = keep.tile([P, F], U32, align_bytes=64)
         w1_planes = keep.tile([P, F], U8, align_bytes=64)
@@ -197,10 +207,10 @@ def tile_simplepredictor_t_kernel(
             w1_stage[:, 4 * HALF * (2 + g) : 4 * HALF * (3 + g)].rearrange("p (c t) -> p c t", t=4) for g in range(2)
         ]
 
-        def interleave_w1(g):
+        def interleave_w1(g, blocks):
             copy = (nc.vector.tensor_copy, nc.scalar.copy)[g]
             src = w1_rows[:, :, HALF * g : HALF * g + HALF].rearrange("p t (m u e) -> p u m e t", u=2, e=2)
-            for u in range(2):
+            for u in blocks:
                 copy(out=w1_words[g][:, hidden_block(0, u), :].rearrange("p (m e) t -> p m e t", e=2), in_=src[:, u])
 
         def quantise_w1(g):
@@ -231,6 +241,9 @@ def tile_simplepredictor_t_kernel(
                 in_=w2_rows[:, g, :, cols].rearrange("p t (c i) -> p c t i", i=4),
             )
 
+        def gpsimd_copy(out, in_):
+            nc.gpsimd.tensor_scalar(out=out, in0=in_, scalar1=1.0, scalar2=0.0, op0=ALU.mult, op1=ALU.add)
+
         def quantise_w2(g):
             nc.vector.quantize_mx(
                 out=w2_codes[:, g, :].bitcast(FP8X4),
@@ -240,10 +253,12 @@ def tile_simplepredictor_t_kernel(
 
         st = {}
         pooled = [0] * NT
+        added = [0] * NT
+        groups = [[] for i in range(NT)]
 
         def pool(i, q):
             if q == 0:
-                st["sums", i] = psum.tile([P, P, 4], F32, tag="pool", name="sums")
+                st["sums", i] = psum.tile([P, P, 4], F32, tag="pool%d" % (i % 2), bufs=1, name="sums")
             r = rows_per_partition(i, q)
             width = 8 * r
             x = quarters(i, q, 1).rearrange("p (c x) -> p c x", x=r * D)
@@ -261,30 +276,44 @@ def tile_simplepredictor_t_kernel(
             if q == QUARTERS - 1:
                 give_back(("ctx", i))
 
-        def add_pairs(i, q, engine=nc.vector, tag="pairs", bufs=PAIR_BUFFERS):
-            pairs = work.tile([P, F], F32, tag=tag, bufs=bufs, align_bytes=64, name="pairs")
-            x = quarters(i, q, 1).rearrange("b (h c n t) -> b h c t n", h=2, n=4, t=4)
+        def add_pairs(i, n, engine=nc.vector, tag="pairs", bufs=PAIR_BUFFERS):
+            l0 = added[i]
+            added[i] += 2 * n
+            pairs = work.tile([P, n * D], F32, tag=tag, bufs=bufs, align_bytes=64, name="pairs")
+            x = ctx[i][:, D * l0 : D * added[i]].rearrange("b (h c k t) -> b h c t k", h=2, k=4, t=4)
             engine.tensor_tensor(
-                out=pairs[:].rearrange("b (t c n) -> b c t n", t=4, n=4), in0=x[:, 0], in1=x[:, 1], op=ALU.add
+                out=pairs[:].rearrange("b (t c k) -> b c t k", t=4, k=4), in0=x[:, 0], in1=x[:, 1], op=ALU.add
             )
-            st["pairs", i, q] = pairs
-            if q == QUARTERS - 1:
+            groups[i].append((pairs, n, l0 == 0, added[i] == L))
+            if added[i] == L:
                 give_back(("ctx", i))
 
         def pool_whole(i, q):
-            if q == 0:
-                st["sums", i] = psum.tile([P, 4, P], F32, tag="pool", name="sums")
+            pairs, n, first, last = groups[i][q]
+            if first:
+                st["sums", i] = psum.tile([P, 4, P], F32, tag="pool%d" % (i % 2), bufs=1, name="sums")
             for t in range(4):
-                for j in range(2):
-                    w0 = 2 * P * t + P * j
+                for j in range(n):
+                    w0 = P * (n * t + j)
                     nc.tensor.matmul(
                         out=st["sums", i][:, t, :],
-                        lhsT=st["pairs", i, q][:, w0 : w0 + P],
+                        lhsT=pairs[:, w0 : w0 + P],
                         rhs=ident_f32[:],
                         is_transpose=True,
-                        start=(q, t, j) == (0, 0, 0),
-                        stop=(q, t, j) == (QUARTERS - 1, 3, 1),
+                        start=first and (t, j) == (0, 0),
+                        stop=last and (t, j) == (3, n - 1),
                     )
+
+        def add_next(number, engine=nc.vector, tag="pairs", bufs=PAIR_BUFFERS):
+            for i in WHOLE:
+                n = min(number, (L - added[i]) // 2)
+                if n:
+                    add_pairs(i, n, engine, tag, bufs)
+                    number = number - n
+                    tag, bufs = "pairs", PAIR_BUFFERS
+
+        def pool_ready(i):
+            pool_until(i, len(groups[i]) - 1 if i in WHOLE else QUARTERS - 1)
 
         def pool_until(i, last):
             while pooled[i] <= last:
@@ -356,8 +385,8 @@ def tile_simplepredictor_t_kernel(
 
         def inverse_deviation(i):
             var_eps = work.tile([P, 1], F32, tag="var_eps", name="var_eps")
-            nc.scalar.activation(
-                out=var_eps[:], in_=st["scaled_var", i][:], func=ACT.Copy, scale=1.0 / F**3, bias=LN_EPS
+            nc.vector.tensor_scalar(
+                out=var_eps[:], in0=st["scaled_var", i][:], scalar1=1.0 / F**3, scalar2=LN_EPS, op0=ALU.mult, op1=ALU.add
             )
             rstd = work.tile([P, 1], F32, tag="rstd", name="rstd")
             nc.gpsimd.tensor_tensor(out=rstd[:], in0=var_eps[:], in1=minus_half[:], op=ALU.pow)
@@ -375,57 +404,65 @@ def tile_simplepredictor_t_kernel(
             )
             st["centred", i] = centred
 
-        def normalise(i):
-            hn = work.tile([P, F], BF16, tag="hn", name="hn")
+        def normalise(i, passes=(0, 1)):
+            if passes[0] == 0:
+                st["hn", i] = work.tile([P, F], BF16, tag="hn", name="hn")
+            cols = slice(HALF * passes[0], HALF * passes[-1] + HALF)
             nc.vector.scalar_tensor_tensor(
-                out=hn[:], in0=st["centred", i][:], scalar=st["rstd", i][:], in1=as_entries(beta_turned), op0=ALU.mult, op1=ALU.add
+                out=st["hn", i][:, cols],
+                in0=st["centred", i][:, cols],
+                scalar=st["rstd", i][:],
+                in1=as_entries(beta_turned)[:, cols],
+                op0=ALU.mult,
+                op1=ALU.add,
             )
-            st["hn", i] = hn
 
-        def transpose_hn(i):
-            turned = psum.tile([P, 2, 2, P], F32, tag="turned_hn", bufs=1, name="turned_hn")
+        def transpose_hn(i, passes=(0, 1), tag="turned_hn"):
+            turned = psum.tile([P, len(passes), 2, P], F32, tag=tag, bufs=1, name="turned_hn")
             words = st["hn", i][:].bitcast(F32)
-            for g in range(2):
+            for k, g in enumerate(passes):
                 for u in range(2):
                     w0 = 256 * g + 128 * u
-                    nc.tensor.transpose(turned[:, g, u, :], words[:, w0 : w0 + 128], ident_f32[:])
-            st["turned_hn", i] = turned
+                    nc.tensor.transpose(turned[:, k, u, :], words[:, w0 : w0 + 128], ident_f32[:])
+            st["turned_hn", i, passes] = turned
 
-        def words_tag(i):
-            return "words%d" % (i % WORD_BUFFERS)
-
-        def interleave_hn(i):
-            hn_words = work.tile([P, 2 * P * 4], BF16, align_bytes=64, tag=words_tag(i), bufs=1, name="hn_words")
+        def interleave_hn(i, passes=(0, 1)):
+            hn_words = work.tile([P, len(passes) * P * 4], BF16, align_bytes=64, tag="hn_words", name="hn_words")
             nc.scalar.copy(
-                out=hn_words[:].bitcast(F32).rearrange("p (g b u) -> p g b u", g=2, u=2),
-                in_=st["turned_hn", i][:].rearrange("p g u b -> p g b u"),
+                out=hn_words[:].bitcast(F32).rearrange("p (g b u) -> p g b u", b=P, u=2),
+                in_=st["turned_hn", i, passes][:].rearrange("p g u b -> p g b u"),
             )
-            st["hn_words", i] = hn_words
+            st["hn_words", i, passes] = hn_words
 
-        def quantise_hn(i):
-            codes = work.tile([P, 2 * P], U32, align_bytes=64, tag="hn_codes", name="hn_codes")
-            plane = work.tile([P, 2 * P], U8, align_bytes=64, tag="hn_plane", name="hn_plane")
-            nc.vector.quantize_mx(out=codes[:].bitcast(FP8X4), scales=plane[:], in_=st["hn_words", i][:])
-            st["hn_codes", i], st["hn_plane", i] = codes, plane
+        def quantise_hn(i, passes=(0, 1)):
+            codes = work.tile([P, len(passes) * P], U32, align_bytes=64, tag="hn_codes", name="hn_codes")
+            plane = work.tile([P, len(passes) * P], U8, align_bytes=64, tag="hn_plane", name="hn_plane")
+            nc.vector.quantize_mx(out=codes[:].bitcast(FP8X4), scales=plane[:], in_=st["hn_words", i, passes][:])
+            st["hn_codes", i, passes], st["hn_plane", i, passes] = codes, plane
 
-        def multiply_w2(i):
-            acc = psum.tile([P, D], F32, tag="out", bufs=1, name="acc2")
-            for g in range(2):
-                part = slice(P * g, P * g + P)
+        def multiply_w2(i, passes=(0, 1)):
+            if passes[0] == 0:
+                st["acc2", i] = psum.tile([P, D], F32, tag="out", bufs=1, name="acc2")
+            for k, g in enumerate(passes):
+                part = slice(P * k, P * k + P)
                 nc.tensor.matmul_mx(
-                    out=acc[:],
-                    lhsT=st["hn_codes", i][:, part].bitcast(FP8X4),
-                    lhsT_scale=st["hn_plane", i][:, part],
+                    out=st["acc2", i][:],
+                    lhsT=st["hn_codes", i, passes][:, part].bitcast(FP8X4),
+                    lhsT_scale=st["hn_plane", i, passes][:, part],
                     rhs=w2_codes[:, g, :].bitcast(FP8X4),
                     rhs_scale=w2_planes[:, g, :],
                     start=(g == 0),
                     stop=(g == 1),
                 )
-            st["acc2", i] = acc
 
-        def mask_b2(i):
-            masked = work.tile([P, D], BF16, tag="b2_masked", name="b2_masked")
-            nc.vector.tensor_scalar_mul(masked[:], b2_all[:], valid[:, i, 0:1])
+        def mask_b2(i, engine="vector"):
+            if ("b2_masked", i) in st:
+                return
+            masked = keep.tile([P, D], BF16, name="b2_masked%d" % i)
+            if engine == "vector":
+                nc.vector.tensor_scalar_mul(masked[:], b2_all[:], valid[:, i, 0:1])
+            else:
+                nc.scalar.activation(out=masked[:], in_=b2_all[:], func=ACT.Copy, scale=valid[:, i, 0:1])
             st["b2_masked", i] = masked
 
         waiting = []
@@ -440,7 +477,16 @@ def tile_simplepredictor_t_kernel(
                 op0=ALU.mult,
                 op1=ALU.add,
             )
+            store_slots(i, 1)
             waiting.extend((i, j) for j in range(1, T))
+
+        def store_slots(i, end):
+            ends = (0, T) if i < FIRST_STORED_IN_HALVES else (0, T // 2, T) if i < LAST else LAST_PARTS
+            if end in ends:
+                cols = slice(D * ends[ends.index(end) - 1], D * end)
+                nc.sync.dma_start(
+                    out=out[P * i : P * i + P].rearrange("b j d -> b (j d)")[:, cols], in_=st["slots", i][:, cols]
+                )
 
         def fill_slots(number, engine):
             for i, j in waiting[:number]:
@@ -454,16 +500,10 @@ def tile_simplepredictor_t_kernel(
                     nc.gpsimd.tensor_scalar(out=dst, in0=src, scalar1=mask, scalar2=0.0, op0=ALU.mult, op1=ALU.add)
                 else:
                     nc.scalar.activation(out=dst, in_=src, func=ACT.Copy, scale=mask)
-                together = T if i < FIRST_STORED_IN_HALVES else T // 2
-                if (j + 1) % together == 0:
-                    cols = slice(D * (j + 1 - together), D * (j + 1))
-                    nc.sync.dma_start(
-                        out=out[P * i : P * i + P].rearrange("b j d -> b (j d)")[:, cols], in_=st["slots", i][:, cols]
-                    )
+                store_slots(i, j + 1)
 
         target_n = keep.tile([P, 8], F32)
         picked = keep.tile([P, 16, 8], BF16)
-        n_of_row = keep.tile([P, NT], F32)
         valid = keep.tile([P, NT, T], F32)
 
         def count_targets():
@@ -473,7 +513,7 @@ def tile_simplepredictor_t_kernel(
                 in1=mod16[:].unsqueeze(2).to_broadcast([P, 16, 8]),
                 op=ALU.mult,
             )
-            n_psum = psum.tile([P, NT], F32, tag="out", bufs=1, name="n_psum")
+            n_psum = psum.tile([P, NT], F32, tag="beta", bufs=1, name="n_psum")
             nc.tensor.matmul(
                 out=n_psum[:], lhsT=picked[:].rearrange("p q i -> p (q i)"), rhs=pooling[1][1][:], start=True, stop=True
             )
@@ -481,13 +521,13 @@ def tile_simplepredictor_t_kernel(
 
         def spread_b1(turned):
             dst = keep.tile([P, F], BF16, name="b1_all")
-            nc.scalar.copy(out=dst[:].bitcast(F32), in_=turned[:].rearrange("p c m -> p (c m)"))
+            nc.scalar.copy(out=dst[:].bitcast(F32), in_=turned[:].rearrange("p g u m -> p (g u m)"))
             return dst
 
         def spread_b2(turned):
             dst = keep.tile([P, D], BF16, name="b2_all")
             nc.scalar.copy(
-                out=dst[:].bitcast(F32).rearrange("p (m u) -> p m u", u=2), in_=turned[:].rearrange("p u m -> p m u")
+                out=dst[:].bitcast(F32).rearrange("p (m u) -> p m u", u=2), in_=turned[:, 0].rearrange("p u m -> p m u")
             )
             return dst
 
@@ -495,178 +535,187 @@ def tile_simplepredictor_t_kernel(
             nc.vector.tensor_tensor(
                 out=valid[:],
                 in0=slot_index[:].unsqueeze(1).to_broadcast([P, NT, T]),
-                in1=n_of_row[:].unsqueeze(2).to_broadcast([P, NT, T]),
+                in1=st["n_psum"][:].unsqueeze(2).to_broadcast([P, NT, T]),
                 op=ALU.is_lt,
             )
 
         nc.vector.tensor_reduce(out=count[:], in_=cmask[:], axis=X, op=ALU.add)
-        nc.vector.tensor_copy(out=pooling[2][1][:], in_=pooling[2][0][:])
         nc.vector.tensor_scalar_max(count_or_1[:], count[:], 1.0)
-        nc.vector.tensor_copy(out=pooling[4][1][:], in_=pooling[4][0][:])
         nc.vector.reciprocal(reciprocal[:], count_or_1[:])
-        nc.vector.tensor_copy(out=pooling[1][1][:], in_=pooling[1][0][:])
         nc.vector.scalar_tensor_tensor(
             out=factor[:], in0=count[:], scalar=0.0, in1=reciprocal[:], op0=ALU.is_gt, op1=ALU.mult
         )
-        turn_rows(scale_columns, [slice(t, HALF, 4) for t in range(4)])
-        widen_w2(0, range(2))
-        turn_rows(columns, [slice(256 * g + u, 256 * g + 256, 2) for g in range(2) for u in range(2)])
         factor_turned = [turn_factor(0, "out"), turn_factor(1, "turned_hn")]
-        b1_turned = turn_vector(ROW_B1, "hidden", 2)
-        b2_turned = turn_vector(ROW_B2, "hidden", 2, parts=2)
-        widen_w2(0, range(2, 4))
+        scales_turned = turn_rows(scale_rows, 4, HALF)
         for k in range(2):
             spread_factor(k, factor_turned[k])
+        keep_columns(scale_columns[:], scales_turned[:, 0])
+        widen_w2(0, range(4))
+        widen_w2(1, range(3))
+        add_pairs(0, 2)
+        pool_ready(0)
+        make_selections()
+        for q in range(1, QUARTERS):
+            add_pairs(0, 2)
+            pool_ready(0)
+        vectors_turned = turn_rows(vectors, 2, HALF // 2)
+        interleave_w2(0, slice(0, D // 2), nc.vector.tensor_copy)
+        interleave_w1(0, (0, 1))
+        interleave_w1(1, (0,))
+        keep_columns(columns[:], vectors_turned[:, :VECTOR_ROWS])
+        interleave_w1(1, (1,))
+        b1_turned = turn_vector(ROW_B1, "hidden", 2)
         b1_all = spread_b1(b1_turned)
-        b2_all = spread_b2(b2_turned)
-        widen_w2(1, range(2))
-        for q in range(QUARTERS):
-            add_pairs(0, q)
-            pool_until(0, q)
-        interleave_w2(0, slice(0, D), nc.vector.tensor_copy)
-        interleave_w1(0)
-        interleave_w1(1)
-        widen_w2(1, range(2, 4))
-        interleave_w2(1, slice(0, D // 2), nc.scalar.copy)
         scale_mean(0)
         quantise_w1(0)
         quantise_mean(0)
-        pool_until(1, 1)
+        pool_until(1, 0)
         multiply_w1(0, (0,))
         quantise_w1(1)
         give_back("w1")
         multiply_w1(0, (1,))
-        for first in (0, 2):
-            for i in (LAST - 1, LAST):
-                load_rows(i, first, first + 2)
-        quantise_w2(0)
-
+        for i, first, end in ((7, 0, 16), (6, 0, 4)):
+            load_rows(i, first, end)
 
         add_b1(0)
         gelu(0)
         mean_of_h(0)
         pool_until(1, 3)
         gamma_turned = turn_vector(ROW_GAMMA, "gamma", 1)
-        beta_turned = turn_vector(ROW_BETA, "beta", 1)
-        interleave_w2(1, slice(D // 2, D), nc.vector.tensor_copy)
-        nc.vector.tensor_reduce(out=target_n[:], in_=tmask[:], axis=X, op=ALU.add)
+        b2_turned = turn_vector(ROW_B2, "out", 1, halves=1)
         squares(0)
+        interleave_w2(0, slice(D // 2, D), nc.vector.tensor_copy)
+        nc.vector.tensor_reduce(out=target_n[:], in_=tmask[:], axis=X, op=ALU.add)
+        quantise_w2(0)
         scale_mean(1)
-        quantise_w2(1)
-        give_back("w2")
+        count_targets()
         quantise_mean(1)
         multiply_w1(1)
-        count_targets()
         centre(0)
+        valid_slots()
+        beta_turned = turn_vector(ROW_BETA, "beta", 1)
         pool_until(2, 1)
+        b2_all = spread_b2(b2_turned)
+        widen_w2(1, range(3, 4))
+        interleave_w2(1, slice(0, D // 2), nc.scalar.copy)
         inverse_deviation(0)
 
         add_b1(1)
+        add_next(2, nc.gpsimd, "shared", 3)
         gelu(1)
         mean_of_h(1)
-        pool_until(2, 3)
+        pool_until(2, 2)
         normalise(0)
         transpose_hn(0)
+        pool_until(2, 3)
+        interleave_w2(1, slice(D // 2, D), nc.scalar.copy)
         interleave_hn(0)
         squares(1)
-        pool_until(3, 1)
-        scale_mean(2)
-        nc.vector.tensor_copy(out=n_of_row[:], in_=st["n_psum"][:])
+        for i in range(3):
+            mask_b2(i, "scalar")
         centre(1)
+        scale_mean(2)
         quantise_mean(2)
         multiply_w1(2)
-        valid_slots()
-        pool_until(3, 2)
-        mask_b2(0)
-        inverse_deviation(1)
         quantise_hn(0)
+        quantise_w2(1)
+        give_back("w2")
         multiply_w2(0)
+        pool_until(3, 1)
+        inverse_deviation(1)
 
-        for s in range(2, LAST - 1):
-            ahead, q = s + 3 - s % 2, 2 * (s % 2)
+        def open_step(s, pairs):
             add_b1(s)
-            add_pairs(ahead, q, nc.gpsimd, words_tag(s - 2), 1)
+            add_next(pairs, nc.gpsimd, "shared", 3)
             gelu(s)
             mean_of_h(s)
-            pool_until(s + 1, 3)
-            squares(s)
+            if s + 1 not in WHOLE:
+                pool_ready(s + 1)
             normalise(s - 1)
             transpose_hn(s - 1)
+            squares(s)
             first_slot(s - 2)
             interleave_hn(s - 1)
-            pool_until(s + 2, 1)
-            scale_mean(s + 1)
+            pool_ready(s + 1)
+            if s + 2 in WHOLE:
+                pool_until(s + 2, 1)
+            elif 2 < s < LAST - 1:
+                pool_until(s + 2, 1)
             centre(s)
+            scale_mean(s + 1)
+
+        for s in range(2, LAST - 1):
+            open_step(s, 2)
+            fill_slots(1, "vector")
             quantise_mean(s + 1)
             multiply_w1(s + 1)
             mask_b2(s - 1)
-            last = s == LAST - 2
-            if last:
-                quantise_hn(s - 1)
-                multiply_w2(s - 1)
-            if s > 2:
-                pool_until(s + 2, 2)
-            fill_slots(1, "vector")
-            add_pairs(ahead, q + 1)
-            fill_slots(1, "scalar")
+            quantise_hn(s - 1)
+            multiply_w2(s - 1)
+            if s % 2 == 0:
+                fill_slots(1, "vector")
+            add_next(1)
             inverse_deviation(s)
-            if not last:
-                quantise_hn(s - 1)
-                multiply_w2(s - 1)
+            if s + 2 in WHOLE:
+                pool_ready(s + 2)
+            else:
+                pool_until(s + 2, 1 if s == 2 else 2)
             fill_slots(len(waiting), "scalar")
 
         s = LAST - 1
         add_b1(s)
+        add_next(2, nc.gpsimd, "shared", 3)
         gelu(s)
         mean_of_h(s)
-        pool_until(LAST, 3)
-        first_slot(s - 2)
-        for engine in ("gpsimd", "scalar", "gpsimd", "scalar"):
-            fill_slots(1, engine)
         normalise(s - 1)
         transpose_hn(s - 1)
+        first_slot(s - 2)
+        pool_ready(LAST)
         interleave_hn(s - 1)
         squares(s)
-        scale_mean(LAST)
         centre(s)
+        quantise_hn(s - 1)
+        multiply_w2(s - 1)
+        fill_slots(3, "vector")
+        scale_mean(LAST)
+        inverse_deviation(s)
         quantise_mean(LAST)
         multiply_w1(LAST)
         mask_b2(s - 1)
-        quantise_hn(s - 1)
-        multiply_w2(s - 1)
-        fill_slots(2, "vector")
-        fill_slots(1, "scalar")
-        inverse_deviation(s)
+        fill_slots(len(waiting), "scalar")
 
-        add_b1(LAST)
-        gelu(LAST)
         first_slot(LAST - 2)
-        for engine in ("gpsimd", "scalar", "gpsimd"):
-            fill_slots(1, engine)
-        mean_of_h(LAST)
-        squares(LAST)
         normalise(LAST - 1)
         transpose_hn(LAST - 1)
-        inverse_deviation(LAST)
+        add_b1(LAST)
+        for engine in ("gpsimd", "scalar", "gpsimd", "scalar"):
+            fill_slots(1, engine)
         interleave_hn(LAST - 1)
-        centre(LAST)
+        gelu(LAST)
+        mean_of_h(LAST)
+        squares(LAST)
         mask_b2(LAST - 1)
-        fill_slots(2, "vector")
         quantise_hn(LAST - 1)
         multiply_w2(LAST - 1)
-        fill_slots(len(waiting), "scalar")
-        normalise(LAST)
-        transpose_hn(LAST)
+        fill_slots(3, "vector")
+        centre(LAST)
+        inverse_deviation(LAST)
         first_slot(LAST - 1)
-        mask_b2(LAST)
-        fill_slots(2, "vector")
-        fill_slots(1, "scalar")
-        interleave_hn(LAST)
+        mask_b2(LAST, "scalar")
         fill_slots(1, "vector")
-        quantise_hn(LAST)
-        multiply_w2(LAST)
-        fill_slots(1, "scalar")
-        fill_slots(len(waiting), "vector")
+        for g, tag in enumerate(("turned_hn", "pool0")):
+            normalise(LAST, (g,))
+            transpose_hn(LAST, (g,), tag)
+        fill_slots(2, "scalar")
+        for g in range(2):
+            interleave_hn(LAST, (g,))
+        fill_slots(2, "vector")
+        quantise_hn(LAST, (0,))
+        multiply_w2(LAST, (0,))
+        fill_slots(1, "vector")
+        quantise_hn(LAST, (1,))
+        multiply_w2(LAST, (1,))
+        fill_slots(1, "vector")
         first_slot(LAST)
         while waiting:
             fill_slots(2, "vector")

@@ -127,7 +127,7 @@ def tile_simplepredictor_t_kernel(
         load_rows(1, 2, 4)
         tmask = keep.tile([P, 8, L], BF16)
         nc.sync.dma_start(out=tmask[:], in_=target_mask.rearrange("(p i) l -> p i l", i=8))
-        for i, first, end in ((2, 0, 1), (5, 0, 4), (2, 1, 2), (2, 2, 4), (5, 4, 8), (3, 0, 2), (3, 2, 4), (5, 8, 16), (4, 0, 2), (4, 2, 4)):
+        for i, first, end in ((2, 0, 1), (5, 0, 6), (2, 1, 2), (2, 2, 4), (5, 6, 12), (3, 0, 2), (3, 2, 4), (5, 12, 16), (4, 0, 2), (4, 2, 4)):
             load_rows(i, first, end)
         w2_stage = big_tile(16 * D, BF16, "w2_stage", "w2")
 
@@ -601,7 +601,7 @@ def tile_simplepredictor_t_kernel(
         inverse_deviation(0)
 
         add_b1(1)
-        add_next(2, nc.gpsimd, "shared", 3)
+        add_next(3, nc.gpsimd, "shared", 3)
         gelu(1)
         mean_of_h(1)
         pool_until(2, 2)
@@ -638,23 +638,21 @@ def tile_simplepredictor_t_kernel(
             interleave_hn(s - 1)
             pool_ready(s + 1)
             if s + 2 in WHOLE:
-                pool_until(s + 2, 1)
+                pool_until(s + 2, 0)
             elif 2 < s < LAST - 1:
                 pool_until(s + 2, 1)
             centre(s)
             scale_mean(s + 1)
 
         for s in range(2, LAST - 1):
-            open_step(s, 2)
+            open_step(s, 2 if s == 3 else 3)
             fill_slots(1, "vector")
             quantise_mean(s + 1)
             multiply_w1(s + 1)
             mask_b2(s - 1)
             quantise_hn(s - 1)
             multiply_w2(s - 1)
-            if s % 2 == 0:
-                fill_slots(1, "vector")
-            add_next(1)
+            fill_slots(1, "vector")
             inverse_deviation(s)
             if s + 2 in WHOLE:
                 pool_ready(s + 2)

from contextlib import ExitStack

import concourse.mybir as mybir
from concourse.masks import make_identity

B, L, D, T = 1024, 16, 512, 8
F = 2 * D
LN_EPS = 1e-5

FLOPS = 2 * B * D * F + 2 * B * F * D

P = 128
NT = B // P
LAST = NT - 1
HALF = F // 2
QUARTERS = 4

WHOLE = (0, 5, 7)

WIDE_QUARTERS = 5

FIRST_BY_HALVES = 2

FIRST_STORED_IN_HALVES = 4

LAST_PARTS = (0, T // 2, T)

BIG_BUFFERS = 8

PAIR_BUFFERS = 4

WORD_BUFFERS = 3

ROW_B1, ROW_GAMMA, ROW_BETA, ROW_B2 = 0, 1, 2, 3
VECTOR_ROWS = 4

F32 = mybir.dt.float32
BF16 = mybir.dt.bfloat16
U32 = mybir.dt.uint32
U8 = mybir.dt.uint8
FP8 = mybir.dt.float8_e4m3fn
FP8X4 = mybir.dt.float8_e4m3fn_x4
ALU = mybir.AluOpType
ACT = mybir.ActivationFunctionType
X = mybir.AxisListType.X


def rows_per_partition(i, quarter):
    earlier = QUARTERS * len([k for k in range(i) if k not in WHOLE]) + quarter
    return 4 if earlier < WIDE_QUARTERS else 2


def hidden_block(g, u):
    c0 = HALF * g + 256 * u
    return slice(c0, c0 + 256)


def tile_simplepredictor_t_kernel(
    tc, context_repr, target_mask, context_mask, W1, b1, gamma, beta, W2_bytes, W2_scale, b2, num_targets, out
):
    nc = tc.nc
    assert num_targets == T
    with ExitStack() as es:
        keep = es.enter_context(tc.tile_pool(name="keep", bufs=1))
        big = es.enter_context(tc.tile_pool(name="big", bufs=1))
        work = es.enter_context(tc.tile_pool(name="work", bufs=2))
        psum = es.enter_context(tc.psum_pool(name="psum", bufs=2))

        es.enter_context(tc.manual_schedule())

        free = list(range(BIG_BUFFERS))
        held = {}

        def big_tile(width, dtype, name, key):
            held[key] = free[0]
            free.remove(held[key])
            return big.tile([P, width], dtype, tag="big%d" % held[key], align_bytes=64, name=name)

        def give_back(key):
            free.append(held[key])

        cmask = keep.tile([P, 8, L], BF16)
        nc.sync.dma_start(out=cmask[:], in_=context_mask.rearrange("(p i) l -> p i l", i=8))
        scale_rows = keep.tile([P, HALF], F32)
        nc.vector.memset(scale_rows[:], 0.0)
        vectors = keep.tile([P, HALF // 2], F32)
        nc.vector.memset(vectors[:], 0.0)

        rows = context_repr.rearrange("b l d -> (b l) d")
        ctx = {}

        def quarters(i, q, n):
            return ctx[i][:, 4 * D * q : 4 * D * (q + n)]

        def load_rows(i, first, end):
            if i not in ctx:
                ctx[i] = big_tile(L * D, BF16, "ctx", ("ctx", i))
            if i in WHOLE:
                src = context_repr[P * i : P * i + P].rearrange("b l d -> b (l d)")
                nc.sync.dma_start(out=ctx[i][:, D * first : D * end], in_=src[:, D * first : D * end])
            else:
                n = end - first
                r = rows_per_partition(i, first)
                assert all(rows_per_partition(i, q) == r for q in range(first, end))
                row0 = 512 * (QUARTERS * i + first)
                nc.sync.dma_start(
                    out=quarters(i, first, n).rearrange("p (c x) -> p c x", x=r * D),
                    in_=rows[row0 : row0 + 512 * n, :].rearrange("(c p r) d -> p c (r d)", p=P, r=r),
                )

        load_rows(0, 0, 4)
        w2_bytes = keep.tile([P, 2, 4, D], U8)
        nc.sync.dma_start(
            out=w2_bytes[:].rearrange("p g t n -> p g (t n)"), in_=W2_bytes.rearrange("(g p t) n -> p g (t n)", g=2, t=4)
        )
        nc.sync.dma_start(out=scale_rows[0 : P : P // 2, :], in_=W2_scale.rearrange("(g k) o -> g (k o)", g=2))
        load_rows(0, 4, 8)
        load_rows(0, 8, 12)
        load_rows(0, 12, 16)
        w1_stage = big_tile(8 * F, BF16, "w1_stage", "w1")
        w1_rows = w1_stage[:, : 4 * F].rearrange("p (t c) -> p t c", t=4)
        nc.sync.dma_start(out=w1_rows, in_=W1.rearrange("(p t) c -> p t c", t=4))
        for row, vec in enumerate((b1, gamma, beta)):
            nc.sync.dma_start(out=vectors[row : P : P // 2, :].bitcast(BF16), in_=vec.rearrange("(g f) -> g f", g=2))
        nc.sync.dma_start(out=vectors[ROW_B2 : ROW_B2 + 1, :].bitcast(BF16), in_=b2.rearrange("(o f) -> o f", o=1))
        load_rows(1, 0, 2)
        load_rows(1, 2, 4)
        tmask = keep.tile([P, 8, L], BF16)
        nc.sync.dma_start(out=tmask[:], in_=target_mask.rearrange("(p i) l -> p i l", i=8))
        for i, first, end in ((2, 0, 1), (5, 0, 6), (2, 1, 2), (2, 2, 4), (5, 6, 12), (3, 0, 2), (3, 2, 4), (5, 12, 16), (4, 0, 2), (4, 2, 4)):
            load_rows(i, first, end)
        w2_stage = big_tile(16 * D, BF16, "w2_stage", "w2")

        ident_f32 = keep.tile([P, P], F32)
        make_identity(nc, ident_f32[:])
        minus_half = keep.tile([P, 1], F32)
        nc.vector.memset(minus_half[:], -0.5)
        slot_index = keep.tile([P, T], F32)
        for j in range(T):
            nc.vector.memset(slot_index[:, j : j + 1], float(j))

        def selection(r):
            sel_f32 = keep.tile([P, 8 * r], F32, name="selection%d_f32" % r)
            sel = keep.tile([P, 8 * r], BF16, name="selection%d" % r)
            nc.vector.tensor_reduce(
                out=sel_f32[:], in_=ident_f32[:].rearrange("p (j q) -> p j q", q=L // r), axis=X, op=ALU.add
            )
            return sel_f32, sel

        pooling = {}
        mod16 = keep.tile([P, 16], F32)

        def make_selections():
            for r in (1, 2, 4):
                pooling[r] = selection(r)
            nc.vector.tensor_reduce(
                out=mod16[:], in_=ident_f32[:].rearrange("p (j q) -> p q j", q=16), axis=X, op=ALU.add
            )
            for r in (1, 2, 4):
                nc.vector.tensor_copy(out=pooling[r][1][:], in_=pooling[r][0][:])

        count = keep.tile([P, 8], F32)
        count_or_1 = keep.tile([P, 8], F32)
        reciprocal = keep.tile([P, 8], F32)
        factor = keep.tile([P, 8], F32)
        factor_all = keep.tile([P, B], F32)

        def turn_factor(k, tag):
            turned = psum.tile([P, 4, P], F32, tag=tag, bufs=1, name="turned")
            for i in range(4):
                column = factor[:, 4 * k + i : 4 * k + i + 1]
                nc.tensor.transpose(turned[:, i, :], column.to_broadcast([P, P]), ident_f32[:])
            return turned

        def spread_factor(k, turned):
            nc.scalar.copy(
                out=factor_all[:].rearrange("p (n i) -> p n i", i=8)[:, :, 4 * k : 4 * k + 4],
                in_=turned[:].rearrange("p i n -> p n i"),
            )

        scale_columns = keep.tile([P, 2, 4], F32)
        columns = keep.tile([P, VECTOR_ROWS, 2, 2], F32)

        def turn_rows(src, step, width):
            turned = psum.tile([P, step, P], F32, tag="hidden", name="turned")
            for c in range(step):
                nc.tensor.transpose(turned[:, c, :], src[:, c : width : step], ident_f32[:])
            return turned[:].rearrange("p c (g row) -> p row g c", g=2)

        def keep_columns(dst, turned):
            nc.scalar.copy(out=dst, in_=turned)

        def turn_vector(row, tag, bufs, halves=2):
            turned = psum.tile([P, halves, 2, P], F32, tag=tag, bufs=bufs, name="turned")
            for g in range(halves):
                for u in range(2):
                    column = columns[:, row, g, u : u + 1]
                    nc.tensor.transpose(turned[:, g, u, :], column.to_broadcast([P, P]), ident_f32[:])
            return turned

        def as_entries(turned):
            return turned[:].rearrange("p g u m -> p (g u m)").bitcast(BF16)

        w1_codes = keep.tile([P, F], U32, align_bytes=64)
        w1_planes = keep.tile([P, F], U8, align_bytes=64)
        w1_words = [
            w1_stage[:, 4 * HALF * (2 + g) : 4 * HALF * (3 + g)].rearrange("p (c t) -> p c t", t=4) for g in range(2)
        ]

        def interleave_w1(g, blocks):
            copy = (nc.vector.tensor_copy, nc.scalar.copy)[g]
            src = w1_rows[:, :, HALF * g : HALF * g + HALF].rearrange("p t (m u e) -> p u m e t", u=2, e=2)
            for u in blocks:
                copy(out=w1_words[g][:, hidden_block(0, u), :].rearrange("p (m e) t -> p m e t", e=2), in_=src[:, u])

        def quantise_w1(g):
            cols = slice(HALF * g, HALF * g + HALF)
            nc.vector.quantize_mx(
                out=w1_codes[:, cols].bitcast(FP8X4),
                scales=w1_planes[:, cols],
                in_=w1_words[g].rearrange("p c t -> p (c t)"),
            )

        w2_rows = w2_stage[:, : 8 * D].rearrange("p (g t n) -> p g t n", g=2, t=4)
        w2_words = [w2_stage[:, 4 * D * (2 + g) : 4 * D * (3 + g)].rearrange("p (n t) -> p n t", t=4) for g in range(2)]
        w2_codes = keep.tile([P, 2, D], U32, align_bytes=64)
        w2_planes = keep.tile([P, 2, D], U8, align_bytes=64)

        def widen_w2(g, positions):
            for t in positions:
                nc.scalar.activation(
                    out=w2_rows[:, g, t, :],
                    in_=w2_bytes[:, g, t, :].bitcast(FP8),
                    func=ACT.Copy,
                    scale=scale_columns[:, g, t : t + 1],
                )

        def interleave_w2(g, cols, copy):
            copy(
                out=w2_words[g][:, cols].rearrange("p (c i) t -> p c t i", i=4),
                in_=w2_rows[:, g, :, cols].rearrange("p t (c i) -> p c t i", i=4),
            )

        def gpsimd_copy(out, in_):
            nc.gpsimd.tensor_scalar(out=out, in0=in_, scalar1=1.0, scalar2=0.0, op0=ALU.mult, op1=ALU.add)

        def quantise_w2(g):
            nc.vector.quantize_mx(
                out=w2_codes[:, g, :].bitcast(FP8X4),
                scales=w2_planes[:, g, :],
                in_=w2_words[g].rearrange("p n t -> p (n t)"),
            )

        st = {}
        pooled = [0] * NT
        added = [0] * NT
        groups = [[] for i in range(NT)]

        def pool(i, q):
            if q == 0:
                st["sums", i] = psum.tile([P, P, 4], F32, tag="pool%d" % (i % 2), bufs=1, name="sums")
            r = rows_per_partition(i, q)
            width = 8 * r
            x = quarters(i, q, 1).rearrange("p (c x) -> p c x", x=r * D)
            for c in range(4 // r):
                b0 = 32 * q + width * c
                for t in range(4):
                    for e in range(r):
                        nc.tensor.matmul(
                            out=st["sums", i][:, b0 : b0 + width, t],
                            lhsT=x[:, c, D * e + t : D * e + D : 4],
                            rhs=pooling[r][1][:],
                            start=(e == 0),
                            stop=(e == r - 1),
                        )
            if q == QUARTERS - 1:
                give_back(("ctx", i))

        def add_pairs(i, n, engine=nc.vector, tag="pairs", bufs=PAIR_BUFFERS):
            l0 = added[i]
            added[i] += 2 * n
            pairs = work.tile([P, n * D], F32, tag=tag, bufs=bufs, align_bytes=64, name="pairs")
            x = ctx[i][:, D * l0 : D * added[i]].rearrange("b (h c k t) -> b h c t k", h=2, k=4, t=4)
            engine.tensor_tensor(
                out=pairs[:].rearrange("b (t c k) -> b c t k", t=4, k=4), in0=x[:, 0], in1=x[:, 1], op=ALU.add
            )
            groups[i].append((pairs, n, l0 == 0, added[i] == L))
            if added[i] == L:
                give_back(("ctx", i))

        def pool_whole(i, q):
            pairs, n, first, last = groups[i][q]
            if first:
                st["sums", i] = psum.tile([P, 4, P], F32, tag="pool%d" % (i % 2), bufs=1, name="sums")
            for t in range(4):
                for j in range(n):
                    w0 = P * (n * t + j)
                    nc.tensor.matmul(
                        out=st["sums", i][:, t, :],
                        lhsT=pairs[:, w0 : w0 + P],
                        rhs=ident_f32[:],
                        is_transpose=True,
                        start=first and (t, j) == (0, 0),
                        stop=last and (t, j) == (3, n - 1),
                    )

        def add_next(number, engine=nc.vector, tag="pairs", bufs=PAIR_BUFFERS):
            for i in WHOLE:
                n = min(number, (L - added[i]) // 2)
                if n:
                    add_pairs(i, n, engine, tag, bufs)
                    number = number - n
                    tag, bufs = "pairs", PAIR_BUFFERS

        def pool_ready(i):
            pool_until(i, len(groups[i]) - 1 if i in WHOLE else QUARTERS - 1)

        def pool_until(i, last):
            while pooled[i] <= last:
                (pool_whole if i in WHOLE else pool)(i, pooled[i])
                pooled[i] += 1

        def scale_mean(i):
            mean = work.tile([P, P, 4], BF16, align_bytes=64, tag="mean", name="mean")
            nc.vector.tensor_tensor(
                out=mean[:],
                in0=st["sums", i][:].rearrange("p t b -> p b t") if i in WHOLE else st["sums", i][:],
                in1=factor_all[:, P * i : P * i + P].unsqueeze(2).to_broadcast([P, P, 4]),
                op=ALU.mult,
            )
            st["mean", i] = mean

        def quantise_mean(i):
            codes = work.tile([P, P], U32, align_bytes=64, tag="mean_codes", name="mean_codes")
            plane = work.tile([P, P], U8, align_bytes=64, tag="mean_plane", name="mean_plane")
            nc.vector.quantize_mx(
                out=codes[:].bitcast(FP8X4), scales=plane[:], in_=st["mean", i][:].rearrange("p b t -> p (b t)")
            )
            st["mean_codes", i], st["mean_plane", i] = codes, plane

        def multiply_w1(i, halves=(0, 1)):
            for g in halves:
                cols = slice(HALF * g, HALF * g + HALF)
                acc = psum.tile([P, HALF], F32, tag="hidden", name="acc")
                nc.tensor.matmul_mx(
                    out=acc[:],
                    lhsT=st["mean_codes", i][:].bitcast(FP8X4),
                    lhsT_scale=st["mean_plane", i][:],
                    rhs=w1_codes[:, cols].bitcast(FP8X4),
                    rhs_scale=w1_planes[:, cols],
                    start=True,
                    stop=True,
                )
                st["acc", i, g] = acc

        def add_b1(i):
            v = work.tile([P, F], F32, tag="v", name="v")
            for g in range(2):
                cols = slice(HALF * g, HALF * g + HALF)
                nc.vector.tensor_tensor(out=v[:, cols], in0=st["acc", i, g][:], in1=b1_all[:, cols], op=ALU.add)
            st["v", i] = v

        def gelu(i):
            h = work.tile([P, F], F32, tag="h", name="h")
            total = work.tile([P, 1], F32, tag="total", name="total")
            nc.scalar.activation(out=h[:], in_=st["v", i][:], func=ACT.Gelu, accum_out=total[:])
            st["h", i], st["total", i] = h, total

        def mean_of_h(i):
            mu = work.tile([P, 1], F32, tag="mu", name="mu")
            nc.scalar.activation(out=mu[:], in_=st["total", i][:], func=ACT.Copy, scale=1.0 / F)
            st["mu", i] = mu

        def squares(i):
            scaled_var = work.tile([P, 1], F32, tag="scaled_var", name="scaled_var")
            nc.scalar.activation(
                out=st["v", i][:],
                in_=st["h", i][:],
                func=ACT.Square,
                scale=-float(F),
                bias=st["total", i][:],
                accum_out=scaled_var[:],
            )
            st["scaled_var", i] = scaled_var

        def inverse_deviation(i):
            var_eps = work.tile([P, 1], F32, tag="var_eps", name="var_eps")
            nc.vector.tensor_scalar(
                out=var_eps[:], in0=st["scaled_var", i][:], scalar1=1.0 / F**3, scalar2=LN_EPS, op0=ALU.mult, op1=ALU.add
            )
            rstd = work.tile([P, 1], F32, tag="rstd", name="rstd")
            nc.gpsimd.tensor_tensor(out=rstd[:], in0=var_eps[:], in1=minus_half[:], op=ALU.pow)
            st["rstd", i] = rstd

        def centre(i):
            centred = work.tile([P, F], F32, tag="centred", name="centred")
            nc.vector.scalar_tensor_tensor(
                out=centred[:],
                in0=st["h", i][:],
                scalar=st["mu", i][:],
                in1=as_entries(gamma_turned),
                op0=ALU.subtract,
                op1=ALU.mult,
            )
            st["centred", i] = centred

        def normalise(i, passes=(0, 1)):
            if passes[0] == 0:
                st["hn", i] = work.tile([P, F], BF16, tag="hn", name="hn")
            cols = slice(HALF * passes[0], HALF * passes[-1] + HALF)
            nc.vector.scalar_tensor_tensor(
                out=st["hn", i][:, cols],
                in0=st["centred", i][:, cols],
                scalar=st["rstd", i][:],
                in1=as_entries(beta_turned)[:, cols],
                op0=ALU.mult,
                op1=ALU.add,
            )

        def transpose_hn(i, passes=(0, 1), tag="turned_hn"):
            turned = psum.tile([P, len(passes), 2, P], F32, tag=tag, bufs=1, name="turned_hn")
            words = st["hn", i][:].bitcast(F32)
            for k, g in enumerate(passes):
                for u in range(2):
                    w0 = 256 * g + 128 * u
                    nc.tensor.transpose(turned[:, k, u, :], words[:, w0 : w0 + 128], ident_f32[:])
            st["turned_hn", i, passes] = turned

        def interleave_hn(i, passes=(0, 1)):
            hn_words = work.tile([P, len(passes) * P * 4], BF16, align_bytes=64, tag="hn_words", name="hn_words")
            nc.scalar.copy(
                out=hn_words[:].bitcast(F32).rearrange("p (g b u) -> p g b u", b=P, u=2),
                in_=st["turned_hn", i, passes][:].rearrange("p g u b -> p g b u"),
            )
            st["hn_words", i, passes] = hn_words

        def quantise_hn(i, passes=(0, 1)):
            codes = work.tile([P, len(passes) * P], U32, align_bytes=64, tag="hn_codes", name="hn_codes")
            plane = work.tile([P, len(passes) * P], U8, align_bytes=64, tag="hn_plane", name="hn_plane")
            nc.vector.quantize_mx(out=codes[:].bitcast(FP8X4), scales=plane[:], in_=st["hn_words", i, passes][:])
            st["hn_codes", i, passes], st["hn_plane", i, passes] = codes, plane

        def multiply_w2(i, passes=(0, 1)):
            if passes[0] == 0:
                st["acc2", i] = psum.tile([P, D], F32, tag="out", bufs=1, name="acc2")
            for k, g in enumerate(passes):
                part = slice(P * k, P * k + P)
                nc.tensor.matmul_mx(
                    out=st["acc2", i][:],
                    lhsT=st["hn_codes", i, passes][:, part].bitcast(FP8X4),
                    lhsT_scale=st["hn_plane", i, passes][:, part],
                    rhs=w2_codes[:, g, :].bitcast(FP8X4),
                    rhs_scale=w2_planes[:, g, :],
                    start=(g == 0),
                    stop=(g == 1),
                )

        def mask_b2(i, engine="vector"):
            if ("b2_masked", i) in st:
                return
            masked = keep.tile([P, D], BF16, name="b2_masked%d" % i)
            if engine == "vector":
                nc.vector.tensor_scalar_mul(masked[:], b2_all[:], valid[:, i, 0:1])
            else:
                nc.scalar.activation(out=masked[:], in_=b2_all[:], func=ACT.Copy, scale=valid[:, i, 0:1])
            st["b2_masked", i] = masked

        waiting = []

        def first_slot(i):
            st["slots", i] = big_tile(T * D, F32, "slots", ("slots", i))
            nc.vector.scalar_tensor_tensor(
                out=st["slots", i][:, :D],
                in0=st["acc2", i][:],
                scalar=valid[:, i, 0:1],
                in1=st["b2_masked", i][:],
                op0=ALU.mult,
                op1=ALU.add,
            )
            store_slots(i, 1)
            waiting.extend((i, j) for j in range(1, T))

        def store_slots(i, end):
            ends = (0, T) if i < FIRST_STORED_IN_HALVES else (0, T // 2, T) if i < LAST else LAST_PARTS
            if end in ends:
                cols = slice(D * ends[ends.index(end) - 1], D * end)
                nc.sync.dma_start(
                    out=out[P * i : P * i + P].rearrange("b j d -> b (j d)")[:, cols], in_=st["slots", i][:, cols]
                )

        def fill_slots(number, engine):
            for i, j in waiting[:number]:
                waiting.remove((i, j))
                mask = valid[:, i, j : j + 1]
                src = st["slots", i][:, :D]
                dst = st["slots", i][:, D * j : D * j + D]
                if engine == "vector":
                    nc.vector.tensor_scalar_mul(dst, src, mask)
                elif engine == "gpsimd":
                    nc.gpsimd.tensor_scalar(out=dst, in0=src, scalar1=mask, scalar2=0.0, op0=ALU.mult, op1=ALU.add)
                else:
                    nc.scalar.activation(out=dst, in_=src, func=ACT.Copy, scale=mask)
                store_slots(i, j + 1)

        target_n = keep.tile([P, 8], F32)
        picked = keep.tile([P, 16, 8], BF16)
        valid = keep.tile([P, NT, T], F32)

        def count_targets():
            nc.vector.tensor_tensor(
                out=picked[:],
                in0=target_n[:].unsqueeze(1).to_broadcast([P, 16, 8]),
                in1=mod16[:].unsqueeze(2).to_broadcast([P, 16, 8]),
                op=ALU.mult,
            )
            n_psum = psum.tile([P, NT], F32, tag="beta", bufs=1, name="n_psum")
            nc.tensor.matmul(
                out=n_psum[:], lhsT=picked[:].rearrange("p q i -> p (q i)"), rhs=pooling[1][1][:], start=True, stop=True
            )
            st["n_psum"] = n_psum

        def spread_b1(turned):
            dst = keep.tile([P, F], BF16, name="b1_all")
            nc.scalar.copy(out=dst[:].bitcast(F32), in_=turned[:].rearrange("p g u m -> p (g u m)"))
            return dst

        def spread_b2(turned):
            dst = keep.tile([P, D], BF16, name="b2_all")
            nc.scalar.copy(
                out=dst[:].bitcast(F32).rearrange("p (m u) -> p m u", u=2), in_=turned[:, 0].rearrange("p u m -> p m u")
            )
            return dst

        def valid_slots():
            nc.vector.tensor_tensor(
                out=valid[:],
                in0=slot_index[:].unsqueeze(1).to_broadcast([P, NT, T]),
                in1=st["n_psum"][:].unsqueeze(2).to_broadcast([P, NT, T]),
                op=ALU.is_lt,
            )

        nc.vector.tensor_reduce(out=count[:], in_=cmask[:], axis=X, op=ALU.add)
        nc.vector.tensor_scalar_max(count_or_1[:], count[:], 1.0)
        nc.vector.reciprocal(reciprocal[:], count_or_1[:])
        nc.vector.scalar_tensor_tensor(
            out=factor[:], in0=count[:], scalar=0.0, in1=reciprocal[:], op0=ALU.is_gt, op1=ALU.mult
        )
        factor_turned = [turn_factor(0, "out"), turn_factor(1, "turned_hn")]
        scales_turned = turn_rows(scale_rows, 4, HALF)
        for k in range(2):
            spread_factor(k, factor_turned[k])
        keep_columns(scale_columns[:], scales_turned[:, 0])
        widen_w2(0, range(4))
        widen_w2(1, range(3))
        add_pairs(0, 2)
        pool_ready(0)
        make_selections()
        for q in range(1, QUARTERS):
            add_pairs(0, 2)
            pool_ready(0)
        vectors_turned = turn_rows(vectors, 2, HALF // 2)
        interleave_w2(0, slice(0, D // 2), nc.vector.tensor_copy)
        interleave_w1(0, (0, 1))
        interleave_w1(1, (0,))
        keep_columns(columns[:], vectors_turned[:, :VECTOR_ROWS])
        interleave_w1(1, (1,))
        b1_turned = turn_vector(ROW_B1, "hidden", 2)
        b1_all = spread_b1(b1_turned)
        scale_mean(0)
        quantise_w1(0)
        quantise_mean(0)
        pool_until(1, 0)
        multiply_w1(0, (0,))
        quantise_w1(1)
        give_back("w1")
        multiply_w1(0, (1,))
        for i, first, end in ((7, 0, 16), (6, 0, 4)):
            load_rows(i, first, end)

        add_b1(0)
        gelu(0)
        mean_of_h(0)
        pool_until(1, 3)
        gamma_turned = turn_vector(ROW_GAMMA, "gamma", 1)
        b2_turned = turn_vector(ROW_B2, "out", 1, halves=1)
        squares(0)
        interleave_w2(0, slice(D // 2, D), nc.vector.tensor_copy)
        nc.vector.tensor_reduce(out=target_n[:], in_=tmask[:], axis=X, op=ALU.add)
        quantise_w2(0)
        scale_mean(1)
        count_targets()
        quantise_mean(1)
        multiply_w1(1)
        centre(0)
        valid_slots()
        beta_turned = turn_vector(ROW_BETA, "beta", 1)
        pool_until(2, 1)
        b2_all = spread_b2(b2_turned)
        widen_w2(1, range(3, 4))
        interleave_w2(1, slice(0, D // 2), nc.scalar.copy)
        inverse_deviation(0)

        add_b1(1)
        add_next(3, nc.gpsimd, "shared", 3)
        gelu(1)
        mean_of_h(1)
        pool_until(2, 2)
        normalise(0)
        transpose_hn(0)
        pool_until(2, 3)
        interleave_w2(1, slice(D // 2, D), nc.scalar.copy)
        interleave_hn(0)
        squares(1)
        for i in range(3):
            mask_b2(i, "scalar")
        centre(1)
        scale_mean(2)
        quantise_mean(2)
        multiply_w1(2)
        quantise_hn(0)
        quantise_w2(1)
        give_back("w2")
        multiply_w2(0)
        pool_until(3, 1)
        inverse_deviation(1)

        def open_step(s, pairs):
            add_b1(s)
            add_next(pairs, nc.gpsimd, "shared", 3)
            gelu(s)
            mean_of_h(s)
            if s + 1 not in WHOLE:
                pool_ready(s + 1)
            normalise(s - 1)
            transpose_hn(s - 1)
            squares(s)
            first_slot(s - 2)
            interleave_hn(s - 1)
            pool_ready(s + 1)
            if s + 2 in WHOLE:
                pool_until(s + 2, 0)
            elif 2 < s < LAST - 1:
                pool_until(s + 2, 1)
            centre(s)
            scale_mean(s + 1)

        for s in range(2, LAST - 1):
            open_step(s, 2 if s == 3 else 3)
            fill_slots(1, "vector")
            quantise_mean(s + 1)
            multiply_w1(s + 1)
            mask_b2(s - 1)
            quantise_hn(s - 1)
            multiply_w2(s - 1)
            fill_slots(1, "vector")
            inverse_deviation(s)
            if s + 2 in WHOLE:
                pool_ready(s + 2)
            else:
                pool_until(s + 2, 1 if s == 2 else 2)
            fill_slots(len(waiting), "scalar")

        s = LAST - 1
        add_b1(s)
        add_next(2, nc.gpsimd, "shared", 3)
        gelu(s)
        mean_of_h(s)
        normalise(s - 1)
        transpose_hn(s - 1)
        first_slot(s - 2)
        pool_ready(LAST)
        interleave_hn(s - 1)
        squares(s)
        centre(s)
        quantise_hn(s - 1)
        multiply_w2(s - 1)
        fill_slots(3, "vector")
        scale_mean(LAST)
        inverse_deviation(s)
        quantise_mean(LAST)
        multiply_w1(LAST)
        mask_b2(s - 1)
        fill_slots(len(waiting), "scalar")

        first_slot(LAST - 2)
        normalise(LAST - 1)
        transpose_hn(LAST - 1)
        add_b1(LAST)
        for engine in ("gpsimd", "scalar", "gpsimd", "scalar"):
            fill_slots(1, engine)
        interleave_hn(LAST - 1)
        gelu(LAST)
        mean_of_h(LAST)
        squares(LAST)
        mask_b2(LAST - 1)
        quantise_hn(LAST - 1)
        multiply_w2(LAST - 1)
        fill_slots(3, "vector")
        centre(LAST)
        inverse_deviation(LAST)
        first_slot(LAST - 1)
        mask_b2(LAST, "scalar")
        fill_slots(1, "vector")
        for g, tag in enumerate(("turned_hn", "pool0")):
            normalise(LAST, (g,))
            transpose_hn(LAST, (g,), tag)
        fill_slots(2, "scalar")
        for g in range(2):
            interleave_hn(LAST, (g,))
        fill_slots(2, "vector")
        quantise_hn(LAST, (0,))
        multiply_w2(LAST, (0,))
        fill_slots(1, "vector")
        quantise_hn(LAST, (1,))
        multiply_w2(LAST, (1,))
        fill_slots(1, "vector")
        first_slot(LAST)
        while waiting:
            fill_slots(2, "vector")
            fill_slots(1, "scalar")
